import numpy as np
import ml_dtypes


def mxq(x, axis, fmt="e4m3"):
    dtype, down = {"e4m3": (ml_dtypes.float8_e4m3fn, 7), "e5m2": (ml_dtypes.float8_e5m2, 14)}[fmt]
    v = np.moveaxis(np.asarray(x, np.float32).astype(ml_dtypes.bfloat16).astype(np.float64), axis, -1)
    blocks = v.reshape(v.shape[:-1] + (-1, 32))
    amax = np.abs(blocks).max(-1, keepdims=True)
    byte = np.maximum(np.where(amax > 0, np.frexp(amax)[1] - 1 + 127, 0) - down, 1)
    scale = np.exp2(byte - 127.0)
    codes = (blocks / scale).astype(np.float32).astype(dtype).astype(np.float64)
    return np.moveaxis((codes * scale).reshape(v.shape), -1, axis)


WIDE = False


def mx_kscale(k):
    if not WIDE:
        return np.ones(k)
    levels = np.array([10, -10, 5, -5, 0])
    if k % 512:
        return np.exp2(np.random.permutation(np.resize(levels, k // 32))).repeat(32)
    a = np.empty((k // 512, 16))
    for p in range(k // 512):
        a[p, :8] = np.random.permutation(np.resize(levels, 8))
        for g in range(8):
            far = levels[np.abs(levels - a[p, g]) >= 10]
            a[p, g + 8] = far[np.random.randint(len(far))]
    return np.exp2(a.ravel()).repeat(32)


BF16 = ml_dtypes.bfloat16


def bf(x):
    return np.asarray(x, np.float32).astype(BF16)


def f64(x):
    return np.asarray(x).astype(np.float64)


E2M1 = np.array([0.0, 0.5, 1.0, 1.5, 2.0, 3.0, 4.0, 6.0, -0.0, -0.5, -1.0, -1.5, -2.0, -3.0, -4.0, -6.0])


def pack_weight(w, fmt):
    k, n = w.shape
    w = f64(bf(w)).reshape(k // 32, 32, n)
    amax = np.abs(w).max(1)
    if fmt == "e4m3":
        byte = np.frexp(amax)[1] - 1 + 127 - 7
    else:
        mant, ex = np.frexp(amax / 6.0)
        byte = np.where(mant > 0.5, ex, ex - 1) + 127
    byte = np.clip(np.where(amax > 0, byte, 1), 1, 254)
    scaled = (w * np.exp2(127.0 - byte)[:, None, :]).reshape(k, n).astype(np.float32)
    by_word = np.ascontiguousarray(scaled.reshape(k // 512, 128, 4, n).transpose(0, 1, 3, 2))
    if fmt == "e4m3":
        words = by_word.astype(ml_dtypes.float8_e4m3fn).view(np.uint8)
    else:
        c = by_word.astype(ml_dtypes.float4_e2m1fn).view(np.uint8) & 0xF
        words = c[..., 0::2] | (c[..., 1::2] << 4)
    return np.ascontiguousarray(words), np.ascontiguousarray(byte.astype(np.uint8).reshape(k // 512, 16, n))


def unpack_weight(words, scales, fmt):
    g, p, n, _ = words.shape
    if fmt == "e4m3":
        vals = np.ascontiguousarray(words).view(ml_dtypes.float8_e4m3fn).astype(np.float64)
    else:
        nib = np.empty((g, p, n, 4), np.uint8)
        nib[..., 0::2] = words & 0xF
        nib[..., 1::2] = words >> 4
        vals = E2M1[nib]
    vals = vals * np.repeat(np.exp2(scales.astype(np.float64) - 127.0), 8, axis=1)[..., None]
    return vals.transpose(0, 1, 3, 2).reshape(g * 512, n)


N, L, WD, C, O = 128, 64, 512, 512, 512
EPS = 1e-8
CONV_CLAMP = 256.0
ACT_GAIN = np.sqrt(2.0)
LRELU_SLOPE = 0.2
STYLE_WSCALE = 1.0 / np.sqrt(WD)
X_AMP = CONV_CLAMP / 2.0
W_AMP = np.sqrt(EPS)


def draw0():
    s, t = mx_kscale(WD), mx_kscale(C)
    x = bf(np.random.standard_normal((N, L, C)) * X_AMP)
    w = bf(np.random.standard_normal((N, WD)) * s)
    weight = bf(np.random.standard_normal((O, C)) * W_AMP / np.sqrt(C) / t[None, :])
    style_w = np.random.standard_normal((C, WD)) * t[:, None] / s[None, :]
    style_w_words, style_w_scales = pack_weight(style_w.T, "e4m3")
    return {"x": x,
            "w": w,
            "weight": weight,
            "style_w_words": style_w_words,
            "style_w_scales": style_w_scales,
            "style_b": bf((1.0 + 0.1 * np.random.standard_normal(C)) * t),
            "bias": bf(np.random.standard_normal(O) * 0.2 * X_AMP)}


def core(x, w, weight, style_w_words, style_w_scales, style_b, bias):
    wt = f64(weight)
    style = (mxq(f64(w), 1, "e4m3") @ unpack_weight(style_w_words, style_w_scales, "e4m3")) * STYLE_WSCALE + f64(style_b)
    d = mxq(np.square(style), 1, "e4m3") @ mxq(np.square(wt), 1, "e4m3").T
    decoef = 1.0 / np.sqrt(d + EPS)
    x_mod = f64(x) * style[:, None, :]
    y = mxq(x_mod, 2, "e4m3") @ mxq(wt, 1, "e4m3").T
    y = y * decoef[:, None, :]
    y = y + f64(bias)
    y = np.where(y >= 0, y, LRELU_SLOPE * y) * ACT_GAIN
    return np.clip(y, -CONV_CLAMP, CONV_CLAMP)


def e4m3fn_bytes(y):
    return np.clip(np.asarray(y, np.float64), -448.0, 448.0).astype(np.float32).astype(ml_dtypes.float8_e4m3fn).view(np.uint8)


def e4m3fn_values(b):
    return np.asarray(b, np.uint8).view(ml_dtypes.float8_e4m3fn).astype(np.float64)


def setup_inputs():
    d = draw0()
    x0 = np.asarray(d['w']).astype(np.float64)
    s = (np.max(np.abs(x0), axis=(0,), keepdims=True) / 448.0).astype(np.float32)
    out = {}
    for k, v in d.items():
        if k == 'w':
            out['w_bytes'] = e4m3fn_bytes(x0 / s.astype(np.float64))
            out['w_scale'] = s
        else:
            out[k] = v
    return out


def reference(x, w_bytes, w_scale, weight, style_w_words, style_w_scales, style_b, bias):
    return core(x, e4m3fn_values(w_bytes) * w_scale.astype(np.float64), weight, style_w_words, style_w_scales, style_b, bias)

@@ -1,0 +1,371 @@
+from contextlib import ExitStack
+import math
+
+import concourse.mybir as mybir
+from concourse.masks import make_identity
+
+F32 = mybir.dt.float32
+BF16 = mybir.dt.bfloat16
+U32 = mybir.dt.uint32
+I32 = mybir.dt.int32
+U8 = mybir.dt.uint8
+F8 = mybir.dt.float8_e4m3fn
+X4 = mybir.dt.float8_e4m3fn_x4
+ALU = mybir.AluOpType
+ACT = mybir.ActivationFunctionType
+
+N, L, WD, C, O = 128, 64, 512, 512, 512
+P = 128
+J = 2
+GT = P * J
+GROUPS = N * L // GT
+NS = GT // L
+EPS = 1e-8
+HUGE = 3.0e38
+FLOPS = 2 * N * L * C * O + 2 * N * WD * C + 2 * N * C * O
+KINDS = ["P"]
+
+
+FIXED = {}
+
+
+def kind_of(g, j):
+    return FIXED.get((g, j), KINDS[(J * g + j) % len(KINDS)])
+
+
+def tile_modulatemlp_pa_w8_kernel(
+    tc, x, w_bytes, w_scale, weight, style_w_words, style_w_scales, style_b, bias, out
+):
+    nc = tc.nc
+    gain = 0.2 * math.sqrt(2.0)
+    xg = x.rearrange("n l c -> (n l) c").rearrange("(g p j) c -> g p j c", p=P, j=J)
+    og = out.rearrange("n l c -> (n l) c").rearrange("(g p j) c -> g p j c", p=P, j=J)
+
+    with ExitStack() as ctx:
+        const = ctx.enter_context(tc.tile_pool(name="const", bufs=1))
+        xmp = ctx.enter_context(tc.tile_pool(name="xmp", bufs=3))
+        ap = ctx.enter_context(tc.tile_pool(name="ap", bufs=4))
+        op = ctx.enter_context(tc.tile_pool(name="op", bufs=5))
+        psum = ctx.enter_context(tc.psum_pool(name="psum", bufs=1))
+        ctx.enter_context(tc.manual_schedule())
+
+        wb = const.tile([P, WD], U8, name="wb", align_bytes=64)
+        nc.sync.dma_start(out=wb[:], in_=w_bytes)
+        wsc = const.tile([P, 4], F32, name="wsc")
+        nc.sync.dma_start(out=wsc[:], in_=w_scale.rearrange("o (p t) -> p (o t)", t=4))
+        ssc = const.tile([P, C], U8, name="ssc", align_bytes=64)
+        nc.vector.memset(ssc[:].bitcast(U32), 0)
+        for q in range(4):
+            nc.sync.dma_start(
+                out=ssc[32 * q : 32 * q + 4, :].bitcast(I32),
+                in_=style_w_scales[0][4 * q : 4 * q + 4, :].bitcast(I32),
+            )
+        sw = const.tile([P, 4 * C], U8, name="sw", align_bytes=64)
+        nc.sync.dma_start(out=sw[:], in_=style_w_words[0].rearrange("p n t -> p (n t)"))
+        sb = const.tile([P, 4], BF16, name="sb")
+        nc.sync.dma_start(out=sb[:], in_=style_b.rearrange("(p t) -> p t", t=4))
+        wsb = const.tile([P, 4, C], BF16, name="wsb", align_bytes=64)
+        wview = weight.rearrange("(m b) c -> m b c", b=4)
+        for h in range(2):
+            nc.sync.dma_start(out=wsb[:, 2 * h : 2 * h + 2, :], in_=wview[:, 2 * h : 2 * h + 2, :])
+        xtiles = {}
+        bb = const.tile([P, 4], BF16, name="bb")
+        g0 = 0
+        for n_g in [1, 1] + [2] * ((GROUPS - 2) // 2):
+            xt = const.tile([P, n_g, J, C], BF16, name="x%d" % g0, align_bytes=64)
+            nc.sync.dma_start(out=xt[:], in_=xg[g0 : g0 + n_g].rearrange("g p j c -> p g j c"))
+            for k in range(n_g):
+                xtiles[g0 + k] = (xt, k)
+            if g0 == 1:
+                nc.sync.dma_start(out=bb[:], in_=bias.rearrange("(m b) -> m b", b=4))
+            g0 += n_g
+
+        one = const.tile([P, 1], F32, name="one")
+        nc.vector.memset(one[:], 1.0)
+        warm = const.tile([P, 1], F32, name="warm")
+        nc.scalar.activation(warm[:], one[:], ACT.Abs_reciprocal_sqrt)
+        ident = const.tile([P, P], F32, name="ident")
+        make_identity(nc, ident[:])
+
+        def transpose_words(dst, words):
+            for u in range(2):
+                nc.tensor.transpose(dst[:, u, :], words[:, u : C // 2 : 2], ident[:])
+
+        w16 = const.tile([P, WD], BF16, name="w16", align_bytes=64)
+        nc.vector.tensor_copy(out=w16[:], in_=wb[:].bitcast(F8))
+        wtp = psum.tile([P, 2, 2, P], F32, name="wtp", tag="xp", bufs=2)
+        transpose_words(wtp[:, 0], w16[:].bitcast(F32))
+
+        wt = const.tile([P, O, 4], BF16, name="wt", align_bytes=64)
+        wt32 = wt[:].rearrange("p o t -> p (o t)").bitcast(F32)
+        wc = const.tile([P, O], U32, name="wc", align_bytes=64)
+        wcs = const.tile([P, O], U8, name="wcs", align_bytes=64)
+        w2 = const.tile([P, O, 4], BF16, name="w2", align_bytes=64)
+        w2c = const.tile([P, O], U32, name="w2c", align_bytes=64)
+        w2s = const.tile([P, O], U8, name="w2s", align_bytes=64)
+        sq = const.tile([P, N, 4], BF16, name="sq", align_bytes=64)
+        sqc = const.tile([P, N], U32, name="sqc", align_bytes=64)
+        sqs = const.tile([P, N], U8, name="sqs", align_bytes=64)
+        halves = [slice(0, O // 2), slice(O // 2, O)]
+
+        def turn_weight(h):
+            ww = psum.tile([P, 2, 2, P], F32, name="ww", tag="zp", bufs=4)
+            for k in range(2):
+                transpose_words(ww[:, k], wsb[:, 2 * h + k, :].bitcast(F32))
+            nc.scalar.copy(
+                out=wt32[:, 512 * h : 512 * h + 512].rearrange("p (b r u) -> p b r u", b=2, u=2),
+                in_=ww[:].rearrange("p b u r -> p b r u"),
+            )
+
+        sscp = const.tile([P, C], U8, name="sscp", align_bytes=64)
+        nc.vector.tensor_copy(
+            out=sscp[:].rearrange("p (t m) -> p t m", t=4),
+            in_=ssc[:].rearrange("p (m t) -> p t m", t=4),
+        )
+        wm = const.tile([P, N, 4], BF16, name="wm", align_bytes=64)
+        nc.vector.tensor_tensor(
+            out=wm[:].rearrange("p n (u e) -> p n u e", u=2),
+            in0=wtp[:, 0].bitcast(BF16).rearrange("p u (n e) -> p n u e", e=2),
+            in1=wsc[:].rearrange("p (u e) -> p u e", u=2).unsqueeze(1).to_broadcast([P, N, 2, 2]),
+            op=ALU.mult,
+        )
+        swp = const.tile([P, C], I32, name="swp", align_bytes=64)
+        nc.vector.tensor_copy(
+            out=swp[:].rearrange("p (t m) -> p t m", t=4),
+            in_=sw[:].bitcast(I32).rearrange("p (m t) -> p t m", t=4),
+        )
+        wq = const.tile([P, N], U32, name="wq", align_bytes=64)
+        wqs = const.tile([P, N], U8, name="wqs", align_bytes=64)
+        nc.vector.quantize_mx(out=wq[:].bitcast(X4), scales=wqs[:], in_=wm[:].rearrange("p n t -> p (n t)"))
+        turn_weight(0)
+
+        styT = const.tile([P, 4, N], F32, name="styT", align_bytes=64)
+        sp = [
+            psum.tile([P, 2, P], F32, name="sp0", tag="ya", bufs=1),
+            psum.tile([P, 2, P], F32, name="sp1", tag="yb", bufs=1),
+        ]
+        for t in range(4):
+            nc.tensor.matmul_mx(
+                out=sp[t // 2][:, t % 2, :],
+                lhsT=swp[:, P * t : P * t + P].bitcast(X4),
+                lhsT_scale=sscp[:, P * t : P * t + P],
+                rhs=wq[:].bitcast(X4),
+                rhs_scale=wqs[:],
+                start=True,
+                stop=True,
+            )
+        wscale = 1.0 / math.sqrt(WD)
+        for t in range(2):
+            nc.scalar.activation(
+                styT[:, t, :], sp[0][:, t, :], ACT.Identity, scale=wscale, bias=sb[:, t : t + 1]
+            )
+        for t in range(2, 4):
+            nc.vector.tensor_scalar(
+                out=styT[:, t, :], in0=sp[1][:, t - 2, :], scalar1=wscale, scalar2=sb[:, t : t + 1],
+                op0=ALU.mult, op1=ALU.add,
+            )
+        turn_weight(1)
+
+        xp, xm, xq, yy, aa, cc, zz, rr, oo = {}, {}, {}, {}, {}, {}, {}, {}, {}
+
+        def stage_x(g):
+            xt, k = xtiles[g]
+            xp[g] = psum.tile([P, J, 2, P], F32, name="xpt", tag="xp", bufs=2)
+            for j in range(J):
+                transpose_words(xp[g][:, j], xt[:, k, j, :].bitcast(F32))
+
+        def stage_a(g, j):
+            if j == 0:
+                xm[g] = xmp.tile([P, J, P, 4], BF16, name="xm", align_bytes=64)
+            nc.vector.tensor_tensor(
+                out=xm[g][:, j].rearrange("p (n i) (u e) -> p n i u e", n=NS, u=2),
+                in0=xp[g][:, j].bitcast(BF16).rearrange("p u (n i e) -> p n i u e", n=NS, e=2),
+                in1=styT[:, :, NS * g : NS * g + NS]
+                .rearrange("p (u e) n -> p n u e", u=2)
+                .unsqueeze(2)
+                .to_broadcast([P, NS, P // NS, 2, 2]),
+                op=ALU.mult,
+            )
+
+        def stage_b(g):
+            xc = xmp.tile([P, GT], U32, name="xc", align_bytes=64)
+            xs = xmp.tile([P, GT], U8, name="xs", align_bytes=64)
+            nc.vector.quantize_mx(
+                out=xc[:].bitcast(X4), scales=xs[:], in_=xm.pop(g)[:].rearrange("p j r t -> p (j r t)")
+            )
+            xq[g] = (xc, xs)
+
+        def stage_m(g):
+            xc, xs = xq.pop(g)
+            for h in range(2):
+                y = psum.tile([P, 2, GT], F32, name="y%d" % h, tag="ya" if h == 0 else "yb", bufs=1)
+                for k in range(2):
+                    ob = 2 * h + k
+                    nc.tensor.matmul_mx(
+                        out=y[:, k, :],
+                        lhsT=wc[:, P * ob : P * ob + P].bitcast(X4),
+                        lhsT_scale=wcs[:, P * ob : P * ob + P],
+                        rhs=xc[:].bitcast(X4),
+                        rhs_scale=xs[:],
+                        start=True,
+                        stop=True,
+                    )
+                yy[g, h] = y
+
+        def stage_e(g, h, on_vector=False):
+            if h == 0:
+                aa[g] = ap.tile([P, 4, GT], F32, name="a")
+            y = yy.pop((g, h))
+            for k in range(2):
+                ob = 2 * h + k
+                yv = y[:, k, :].rearrange("p (j n i) -> p n j i", j=J, n=NS)
+                av = aa[g][:, ob, :].rearrange("p (j n i) -> p n j i", j=J, n=NS)
+                for n in range(NS):
+                    s = NS * g + n
+                    if on_vector:
+                        nc.vector.tensor_scalar(
+                            out=av[:, n], in0=yv[:, n], scalar1=dT[:, ob, s : s + 1], scalar2=bT[:, ob : ob + 1],
+                            op0=ALU.mult, op1=ALU.add,
+                        )
+                    else:
+                        nc.scalar.activation(
+                            av[:, n], yv[:, n], ACT.Identity, scale=dT[:, ob, s : s + 1], bias=bT[:, ob : ob + 1]
+                        )
+
+        def stage_q(g):
+            for j in range(J):
+                if kind_of(g, j) == "VV":
+                    cc[g, j] = ap.tile([P, 4, P], F32, name="c")
+                    nc.vector.tensor_scalar(
+                        out=cc[g, j][:], in0=aa[g][:, :, P * j : P * j + P], scalar1=0.0, scalar2=4.0,
+                        op0=ALU.max, op1=ALU.mult,
+                    )
+                elif kind_of(g, j) != "P":
+                    c = ap.tile([P, 4, P], F32, name="c")
+                    nc.gpsimd.tensor_scalar(
+                        out=c[:], in0=aa[g][:, :, P * j : P * j + P], scalar1=HUGE, scalar2=0.0,
+                        op0=ALU.min, op1=ALU.max,
+                    )
+                    nc.gpsimd.tensor_scalar(
+                        out=c[:], in0=c[:], scalar1=4.0, scalar2=1.0, op0=ALU.mult, op1=ALU.mult
+                    )
+                    cc[g, j] = c
+
+        def stage_z(g, j):
+            if True:
+                z = psum.tile([P, O], F32, name="z", tag="zp", bufs=4)
+                for ob in range(4):
+                    dst = z[:, P * ob : P * ob + P]
+                    src = aa[g][:, ob, P * j : P * j + P]
+                    if kind_of(g, j) == "P":
+                        nc.tensor.transpose(dst, src, ident[:])
+                    else:
+                        nc.tensor.matmul(dst, lhsT=src, rhs=ident[:], start=True, stop=False, is_transpose=True)
+                        nc.tensor.matmul(
+                            dst, lhsT=cc[g, j][:, ob, :], rhs=ident[:], start=False, stop=True, is_transpose=True
+                        )
+                zz[g, j] = z
+
+        def out_view(g, j):
+            if g not in oo:
+                oo[g] = op.tile([P, J, O], F32, name="o")
+            return oo[g][:, j, :].rearrange("p (m b) -> p m b", b=4)
+
+        def z_view(g, j):
+            return zz[g, j][:].rearrange("p (b m) -> p m b", b=4)
+
+        def stage_c(g, j):
+            if kind_of(g, j) == "QS":
+                nc.scalar.copy(out=out_view(g, j), in_=z_view(g, j))
+            if kind_of(g, j) == "P":
+                rr[g, j] = ap.tile([P, O], F32, name="r", bufs=4)
+                nc.scalar.copy(out=rr[g, j][:].rearrange("p (m b) -> p m b", b=4), in_=z_view(g, j))
+
+        def stage_l(g, j):
+            if kind_of(g, j) in ("QV", "VV"):
+                nc.vector.tensor_scalar(
+                    out=out_view(g, j), in0=z_view(g, j), scalar1=256.0, scalar2=-256.0, op0=ALU.min, op1=ALU.max
+                )
+            if kind_of(g, j) == "P":
+                nc.vector.scalar_tensor_tensor(
+                    out=out_view(g, j),
+                    in0=z_view(g, j),
+                    scalar=5.0,
+                    in1=rr.pop((g, j))[:].rearrange("p (m b) -> p m b", b=4),
+                    op0=ALU.mult,
+                    op1=ALU.max,
+                )
+
+        def stage_k(g, j):
+            if kind_of(g, j) in ("P", "QS"):
+                ov = oo[g][:, j, :]
+                eng = nc.vector if g == GROUPS - 1 else nc.gpsimd
+                eng.tensor_scalar(out=ov, in0=ov, scalar1=256.0, scalar2=-256.0, op0=ALU.min, op1=ALU.max)
+
+        def stage_o(g):
+            nc.sync.dma_start(out=og[g], in_=oo.pop(g)[:])
+
+        stage_x(0)
+        stage_x(1)
+        nc.gpsimd.tensor_tensor(out=w2[:, halves[0], :], in0=wt[:, halves[0], :], in1=wt[:, halves[0], :], op=ALU.mult)
+        nc.scalar.activation(w2[:, halves[1], :], wt[:, halves[1], :], ACT.Square)
+        nc.scalar.activation(sq[:], styT[:].rearrange("p t n -> p n t"), ACT.Square)
+        stage_a(0, 0)
+        nc.vector.quantize_mx(out=wc[:].bitcast(X4), scales=wcs[:], in_=wt[:].rearrange("p o t -> p (o t)"))
+        stage_a(0, 1)
+        nc.vector.quantize_mx(out=w2c[:].bitcast(X4), scales=w2s[:], in_=w2[:].rearrange("p o t -> p (o t)"))
+        nc.vector.quantize_mx(out=sqc[:].bitcast(X4), scales=sqs[:], in_=sq[:].rearrange("p n t -> p (n t)"))
+        stage_b(0)
+        dp = psum.tile([P, 4, N], F32, name="dp", tag="zp", bufs=4)
+        for ob in range(4):
+            nc.tensor.matmul_mx(
+                out=dp[:, ob, :],
+                lhsT=w2c[:, P * ob : P * ob + P].bitcast(X4),
+                lhsT_scale=w2s[:, P * ob : P * ob + P],
+                rhs=sqc[:].bitcast(X4),
+                rhs_scale=sqs[:],
+                start=True,
+                stop=True,
+            )
+        bT = const.tile([P, 4], F32, name="bT")
+        nc.vector.tensor_scalar(out=bT[:], in0=bb[:], scalar1=gain, scalar2=None, op0=ALU.mult)
+        dT = const.tile([P, 4, N], F32, name="dT")
+        nc.scalar.activation(
+            dT[:], dp[:], ACT.Abs_reciprocal_sqrt, scale=1.0 / gain**2, bias=EPS / gain**2
+        )
+
+        def has(g):
+            return 0 <= g < GROUPS
+
+        for i in range(GROUPS + 4):
+            if has(i):
+                stage_m(i)
+            if has(i + 2):
+                stage_x(i + 2)
+            if has(i - 1):
+                stage_z(i - 1, 0)
+            if has(i - 2):
+                stage_z(i - 2, 1)
+            if has(i):
+                stage_e(i, 0)
+                stage_e(i, 1, on_vector=i == GROUPS - 1)
+            if has(i - 1):
+                stage_c(i - 1, 0)
+            if has(i - 2):
+                stage_c(i - 2, 1)
+            if has(i + 1):
+                stage_a(i + 1, 0)
+                stage_a(i + 1, 1)
+            if has(i - 2):
+                stage_l(i - 2, 0)
+            if has(i + 1):
+                stage_b(i + 1)
+            if has(i - 3):
+                stage_l(i - 3, 1)
+            if has(i - 1):
+                stage_q(i - 1)
+            if has(i - 2):
+                stage_k(i - 2, 0)
+            if has(i - 3):
+                stage_k(i - 3, 1)
+                stage_o(i - 3)

@@ -20,17 +20,15 @@ J = 2
 GT = P * J
 GROUPS = N * L // GT
 NS = GT // L
+PS = P // NS
 EPS = 1e-8
-HUGE = 3.0e38
+CLAMP = 256.0
 FLOPS = 2 * N * L * C * O + 2 * N * WD * C + 2 * N * C * O
-KINDS = ["P"]
+AHEAD = 2
 
 
-FIXED = {}
-
-
-def kind_of(g, j):
-    return FIXED.get((g, j), KINDS[(J * g + j) % len(KINDS)])
+def summed(g, j):
+    return g >= GROUPS - 0 or (j == 1 and (False))
 
 
 def tile_modulatemlp_pa_w8_kernel(
@@ -43,7 +41,7 @@ def tile_modulatemlp_pa_w8_kernel(
 
     with ExitStack() as ctx:
         const = ctx.enter_context(tc.tile_pool(name="const", bufs=1))
-        xmp = ctx.enter_context(tc.tile_pool(name="xmp", bufs=3))
+        xmp = ctx.enter_context(tc.tile_pool(name="xmp", bufs=AHEAD + 2))
         ap = ctx.enter_context(tc.tile_pool(name="ap", bufs=4))
         op = ctx.enter_context(tc.tile_pool(name="op", bufs=5))
         psum = ctx.enter_context(tc.psum_pool(name="psum", bufs=1))
@@ -62,23 +60,30 @@ def tile_modulatemlp_pa_w8_kernel(
             )
         sw = const.tile([P, 4 * C], U8, name="sw", align_bytes=64)
         nc.sync.dma_start(out=sw[:], in_=style_w_words[0].rearrange("p n t -> p (n t)"))
-        sb = const.tile([P, 4], BF16, name="sb")
-        nc.sync.dma_start(out=sb[:], in_=style_b.rearrange("(p t) -> p t", t=4))
-        wsb = const.tile([P, 4, C], BF16, name="wsb", align_bytes=64)
         wview = weight.rearrange("(m b) c -> m b c", b=4)
+        wsb = []
         for h in range(2):
-            nc.sync.dma_start(out=wsb[:, 2 * h : 2 * h + 2, :], in_=wview[:, 2 * h : 2 * h + 2, :])
+            wh = const.tile([P, 2, C], BF16, name="wsb%d" % h, align_bytes=64)
+            nc.sync.dma_start(out=wh[:], in_=wview[:, 2 * h : 2 * h + 2, :])
+            wsb.append(wh)
         xtiles = {}
         bb = const.tile([P, 4], BF16, name="bb")
-        g0 = 0
-        for n_g in [1, 1] + [2] * ((GROUPS - 2) // 2):
+        loads = [(0, 1), (1, 1)] + [(g, 2) for g in range(2, GROUPS, 2)]
+
+        def load_x():
+            g0, n_g = loads.pop(0)
             xt = const.tile([P, n_g, J, C], BF16, name="x%d" % g0, align_bytes=64)
             nc.sync.dma_start(out=xt[:], in_=xg[g0 : g0 + n_g].rearrange("g p j c -> p g j c"))
             for k in range(n_g):
                 xtiles[g0 + k] = (xt, k)
-            if g0 == 1:
-                nc.sync.dma_start(out=bb[:], in_=bias.rearrange("(m b) -> m b", b=4))
-            g0 += n_g
+
+        load_x()
+        sb = const.tile([P, 4], BF16, name="sb")
+        nc.sync.dma_start(out=sb[:], in_=style_b.rearrange("(p t) -> p t", t=4))
+        load_x()
+        nc.sync.dma_start(out=bb[:], in_=bias.rearrange("(m b) -> m b", b=4))
+        for k in range(5):
+            load_x()
 
         one = const.tile([P, 1], F32, name="one")
         nc.vector.memset(one[:], 1.0)
@@ -89,12 +94,12 @@ def tile_modulatemlp_pa_w8_kernel(
 
         def transpose_words(dst, words):
             for u in range(2):
-                nc.tensor.transpose(dst[:, u, :], words[:, u : C // 2 : 2], ident[:])
+                nc.tensor.transpose(dst[:, u], words[:, u : C // 2 : 2], ident[:])
 
         w16 = const.tile([P, WD], BF16, name="w16", align_bytes=64)
         nc.vector.tensor_copy(out=w16[:], in_=wb[:].bitcast(F8))
-        wtp = psum.tile([P, 2, 2, P], F32, name="wtp", tag="xp", bufs=2)
-        transpose_words(wtp[:, 0], w16[:].bitcast(F32))
+        wtp = psum.tile([P, 2, P], F32, name="wtp", tag="xp", bufs=2)
+        transpose_words(wtp, w16[:].bitcast(F32))
 
         wt = const.tile([P, O, 4], BF16, name="wt", align_bytes=64)
         wt32 = wt[:].rearrange("p o t -> p (o t)").bitcast(F32)
@@ -111,10 +116,17 @@ def tile_modulatemlp_pa_w8_kernel(
         def turn_weight(h):
             ww = psum.tile([P, 2, 2, P], F32, name="ww", tag="zp", bufs=4)
             for k in range(2):
-                transpose_words(ww[:, k], wsb[:, 2 * h + k, :].bitcast(F32))
+                transpose_words(ww[:, k], wsb[h][:, k, :].bitcast(F32))
             nc.scalar.copy(
                 out=wt32[:, 512 * h : 512 * h + 512].rearrange("p (b r u) -> p b r u", b=2, u=2),
                 in_=ww[:].rearrange("p b u r -> p b r u"),
+            )
+
+        def quantise_half(codes, scales, src, h):
+            nc.vector.quantize_mx(
+                out=codes[:, halves[h]].bitcast(X4),
+                scales=scales[:, halves[h]],
+                in_=src[:, halves[h], :].rearrange("p o t -> p (o t)"),
             )
 
         sscp = const.tile([P, C], U8, name="sscp", align_bytes=64)
@@ -125,7 +137,7 @@ def tile_modulatemlp_pa_w8_kernel(
         wm = const.tile([P, N, 4], BF16, name="wm", align_bytes=64)
         nc.vector.tensor_tensor(
             out=wm[:].rearrange("p n (u e) -> p n u e", u=2),
-            in0=wtp[:, 0].bitcast(BF16).rearrange("p u (n e) -> p n u e", e=2),
+            in0=wtp[:].bitcast(BF16).rearrange("p u (n e) -> p n u e", e=2),
             in1=wsc[:].rearrange("p (u e) -> p u e", u=2).unsqueeze(1).to_broadcast([P, N, 2, 2]),
             op=ALU.mult,
         )
@@ -164,26 +176,25 @@ def tile_modulatemlp_pa_w8_kernel(
                 out=styT[:, t, :], in0=sp[1][:, t - 2, :], scalar1=wscale, scalar2=sb[:, t : t + 1],
                 op0=ALU.mult, op1=ALU.add,
             )
-        turn_weight(1)
 
         xp, xm, xq, yy, aa, cc, zz, rr, oo = {}, {}, {}, {}, {}, {}, {}, {}, {}
 
         def stage_x(g):
             xt, k = xtiles[g]
-            xp[g] = psum.tile([P, J, 2, P], F32, name="xpt", tag="xp", bufs=2)
+            xp[g] = psum.tile([P, 2, NS, J, PS], F32, name="xpt", tag="xp", bufs=2)
             for j in range(J):
-                transpose_words(xp[g][:, j], xt[:, k, j, :].bitcast(F32))
+                transpose_words(xp[g][:, :, :, j, :], xt[:, k, j, :].bitcast(F32))
 
-        def stage_a(g, j):
-            if j == 0:
-                xm[g] = xmp.tile([P, J, P, 4], BF16, name="xm", align_bytes=64)
+        def stage_a(g):
+            xm[g] = xmp.tile([P, GT, 4], BF16, name="xm", align_bytes=64)
             nc.vector.tensor_tensor(
-                out=xm[g][:, j].rearrange("p (n i) (u e) -> p n i u e", n=NS, u=2),
-                in0=xp[g][:, j].bitcast(BF16).rearrange("p u (n i e) -> p n i u e", n=NS, e=2),
+                out=xm[g][:].rearrange("p (n i) (u e) -> p n i u e", n=NS, u=2),
+                in0=xp.pop(g)[:].rearrange("p u n j i -> p u (n j i)").bitcast(BF16)
+                .rearrange("p u (n i e) -> p n i u e", n=NS, e=2),
                 in1=styT[:, :, NS * g : NS * g + NS]
                 .rearrange("p (u e) n -> p n u e", u=2)
                 .unsqueeze(2)
-                .to_broadcast([P, NS, P // NS, 2, 2]),
+                .to_broadcast([P, NS, L, 2, 2]),
                 op=ALU.mult,
             )
 
@@ -191,13 +202,13 @@ def tile_modulatemlp_pa_w8_kernel(
             xc = xmp.tile([P, GT], U32, name="xc", align_bytes=64)
             xs = xmp.tile([P, GT], U8, name="xs", align_bytes=64)
             nc.vector.quantize_mx(
-                out=xc[:].bitcast(X4), scales=xs[:], in_=xm.pop(g)[:].rearrange("p j r t -> p (j r t)")
+                out=xc[:].bitcast(X4), scales=xs[:], in_=xm.pop(g)[:].rearrange("p r t -> p (r t)")
             )
             xq[g] = (xc, xs)
 
-        def stage_m(g):
-            xc, xs = xq.pop(g)
-            for h in range(2):
+        def stage_m(g, hs=(0, 1)):
+            xc, xs = xq[g]
+            for h in hs:
                 y = psum.tile([P, 2, GT], F32, name="y%d" % h, tag="ya" if h == 0 else "yb", bufs=1)
                 for k in range(2):
                     ob = 2 * h + k
@@ -218,7 +229,7 @@ def tile_modulatemlp_pa_w8_kernel(
             y = yy.pop((g, h))
             for k in range(2):
                 ob = 2 * h + k
-                yv = y[:, k, :].rearrange("p (j n i) -> p n j i", j=J, n=NS)
+                yv = y[:, k, :].rearrange("p (n j i) -> p n j i", j=J, n=NS)
                 av = aa[g][:, ob, :].rearrange("p (j n i) -> p n j i", j=J, n=NS)
                 for n in range(NS):
                     s = NS * g + n
@@ -232,39 +243,29 @@ def tile_modulatemlp_pa_w8_kernel(
                             av[:, n], yv[:, n], ACT.Identity, scale=dT[:, ob, s : s + 1], bias=bT[:, ob : ob + 1]
                         )
 
-        def stage_q(g):
-            for j in range(J):
-                if kind_of(g, j) == "VV":
-                    cc[g, j] = ap.tile([P, 4, P], F32, name="c")
-                    nc.vector.tensor_scalar(
-                        out=cc[g, j][:], in0=aa[g][:, :, P * j : P * j + P], scalar1=0.0, scalar2=4.0,
-                        op0=ALU.max, op1=ALU.mult,
-                    )
-                elif kind_of(g, j) != "P":
-                    c = ap.tile([P, 4, P], F32, name="c")
-                    nc.gpsimd.tensor_scalar(
-                        out=c[:], in0=aa[g][:, :, P * j : P * j + P], scalar1=HUGE, scalar2=0.0,
-                        op0=ALU.min, op1=ALU.max,
-                    )
-                    nc.gpsimd.tensor_scalar(
-                        out=c[:], in0=c[:], scalar1=4.0, scalar2=1.0, op0=ALU.mult, op1=ALU.mult
-                    )
-                    cc[g, j] = c
+        def stage_r(g, j):
+            if summed(g, j):
+                cc[g, j] = ap.tile([P, 4, P], F32, name="c", bufs=3)
+                nc.vector.tensor_scalar(
+                    out=cc[g, j][:], in0=aa[g][:, :, P * j : P * j + P], scalar1=0.0, scalar2=4.0,
+                    op0=ALU.max, op1=ALU.mult,
+                )
 
         def stage_z(g, j):
-            if True:
-                z = psum.tile([P, O], F32, name="z", tag="zp", bufs=4)
-                for ob in range(4):
-                    dst = z[:, P * ob : P * ob + P]
-                    src = aa[g][:, ob, P * j : P * j + P]
-                    if kind_of(g, j) == "P":
-                        nc.tensor.transpose(dst, src, ident[:])
-                    else:
-                        nc.tensor.matmul(dst, lhsT=src, rhs=ident[:], start=True, stop=False, is_transpose=True)
-                        nc.tensor.matmul(
-                            dst, lhsT=cc[g, j][:, ob, :], rhs=ident[:], start=False, stop=True, is_transpose=True
-                        )
-                zz[g, j] = z
+            z = psum.tile([P, O], F32, name="z", tag="zp", bufs=4)
+            for ob in range(4):
+                dst = z[:, P * ob : P * ob + P]
+                src = aa[g][:, ob, P * j : P * j + P]
+                if summed(g, j):
+                    nc.tensor.matmul(dst, lhsT=src, rhs=ident[:], start=True, stop=False, is_transpose=True)
+                    nc.tensor.matmul(
+                        dst, lhsT=cc[g, j][:, ob, :], rhs=ident[:], start=False, stop=True, is_transpose=True
+                    )
+                elif j == 0 and ob < 0:
+                    nc.tensor.matmul(dst, lhsT=src, rhs=ident[:], start=True, stop=True)
+                else:
+                    nc.tensor.transpose(dst, src, ident[:])
+            zz[g, j] = z
 
         def out_view(g, j):
             if g not in oo:
@@ -274,19 +275,24 @@ def tile_modulatemlp_pa_w8_kernel(
         def z_view(g, j):
             return zz[g, j][:].rearrange("p (b m) -> p m b", b=4)
 
+        def on_vector_alone(g, j):
+            return summed(g, j) and g >= GROUPS - 0
+
         def stage_c(g, j):
-            if kind_of(g, j) == "QS":
+            if on_vector_alone(g, j):
+                return
+            if summed(g, j):
                 nc.scalar.copy(out=out_view(g, j), in_=z_view(g, j))
-            if kind_of(g, j) == "P":
+            else:
                 rr[g, j] = ap.tile([P, O], F32, name="r", bufs=4)
                 nc.scalar.copy(out=rr[g, j][:].rearrange("p (m b) -> p m b", b=4), in_=z_view(g, j))
 
         def stage_l(g, j):
-            if kind_of(g, j) in ("QV", "VV"):
+            if on_vector_alone(g, j):
                 nc.vector.tensor_scalar(
-                    out=out_view(g, j), in0=z_view(g, j), scalar1=256.0, scalar2=-256.0, op0=ALU.min, op1=ALU.max
+                    out=out_view(g, j), in0=z_view(g, j), scalar1=CLAMP, scalar2=-CLAMP, op0=ALU.min, op1=ALU.max
                 )
-            if kind_of(g, j) == "P":
+            elif not summed(g, j):
                 nc.vector.scalar_tensor_tensor(
                     out=out_view(g, j),
                     in0=z_view(g, j),
@@ -297,75 +303,110 @@ def tile_modulatemlp_pa_w8_kernel(
                 )
 
         def stage_k(g, j):
-            if kind_of(g, j) in ("P", "QS"):
+            if on_vector_alone(g, j):
+                return
+            if g >= GROUPS - 3:
                 ov = oo[g][:, j, :]
-                eng = nc.vector if g == GROUPS - 1 else nc.gpsimd
-                eng.tensor_scalar(out=ov, in0=ov, scalar1=256.0, scalar2=-256.0, op0=ALU.min, op1=ALU.max)
+            elif j == 1:
+                ov = oo[g][:].rearrange("p j o -> p (j o)")
+            else:
+                return
+            eng = nc.vector if J * g + j >= J * GROUPS - 4 else nc.gpsimd
+            eng.tensor_scalar(out=ov, in0=ov, scalar1=CLAMP, scalar2=-CLAMP, op0=ALU.min, op1=ALU.max)
 
-        def stage_o(g):
-            nc.sync.dma_start(out=og[g], in_=oo.pop(g)[:])
+        def stage_o(g, j):
+            if g >= GROUPS - 3:
+                nc.sync.dma_start(out=og[g][:, j, :], in_=oo[g][:, j, :])
+            elif j == 1:
+                nc.sync.dma_start(out=og[g], in_=oo.pop(g)[:])
+                if g % 2 == 1 and loads:
+                    load_x()
+
+        dT = const.tile([P, 4, N], F32, name="dT")
+        bT = const.tile([P, 4], F32, name="bT")
+
+        def demod_half(h):
+            dp = psum.tile([P, 2, N], F32, name="dp", tag="zp", bufs=4)
+            for k in range(2):
+                ob = 2 * h + k
+                nc.tensor.matmul_mx(
+                    out=dp[:, k, :],
+                    lhsT=w2c[:, P * ob : P * ob + P].bitcast(X4),
+                    lhsT_scale=w2s[:, P * ob : P * ob + P],
+                    rhs=sqc[:].bitcast(X4),
+                    rhs_scale=sqs[:],
+                    start=True,
+                    stop=True,
+                )
+            nc.scalar.activation(
+                dT[:, 2 * h : 2 * h + 2, :], dp[:], ACT.Abs_reciprocal_sqrt, scale=1.0 / gain**2, bias=EPS / gain**2
+            )
 
         stage_x(0)
+        turn_weight(1)
         stage_x(1)
-        nc.gpsimd.tensor_tensor(out=w2[:, halves[0], :], in0=wt[:, halves[0], :], in1=wt[:, halves[0], :], op=ALU.mult)
-        nc.scalar.activation(w2[:, halves[1], :], wt[:, halves[1], :], ACT.Square)
         nc.scalar.activation(sq[:], styT[:].rearrange("p t n -> p n t"), ACT.Square)
-        stage_a(0, 0)
-        nc.vector.quantize_mx(out=wc[:].bitcast(X4), scales=wcs[:], in_=wt[:].rearrange("p o t -> p (o t)"))
-        stage_a(0, 1)
-        nc.vector.quantize_mx(out=w2c[:].bitcast(X4), scales=w2s[:], in_=w2[:].rearrange("p o t -> p (o t)"))
-        nc.vector.quantize_mx(out=sqc[:].bitcast(X4), scales=sqs[:], in_=sq[:].rearrange("p n t -> p (n t)"))
+        quantise_half(wc, wcs, wt, 0)
+        stage_a(0)
+        nc.vector.tensor_tensor(out=w2[:, halves[0], :], in0=wt[:, halves[0], :], in1=wt[:, halves[0], :], op=ALU.mult)
+        nc.scalar.activation(w2[:, halves[1], :], wt[:, halves[1], :], ACT.Square)
+        nc.scalar.activation(bT[:], bb[:], ACT.Copy, scale=gain)
         stage_b(0)
-        dp = psum.tile([P, 4, N], F32, name="dp", tag="zp", bufs=4)
-        for ob in range(4):
-            nc.tensor.matmul_mx(
-                out=dp[:, ob, :],
-                lhsT=w2c[:, P * ob : P * ob + P].bitcast(X4),
-                lhsT_scale=w2s[:, P * ob : P * ob + P],
-                rhs=sqc[:].bitcast(X4),
-                rhs_scale=sqs[:],
-                start=True,
-                stop=True,
-            )
-        bT = const.tile([P, 4], F32, name="bT")
-        nc.vector.tensor_scalar(out=bT[:], in0=bb[:], scalar1=gain, scalar2=None, op0=ALU.mult)
-        dT = const.tile([P, 4, N], F32, name="dT")
-        nc.scalar.activation(
-            dT[:], dp[:], ACT.Abs_reciprocal_sqrt, scale=1.0 / gain**2, bias=EPS / gain**2
-        )
+        quantise_half(w2c, w2s, w2, 0)
+        nc.vector.quantize_mx(out=sqc[:].bitcast(X4), scales=sqs[:], in_=sq[:].rearrange("p n t -> p (n t)"))
+        stage_x(2)
+        stage_m(0, (0,))
+        demod_half(0)
+        quantise_half(wc, wcs, wt, 1)
+        quantise_half(w2c, w2s, w2, 1)
+        stage_a(1)
+        stage_m(0, (1,))
+        stage_e(0, 0)
+        demod_half(1)
+        stage_x(3)
+        stage_b(1)
+        stage_a(2)
+        stage_e(0, 1)
+        stage_b(2)
 
         def has(g):
             return 0 <= g < GROUPS
 
-        for i in range(GROUPS + 4):
+        def prepared(i):
+            return [g for g in [i + AHEAD] if has(g)]
+
+        for i in range(1, GROUPS + 4):
+            todo = prepared(i)
             if has(i):
                 stage_m(i)
-            if has(i + 2):
-                stage_x(i + 2)
             if has(i - 1):
+                stage_r(i - 1, 0)
                 stage_z(i - 1, 0)
+            for g in todo:
+                if has(g + 1):
+                    stage_x(g + 1)
             if has(i - 2):
                 stage_z(i - 2, 1)
             if has(i):
                 stage_e(i, 0)
-                stage_e(i, 1, on_vector=i == GROUPS - 1)
+            for g in todo:
+                stage_a(g)
+            if has(i - 2):
+                stage_l(i - 2, 0)
+            if has(i):
+                stage_e(i, 1, on_vector=i >= GROUPS - 1)
             if has(i - 1):
                 stage_c(i - 1, 0)
             if has(i - 2):
                 stage_c(i - 2, 1)
-            if has(i + 1):
-                stage_a(i + 1, 0)
-                stage_a(i + 1, 1)
-            if has(i - 2):
-                stage_l(i - 2, 0)
-            if has(i + 1):
-                stage_b(i + 1)
+            for g in todo:
+                stage_b(g)
+            if has(i - 1):
+                stage_r(i - 1, 1)
             if has(i - 3):
                 stage_l(i - 3, 1)
-            if has(i - 1):
-                stage_q(i - 1)
+                stage_k(i - 3, 1)
+                stage_o(i - 3, 1)
             if has(i - 2):
                 stage_k(i - 2, 0)
-            if has(i - 3):
-                stage_k(i - 3, 1)
-                stage_o(i - 3)
+                stage_o(i - 2, 0)

@@ -60,14 +60,14 @@ def tile_modulatemlp_pa_w8_kernel(
             )
         sw = const.tile([P, 4 * C], U8, name="sw", align_bytes=64)
         nc.sync.dma_start(out=sw[:], in_=style_w_words[0].rearrange("p n t -> p (n t)"))
-        wview = weight.rearrange("(m b) c -> m b c", b=4)
+        wview = weight.rearrange("(b m) c -> m b c", b=4)
         wsb = []
         for h in range(2):
             wh = const.tile([P, 2, C], BF16, name="wsb%d" % h, align_bytes=64)
             nc.sync.dma_start(out=wh[:], in_=wview[:, 2 * h : 2 * h + 2, :])
             wsb.append(wh)
         xtiles = {}
-        bb = const.tile([P, 4], BF16, name="bb")
+        bb = const.tile([P, 4, 2], BF16, name="bb")
         loads = [(0, 1), (1, 1)] + [(g, 2) for g in range(2, GROUPS, 2)]
 
         def load_x():
@@ -81,7 +81,8 @@ def tile_modulatemlp_pa_w8_kernel(
         sb = const.tile([P, 4], BF16, name="sb")
         nc.sync.dma_start(out=sb[:], in_=style_b.rearrange("(p t) -> p t", t=4))
         load_x()
-        nc.sync.dma_start(out=bb[:], in_=bias.rearrange("(m b) -> m b", b=4))
+        with nc.allow_non_contiguous_dma(reason="one bias value a partition and block"):
+            nc.sync.dma_start(out=bb[:, :, 0], in_=bias.rearrange("(b m) -> m b", b=4))
         for k in range(5):
             load_x()
 
@@ -151,14 +152,11 @@ def tile_modulatemlp_pa_w8_kernel(
         nc.vector.quantize_mx(out=wq[:].bitcast(X4), scales=wqs[:], in_=wm[:].rearrange("p n t -> p (n t)"))
         turn_weight(0)
 
-        styT = const.tile([P, 4, N], F32, name="styT", align_bytes=64)
-        sp = [
-            psum.tile([P, 2, P], F32, name="sp0", tag="ya", bufs=1),
-            psum.tile([P, 2, P], F32, name="sp1", tag="yb", bufs=1),
-        ]
+        styT = const.tile([P, N, 4], F32, name="styT", align_bytes=64)
+        sp = psum.tile([P, 4, N], F32, name="sp", tag="ya", bufs=1)
         for t in range(4):
             nc.tensor.matmul_mx(
-                out=sp[t // 2][:, t % 2, :],
+                out=sp[:, t, :],
                 lhsT=swp[:, P * t : P * t + P].bitcast(X4),
                 lhsT_scale=sscp[:, P * t : P * t + P],
                 rhs=wq[:].bitcast(X4),
@@ -166,16 +164,14 @@ def tile_modulatemlp_pa_w8_kernel(
                 start=True,
                 stop=True,
             )
-        wscale = 1.0 / math.sqrt(WD)
-        for t in range(2):
-            nc.scalar.activation(
-                styT[:, t, :], sp[0][:, t, :], ACT.Identity, scale=wscale, bias=sb[:, t : t + 1]
-            )
-        for t in range(2, 4):
-            nc.vector.tensor_scalar(
-                out=styT[:, t, :], in0=sp[1][:, t - 2, :], scalar1=wscale, scalar2=sb[:, t : t + 1],
-                op0=ALU.mult, op1=ALU.add,
-            )
+        nc.vector.scalar_tensor_tensor(
+            out=styT[:],
+            in0=sp[:].rearrange("p t n -> p n t"),
+            scalar=1.0 / math.sqrt(WD),
+            in1=sb[:].unsqueeze(1).to_broadcast([P, N, 4]),
+            op0=ALU.mult,
+            op1=ALU.add,
+        )
 
         xp, xm, xq, yy, aa, cc, zz, rr, oo = {}, {}, {}, {}, {}, {}, {}, {}, {}
 
@@ -191,8 +187,8 @@ def tile_modulatemlp_pa_w8_kernel(
                 out=xm[g][:].rearrange("p (n i) (u e) -> p n i u e", n=NS, u=2),
                 in0=xp.pop(g)[:].rearrange("p u n j i -> p u (n j i)").bitcast(BF16)
                 .rearrange("p u (n i e) -> p n i u e", n=NS, e=2),
-                in1=styT[:, :, NS * g : NS * g + NS]
-                .rearrange("p (u e) n -> p n u e", u=2)
+                in1=styT[:, NS * g : NS * g + NS, :]
+                .rearrange("p n (u e) -> p n u e", u=2)
                 .unsqueeze(2)
                 .to_broadcast([P, NS, L, 2, 2]),
                 op=ALU.mult,
@@ -233,7 +229,7 @@ def tile_modulatemlp_pa_w8_kernel(
                 av = aa[g][:, ob, :].rearrange("p (j n i) -> p n j i", j=J, n=NS)
                 for n in range(NS):
                     s = NS * g + n
-                    if on_vector:
+                    if on_vector or (False):
                         nc.vector.tensor_scalar(
                             out=av[:, n], in0=yv[:, n], scalar1=dT[:, ob, s : s + 1], scalar2=bT[:, ob : ob + 1],
                             op0=ALU.mult, op1=ALU.add,
@@ -261,7 +257,7 @@ def tile_modulatemlp_pa_w8_kernel(
                     nc.tensor.matmul(
                         dst, lhsT=cc[g, j][:, ob, :], rhs=ident[:], start=False, stop=True, is_transpose=True
                     )
-                elif j == 0 and ob < 0:
+                elif False:
                     nc.tensor.matmul(dst, lhsT=src, rhs=ident[:], start=True, stop=True)
                 else:
                     nc.tensor.transpose(dst, src, ident[:])
@@ -270,13 +266,13 @@ def tile_modulatemlp_pa_w8_kernel(
         def out_view(g, j):
             if g not in oo:
                 oo[g] = op.tile([P, J, O], F32, name="o")
-            return oo[g][:, j, :].rearrange("p (m b) -> p m b", b=4)
+            return oo[g][:, j, :]
 
         def z_view(g, j):
-            return zz[g, j][:].rearrange("p (b m) -> p m b", b=4)
+            return zz[g, j][:]
 
         def on_vector_alone(g, j):
-            return summed(g, j) and g >= GROUPS - 0
+            return summed(g, j) and (True)
 
         def stage_c(g, j):
             if on_vector_alone(g, j):
@@ -285,26 +281,22 @@ def tile_modulatemlp_pa_w8_kernel(
                 nc.scalar.copy(out=out_view(g, j), in_=z_view(g, j))
             else:
                 rr[g, j] = ap.tile([P, O], F32, name="r", bufs=4)
-                nc.scalar.copy(out=rr[g, j][:].rearrange("p (m b) -> p m b", b=4), in_=z_view(g, j))
+                nc.scalar.copy(out=rr[g, j][:], in_=z_view(g, j))
 
         def stage_l(g, j):
             if on_vector_alone(g, j):
-                nc.vector.tensor_scalar(
-                    out=out_view(g, j), in0=z_view(g, j), scalar1=CLAMP, scalar2=-CLAMP, op0=ALU.min, op1=ALU.max
-                )
+                nc.vector.tensor_copy(out=out_view(g, j), in_=z_view(g, j))
             elif not summed(g, j):
                 nc.vector.scalar_tensor_tensor(
                     out=out_view(g, j),
                     in0=z_view(g, j),
                     scalar=5.0,
-                    in1=rr.pop((g, j))[:].rearrange("p (m b) -> p m b", b=4),
+                    in1=rr.pop((g, j))[:],
                     op0=ALU.mult,
                     op1=ALU.max,
                 )
 
         def stage_k(g, j):
-            if on_vector_alone(g, j):
-                return
             if g >= GROUPS - 3:
                 ov = oo[g][:, j, :]
             elif j == 1:
@@ -345,12 +337,12 @@ def tile_modulatemlp_pa_w8_kernel(
         stage_x(0)
         turn_weight(1)
         stage_x(1)
-        nc.scalar.activation(sq[:], styT[:].rearrange("p t n -> p n t"), ACT.Square)
+        nc.scalar.activation(sq[:], styT[:], ACT.Square)
         quantise_half(wc, wcs, wt, 0)
         stage_a(0)
         nc.vector.tensor_tensor(out=w2[:, halves[0], :], in0=wt[:, halves[0], :], in1=wt[:, halves[0], :], op=ALU.mult)
         nc.scalar.activation(w2[:, halves[1], :], wt[:, halves[1], :], ACT.Square)
-        nc.scalar.activation(bT[:], bb[:], ACT.Copy, scale=gain)
+        nc.scalar.activation(bT[:], bb[:, :, 0], ACT.Copy, scale=gain)
         stage_b(0)
         quantise_half(w2c, w2s, w2, 0)
         nc.vector.quantize_mx(out=sqc[:].bitcast(X4), scales=sqs[:], in_=sq[:].rearrange("p n t -> p (n t)"))

@@ -51,6 +51,11 @@ def tile_modulatemlp_pa_w8_kernel(
         nc.sync.dma_start(out=wb[:], in_=w_bytes)
         wsc = const.tile([P, 4], F32, name="wsc")
         nc.sync.dma_start(out=wsc[:], in_=w_scale.rearrange("o (p t) -> p (o t)", t=4))
+        wview = weight.rearrange("(b m) c -> m b c", b=4)
+        wsb = [const.tile([P, 2, C], BF16, name="wsb%d" % h, align_bytes=64) for h in range(2)]
+        nc.sync.dma_start(out=wsb[0][:], in_=wview[:, 0:2, :])
+        sw = const.tile([P, 4 * C], U8, name="sw", align_bytes=64)
+        nc.sync.dma_start(out=sw[:], in_=style_w_words[0].rearrange("p n t -> p (n t)"))
         ssc = const.tile([P, C], U8, name="ssc", align_bytes=64)
         nc.vector.memset(ssc[:].bitcast(U32), 0)
         for q in range(4):
@@ -58,14 +63,7 @@ def tile_modulatemlp_pa_w8_kernel(
                 out=ssc[32 * q : 32 * q + 4, :].bitcast(I32),
                 in_=style_w_scales[0][4 * q : 4 * q + 4, :].bitcast(I32),
             )
-        sw = const.tile([P, 4 * C], U8, name="sw", align_bytes=64)
-        nc.sync.dma_start(out=sw[:], in_=style_w_words[0].rearrange("p n t -> p (n t)"))
-        wview = weight.rearrange("(b m) c -> m b c", b=4)
-        wsb = []
-        for h in range(2):
-            wh = const.tile([P, 2, C], BF16, name="wsb%d" % h, align_bytes=64)
-            nc.sync.dma_start(out=wh[:], in_=wview[:, 2 * h : 2 * h + 2, :])
-            wsb.append(wh)
+        nc.sync.dma_start(out=wsb[1][:], in_=wview[:, 2:4, :])
         xtiles = {}
         bb = const.tile([P, 4, 2], BF16, name="bb")
         loads = [(0, 1), (1, 1)] + [(g, 2) for g in range(2, GROUPS, 2)]
@@ -130,11 +128,8 @@ def tile_modulatemlp_pa_w8_kernel(
                 in_=src[:, halves[h], :].rearrange("p o t -> p (o t)"),
             )
 
-        sscp = const.tile([P, C], U8, name="sscp", align_bytes=64)
-        nc.vector.tensor_copy(
-            out=sscp[:].rearrange("p (t m) -> p t m", t=4),
-            in_=ssc[:].rearrange("p (m t) -> p t m", t=4),
-        )
+        turn_weight(0)
+        nc.scalar.activation(w2[:, halves[0], :], wt[:, halves[0], :], ACT.Square)
         wm = const.tile([P, N, 4], BF16, name="wm", align_bytes=64)
         nc.vector.tensor_tensor(
             out=wm[:].rearrange("p n (u e) -> p n u e", u=2),
@@ -150,7 +145,12 @@ def tile_modulatemlp_pa_w8_kernel(
         wq = const.tile([P, N], U32, name="wq", align_bytes=64)
         wqs = const.tile([P, N], U8, name="wqs", align_bytes=64)
         nc.vector.quantize_mx(out=wq[:].bitcast(X4), scales=wqs[:], in_=wm[:].rearrange("p n t -> p (n t)"))
-        turn_weight(0)
+        sscp = const.tile([P, C], U8, name="sscp", align_bytes=64)
+        nc.vector.tensor_copy(
+            out=sscp[:].rearrange("p (t m) -> p t m", t=4),
+            in_=ssc[:].rearrange("p (m t) -> p t m", t=4),
+        )
+        quantise_half(wc, wcs, wt, 0)
 
         styT = const.tile([P, N, 4], F32, name="styT", align_bytes=64)
         sp = psum.tile([P, 4, N], F32, name="sp", tag="ya", bufs=1)
@@ -229,7 +229,7 @@ def tile_modulatemlp_pa_w8_kernel(
                 av = aa[g][:, ob, :].rearrange("p (j n i) -> p n j i", j=J, n=NS)
                 for n in range(NS):
                     s = NS * g + n
-                    if on_vector or (False):
+                    if on_vector or (h == 1 and g % 8 == 3):
                         nc.vector.tensor_scalar(
                             out=av[:, n], in0=yv[:, n], scalar1=dT[:, ob, s : s + 1], scalar2=bT[:, ob : ob + 1],
                             op0=ALU.mult, op1=ALU.add,
@@ -297,17 +297,17 @@ def tile_modulatemlp_pa_w8_kernel(
                 )
 
         def stage_k(g, j):
-            if g >= GROUPS - 3:
+            if g >= GROUPS - 4:
                 ov = oo[g][:, j, :]
             elif j == 1:
                 ov = oo[g][:].rearrange("p j o -> p (j o)")
             else:
                 return
-            eng = nc.vector if J * g + j >= J * GROUPS - 4 else nc.gpsimd
+            eng = nc.vector if J * g + j >= J * GROUPS - 8 else nc.gpsimd
             eng.tensor_scalar(out=ov, in0=ov, scalar1=CLAMP, scalar2=-CLAMP, op0=ALU.min, op1=ALU.max)
 
         def stage_o(g, j):
-            if g >= GROUPS - 3:
+            if g >= GROUPS - 4:
                 nc.sync.dma_start(out=og[g][:, j, :], in_=oo[g][:, j, :])
             elif j == 1:
                 nc.sync.dma_start(out=og[g], in_=oo.pop(g)[:])
@@ -335,26 +335,23 @@ def tile_modulatemlp_pa_w8_kernel(
             )
 
         stage_x(0)
+        nc.scalar.activation(sq[:], styT[:], ACT.Square)
         turn_weight(1)
         stage_x(1)
-        nc.scalar.activation(sq[:], styT[:], ACT.Square)
-        quantise_half(wc, wcs, wt, 0)
-        stage_a(0)
-        nc.vector.tensor_tensor(out=w2[:, halves[0], :], in0=wt[:, halves[0], :], in1=wt[:, halves[0], :], op=ALU.mult)
         nc.scalar.activation(w2[:, halves[1], :], wt[:, halves[1], :], ACT.Square)
         nc.scalar.activation(bT[:], bb[:, :, 0], ACT.Copy, scale=gain)
-        stage_b(0)
         quantise_half(w2c, w2s, w2, 0)
+        stage_a(0)
         nc.vector.quantize_mx(out=sqc[:].bitcast(X4), scales=sqs[:], in_=sq[:].rearrange("p n t -> p (n t)"))
-        stage_x(2)
-        stage_m(0, (0,))
-        demod_half(0)
         quantise_half(wc, wcs, wt, 1)
+        stage_b(0)
+        demod_half(0)
+        stage_m(0)
         quantise_half(w2c, w2s, w2, 1)
         stage_a(1)
-        stage_m(0, (1,))
         stage_e(0, 0)
         demod_half(1)
+        stage_x(2)
         stage_x(3)
         stage_b(1)
         stage_a(2)
@@ -372,7 +369,6 @@ def tile_modulatemlp_pa_w8_kernel(
             if has(i):
                 stage_m(i)
             if has(i - 1):
-                stage_r(i - 1, 0)
                 stage_z(i - 1, 0)
             for g in todo:
                 if has(g + 1):
@@ -386,19 +382,20 @@ def tile_modulatemlp_pa_w8_kernel(
             if has(i - 2):
                 stage_l(i - 2, 0)
             if has(i):
-                stage_e(i, 1, on_vector=i >= GROUPS - 1)
+                stage_e(i, 1, on_vector=i >= GROUPS - 2)
             if has(i - 1):
                 stage_c(i - 1, 0)
             if has(i - 2):
                 stage_c(i - 2, 1)
+            if has(i - 3):
+                stage_l(i - 3, 1)
             for g in todo:
                 stage_b(g)
             if has(i - 1):
                 stage_r(i - 1, 1)
-            if has(i - 3):
-                stage_l(i - 3, 1)
-                stage_k(i - 3, 1)
-                stage_o(i - 3, 1)
             if has(i - 2):
                 stage_k(i - 2, 0)
                 stage_o(i - 2, 0)
+            if has(i - 3):
+                stage_k(i - 3, 1)
+                stage_o(i - 3, 1)

@@ -41,7 +41,7 @@ def tile_modulatemlp_pa_w8_kernel(
 
     with ExitStack() as ctx:
         const = ctx.enter_context(tc.tile_pool(name="const", bufs=1))
-        xmp = ctx.enter_context(tc.tile_pool(name="xmp", bufs=AHEAD + 2))
+        xmp = ctx.enter_context(tc.tile_pool(name="xmp", bufs=AHEAD + 2 + GROUPS // 99))
         ap = ctx.enter_context(tc.tile_pool(name="ap", bufs=4))
         op = ctx.enter_context(tc.tile_pool(name="op", bufs=5))
         psum = ctx.enter_context(tc.psum_pool(name="psum", bufs=1))
@@ -152,11 +152,14 @@ def tile_modulatemlp_pa_w8_kernel(
         )
         quantise_half(wc, wcs, wt, 0)
 
-        styT = const.tile([P, N, 4], F32, name="styT", align_bytes=64)
-        sp = psum.tile([P, 4, N], F32, name="sp", tag="ya", bufs=1)
+        styT = const.tile([P, 4, N], F32, name="styT", align_bytes=64)
+        sp = [
+            psum.tile([P, 2, P], F32, name="sp0", tag="ya", bufs=1),
+            psum.tile([P, 2, P], F32, name="sp1", tag="yb", bufs=1),
+        ]
         for t in range(4):
             nc.tensor.matmul_mx(
-                out=sp[:, t, :],
+                out=sp[t // 2][:, t % 2, :],
                 lhsT=swp[:, P * t : P * t + P].bitcast(X4),
                 lhsT_scale=sscp[:, P * t : P * t + P],
                 rhs=wq[:].bitcast(X4),
@@ -164,14 +167,16 @@ def tile_modulatemlp_pa_w8_kernel(
                 start=True,
                 stop=True,
             )
-        nc.vector.scalar_tensor_tensor(
-            out=styT[:],
-            in0=sp[:].rearrange("p t n -> p n t"),
-            scalar=1.0 / math.sqrt(WD),
-            in1=sb[:].unsqueeze(1).to_broadcast([P, N, 4]),
-            op0=ALU.mult,
-            op1=ALU.add,
-        )
+        wscale = 1.0 / math.sqrt(WD)
+        for t in range(2):
+            nc.scalar.activation(
+                styT[:, t, :], sp[0][:, t, :], ACT.Identity, scale=wscale, bias=sb[:, t : t + 1]
+            )
+        for t in range(2, 4):
+            nc.vector.tensor_scalar(
+                out=styT[:, t, :], in0=sp[1][:, t - 2, :], scalar1=wscale, scalar2=sb[:, t : t + 1],
+                op0=ALU.mult, op1=ALU.add,
+            )
 
         xp, xm, xq, yy, aa, cc, zz, rr, oo = {}, {}, {}, {}, {}, {}, {}, {}, {}
 
@@ -187,8 +192,8 @@ def tile_modulatemlp_pa_w8_kernel(
                 out=xm[g][:].rearrange("p (n i) (u e) -> p n i u e", n=NS, u=2),
                 in0=xp.pop(g)[:].rearrange("p u n j i -> p u (n j i)").bitcast(BF16)
                 .rearrange("p u (n i e) -> p n i u e", n=NS, e=2),
-                in1=styT[:, NS * g : NS * g + NS, :]
-                .rearrange("p n (u e) -> p n u e", u=2)
+                in1=styT[:, :, NS * g : NS * g + NS]
+                .rearrange("p (u e) n -> p n u e", u=2)
                 .unsqueeze(2)
                 .to_broadcast([P, NS, L, 2, 2]),
                 op=ALU.mult,
@@ -229,7 +234,7 @@ def tile_modulatemlp_pa_w8_kernel(
                 av = aa[g][:, ob, :].rearrange("p (j n i) -> p n j i", j=J, n=NS)
                 for n in range(NS):
                     s = NS * g + n
-                    if on_vector or (h == 1 and g % 8 == 3):
+                    if on_vector or (h == 1 and g % 16 == 7):
                         nc.vector.tensor_scalar(
                             out=av[:, n], in0=yv[:, n], scalar1=dT[:, ob, s : s + 1], scalar2=bT[:, ob : ob + 1],
                             op0=ALU.mult, op1=ALU.add,
@@ -297,17 +302,17 @@ def tile_modulatemlp_pa_w8_kernel(
                 )
 
         def stage_k(g, j):
-            if g >= GROUPS - 4:
+            if g >= GROUPS - 3:
                 ov = oo[g][:, j, :]
             elif j == 1:
                 ov = oo[g][:].rearrange("p j o -> p (j o)")
             else:
                 return
-            eng = nc.vector if J * g + j >= J * GROUPS - 8 else nc.gpsimd
+            eng = nc.vector if J * g + j >= J * GROUPS - 6 else nc.gpsimd
             eng.tensor_scalar(out=ov, in0=ov, scalar1=CLAMP, scalar2=-CLAMP, op0=ALU.min, op1=ALU.max)
 
         def stage_o(g, j):
-            if g >= GROUPS - 4:
+            if g >= GROUPS - 3:
                 nc.sync.dma_start(out=og[g][:, j, :], in_=oo[g][:, j, :])
             elif j == 1:
                 nc.sync.dma_start(out=og[g], in_=oo.pop(g)[:])
@@ -335,7 +340,7 @@ def tile_modulatemlp_pa_w8_kernel(
             )
 
         stage_x(0)
-        nc.scalar.activation(sq[:], styT[:], ACT.Square)
+        nc.scalar.activation(sq[:], styT[:].rearrange("p t n -> p n t"), ACT.Square)
         turn_weight(1)
         stage_x(1)
         nc.scalar.activation(w2[:, halves[1], :], wt[:, halves[1], :], ACT.Square)
@@ -362,7 +367,8 @@ def tile_modulatemlp_pa_w8_kernel(
             return 0 <= g < GROUPS
 
         def prepared(i):
-            return [g for g in [i + AHEAD] if has(g)]
+            first, last = i + AHEAD + (i - 1) // 99, i + AHEAD + i // 99
+            return [g for g in range(first, last + 1) if has(g)]
 
         for i in range(1, GROUPS + 4):
             todo = prepared(i)
@@ -370,17 +376,21 @@ def tile_modulatemlp_pa_w8_kernel(
                 stage_m(i)
             if has(i - 1):
                 stage_z(i - 1, 0)
-            for g in todo:
+            for g in todo[:1]:
                 if has(g + 1):
                     stage_x(g + 1)
             if has(i - 2):
                 stage_z(i - 2, 1)
             if has(i):
                 stage_e(i, 0)
-            for g in todo:
+            for g in todo[:1]:
                 stage_a(g)
             if has(i - 2):
                 stage_l(i - 2, 0)
+            for g in todo[1:]:
+                if has(g + 1):
+                    stage_x(g + 1)
+                stage_a(g)
             if has(i):
                 stage_e(i, 1, on_vector=i >= GROUPS - 2)
             if has(i - 1):

@@ -28,7 +28,7 @@ AHEAD = 2
 
 
 def summed(g, j):
-    return g >= GROUPS - 0 or (j == 1 and (False))
+    return g >= GROUPS - 0 or (j == 1 and (g < 29))
 
 
 def tile_modulatemlp_pa_w8_kernel(
@@ -41,7 +41,7 @@ def tile_modulatemlp_pa_w8_kernel(
 
     with ExitStack() as ctx:
         const = ctx.enter_context(tc.tile_pool(name="const", bufs=1))
-        xmp = ctx.enter_context(tc.tile_pool(name="xmp", bufs=AHEAD + 2 + GROUPS // 99))
+        xmp = ctx.enter_context(tc.tile_pool(name="xmp", bufs=AHEAD + 2))
         ap = ctx.enter_context(tc.tile_pool(name="ap", bufs=4))
         op = ctx.enter_context(tc.tile_pool(name="op", bufs=5))
         psum = ctx.enter_context(tc.psum_pool(name="psum", bufs=1))
@@ -178,7 +178,7 @@ def tile_modulatemlp_pa_w8_kernel(
                 op0=ALU.mult, op1=ALU.add,
             )
 
-        xp, xm, xq, yy, aa, cc, zz, rr, oo = {}, {}, {}, {}, {}, {}, {}, {}, {}
+        xp, xm, xq, yy, aa, cc, zz, rr, oo, clipped = {}, {}, {}, {}, {}, {}, {}, {}, {}, {}
 
         def stage_x(g):
             xt, k = xtiles[g]
@@ -187,9 +187,9 @@ def tile_modulatemlp_pa_w8_kernel(
                 transpose_words(xp[g][:, :, :, j, :], xt[:, k, j, :].bitcast(F32))
 
         def stage_a(g):
-            xm[g] = xmp.tile([P, GT, 4], BF16, name="xm", align_bytes=64)
+            xm[g] = xmp.tile([P, J * O], F32, name="xm", align_bytes=64, bufs=5)
             nc.vector.tensor_tensor(
-                out=xm[g][:].rearrange("p (n i) (u e) -> p n i u e", n=NS, u=2),
+                out=xm[g][:, : 2 * GT].bitcast(BF16).rearrange("p (n i u e) -> p n i u e", n=NS, u=2, e=2),
                 in0=xp.pop(g)[:].rearrange("p u n j i -> p u (n j i)").bitcast(BF16)
                 .rearrange("p u (n i e) -> p n i u e", n=NS, e=2),
                 in1=styT[:, :, NS * g : NS * g + NS]
@@ -203,7 +203,7 @@ def tile_modulatemlp_pa_w8_kernel(
             xc = xmp.tile([P, GT], U32, name="xc", align_bytes=64)
             xs = xmp.tile([P, GT], U8, name="xs", align_bytes=64)
             nc.vector.quantize_mx(
-                out=xc[:].bitcast(X4), scales=xs[:], in_=xm.pop(g)[:].rearrange("p r t -> p (r t)")
+                out=xc[:].bitcast(X4), scales=xs[:], in_=xm[g][:, : 2 * GT].bitcast(BF16)
             )
             xq[g] = (xc, xs)
 
@@ -234,7 +234,7 @@ def tile_modulatemlp_pa_w8_kernel(
                 av = aa[g][:, ob, :].rearrange("p (j n i) -> p n j i", j=J, n=NS)
                 for n in range(NS):
                     s = NS * g + n
-                    if on_vector or (h == 1 and g % 16 == 7):
+                    if on_vector or (False):
                         nc.vector.tensor_scalar(
                             out=av[:, n], in0=yv[:, n], scalar1=dT[:, ob, s : s + 1], scalar2=bT[:, ob : ob + 1],
                             op0=ALU.mult, op1=ALU.add,
@@ -277,7 +277,7 @@ def tile_modulatemlp_pa_w8_kernel(
             return zz[g, j][:]
 
         def on_vector_alone(g, j):
-            return summed(g, j) and (True)
+            return summed(g, j) and (g % 3 == 1)
 
         def stage_c(g, j):
             if on_vector_alone(g, j):
@@ -304,18 +304,18 @@ def tile_modulatemlp_pa_w8_kernel(
         def stage_k(g, j):
             if g >= GROUPS - 3:
                 ov = oo[g][:, j, :]
+                nc.vector.tensor_scalar(out=ov, in0=ov, scalar1=CLAMP, scalar2=-CLAMP, op0=ALU.min, op1=ALU.max)
             elif j == 1:
-                ov = oo[g][:].rearrange("p j o -> p (j o)")
-            else:
-                return
-            eng = nc.vector if J * g + j >= J * GROUPS - 6 else nc.gpsimd
-            eng.tensor_scalar(out=ov, in0=ov, scalar1=CLAMP, scalar2=-CLAMP, op0=ALU.min, op1=ALU.max)
+                src = oo[g][:].rearrange("p j o -> p (j o)")
+                dst = xm[g + 3 + AHEAD][:] if g + 3 + AHEAD in xm else src
+                nc.gpsimd.tensor_scalar(out=dst, in0=src, scalar1=CLAMP, scalar2=-CLAMP, op0=ALU.min, op1=ALU.max)
+                clipped[g] = dst
 
         def stage_o(g, j):
             if g >= GROUPS - 3:
                 nc.sync.dma_start(out=og[g][:, j, :], in_=oo[g][:, j, :])
             elif j == 1:
-                nc.sync.dma_start(out=og[g], in_=oo.pop(g)[:])
+                nc.sync.dma_start(out=og[g].rearrange("p j c -> p (j c)"), in_=clipped.pop(g))
                 if g % 2 == 1 and loads:
                     load_x()
 
@@ -367,45 +367,38 @@ def tile_modulatemlp_pa_w8_kernel(
             return 0 <= g < GROUPS
 
         def prepared(i):
-            first, last = i + AHEAD + (i - 1) // 99, i + AHEAD + i // 99
-            return [g for g in range(first, last + 1) if has(g)]
+            return [g for g in [i + AHEAD] if has(g)]
 
         for i in range(1, GROUPS + 4):
             todo = prepared(i)
             if has(i):
                 stage_m(i)
-            if has(i - 1):
-                stage_z(i - 1, 0)
-            for g in todo[:1]:
+            if has(i - 2):
+                stage_z(i - 2, 0)
+            for g in todo:
                 if has(g + 1):
                     stage_x(g + 1)
             if has(i - 2):
                 stage_z(i - 2, 1)
             if has(i):
                 stage_e(i, 0)
-            for g in todo[:1]:
+            for g in todo:
                 stage_a(g)
-            if has(i - 2):
-                stage_l(i - 2, 0)
-            for g in todo[1:]:
-                if has(g + 1):
-                    stage_x(g + 1)
-                stage_a(g)
-            if has(i):
-                stage_e(i, 1, on_vector=i >= GROUPS - 2)
-            if has(i - 1):
-                stage_c(i - 1, 0)
-            if has(i - 2):
-                stage_c(i - 2, 1)
             if has(i - 3):
                 stage_l(i - 3, 1)
-            for g in todo:
-                stage_b(g)
+            if has(i):
+                stage_e(i, 1, on_vector=i >= GROUPS - 2)
+            if has(i - 2):
+                stage_c(i - 2, 0)
+                stage_c(i - 2, 1)
+            if has(i - 3):
+                stage_l(i - 3, 0)
             if has(i - 1):
                 stage_r(i - 1, 1)
-            if has(i - 2):
-                stage_k(i - 2, 0)
-                stage_o(i - 2, 0)
+            for g in todo:
+                stage_b(g)
             if has(i - 3):
                 stage_k(i - 3, 1)
                 stage_o(i - 3, 1)
+                stage_k(i - 3, 0)
+                stage_o(i - 3, 0)

@@ -25,10 +25,14 @@ EPS = 1e-8
 CLAMP = 256.0
 FLOPS = 2 * N * L * C * O + 2 * N * WD * C + 2 * N * C * O
 AHEAD = 2
+SHARE = 2
+EARLY_SHARE = 0
+TAIL = 3
+PRELOAD = 5
 
 
 def summed(g, j):
-    return g >= GROUPS - 0 or (j == 1 and (g < 29))
+    return j == 1 and g < GROUPS - TAIL
 
 
 def tile_modulatemlp_pa_w8_kernel(
@@ -42,11 +46,15 @@ def tile_modulatemlp_pa_w8_kernel(
     with ExitStack() as ctx:
         const = ctx.enter_context(tc.tile_pool(name="const", bufs=1))
         xmp = ctx.enter_context(tc.tile_pool(name="xmp", bufs=AHEAD + 2))
-        ap = ctx.enter_context(tc.tile_pool(name="ap", bufs=4))
+        ap = ctx.enter_context(tc.tile_pool(name="ap", bufs=3))
         op = ctx.enter_context(tc.tile_pool(name="op", bufs=5))
         psum = ctx.enter_context(tc.psum_pool(name="psum", bufs=1))
         ctx.enter_context(tc.manual_schedule())
 
+        ssc = const.tile([P, C], U8, name="ssc", align_bytes=64)
+        nc.vector.memset(ssc[:].bitcast(U32), 0)
+        one = const.tile([P, 1], F32, name="one")
+        nc.vector.memset(one[:], 1.0)
         wb = const.tile([P, WD], U8, name="wb", align_bytes=64)
         nc.sync.dma_start(out=wb[:], in_=w_bytes)
         wsc = const.tile([P, 4], F32, name="wsc")
@@ -56,14 +64,11 @@ def tile_modulatemlp_pa_w8_kernel(
         nc.sync.dma_start(out=wsb[0][:], in_=wview[:, 0:2, :])
         sw = const.tile([P, 4 * C], U8, name="sw", align_bytes=64)
         nc.sync.dma_start(out=sw[:], in_=style_w_words[0].rearrange("p n t -> p (n t)"))
-        ssc = const.tile([P, C], U8, name="ssc", align_bytes=64)
-        nc.vector.memset(ssc[:].bitcast(U32), 0)
         for q in range(4):
             nc.sync.dma_start(
                 out=ssc[32 * q : 32 * q + 4, :].bitcast(I32),
                 in_=style_w_scales[0][4 * q : 4 * q + 4, :].bitcast(I32),
             )
-        nc.sync.dma_start(out=wsb[1][:], in_=wview[:, 2:4, :])
         xtiles = {}
         bb = const.tile([P, 4, 2], BF16, name="bb")
         loads = [(0, 1), (1, 1)] + [(g, 2) for g in range(2, GROUPS, 2)]
@@ -75,17 +80,16 @@ def tile_modulatemlp_pa_w8_kernel(
             for k in range(n_g):
                 xtiles[g0 + k] = (xt, k)
 
-        load_x()
         sb = const.tile([P, 4], BF16, name="sb")
+        load_x()
         nc.sync.dma_start(out=sb[:], in_=style_b.rearrange("(p t) -> p t", t=4))
+        nc.sync.dma_start(out=wsb[1][:], in_=wview[:, 2:4, :])
         load_x()
         with nc.allow_non_contiguous_dma(reason="one bias value a partition and block"):
             nc.sync.dma_start(out=bb[:, :, 0], in_=bias.rearrange("(b m) -> m b", b=4))
-        for k in range(5):
+        for k in range(PRELOAD):
             load_x()
 
-        one = const.tile([P, 1], F32, name="one")
-        nc.vector.memset(one[:], 1.0)
         warm = const.tile([P, 1], F32, name="warm")
         nc.scalar.activation(warm[:], one[:], ACT.Abs_reciprocal_sqrt)
         ident = const.tile([P, P], F32, name="ident")
@@ -94,11 +98,6 @@ def tile_modulatemlp_pa_w8_kernel(
         def transpose_words(dst, words):
             for u in range(2):
                 nc.tensor.transpose(dst[:, u], words[:, u : C // 2 : 2], ident[:])
-
-        w16 = const.tile([P, WD], BF16, name="w16", align_bytes=64)
-        nc.vector.tensor_copy(out=w16[:], in_=wb[:].bitcast(F8))
-        wtp = psum.tile([P, 2, P], F32, name="wtp", tag="xp", bufs=2)
-        transpose_words(wtp, w16[:].bitcast(F32))
 
         wt = const.tile([P, O, 4], BF16, name="wt", align_bytes=64)
         wt32 = wt[:].rearrange("p o t -> p (o t)").bitcast(F32)
@@ -110,6 +109,9 @@ def tile_modulatemlp_pa_w8_kernel(
         sq = const.tile([P, N, 4], BF16, name="sq", align_bytes=64)
         sqc = const.tile([P, N], U32, name="sqc", align_bytes=64)
         sqs = const.tile([P, N], U8, name="sqs", align_bytes=64)
+        styT = const.tile([P, 4, N], F32, name="styT", align_bytes=64)
+        dT = const.tile([P, 4, N], F32, name="dT")
+        bT = const.tile([P, 4], F32, name="bT")
         halves = [slice(0, O // 2), slice(O // 2, O)]
 
         def turn_weight(h):
@@ -121,6 +123,12 @@ def tile_modulatemlp_pa_w8_kernel(
                 in_=ww[:].rearrange("p b u r -> p b r u"),
             )
 
+        def square_half(h, on_vector):
+            if on_vector:
+                nc.vector.tensor_tensor(out=w2[:, halves[h], :], in0=wt[:, halves[h], :], in1=wt[:, halves[h], :], op=ALU.mult)
+            else:
+                nc.scalar.activation(w2[:, halves[h], :], wt[:, halves[h], :], ACT.Square)
+
         def quantise_half(codes, scales, src, h):
             nc.vector.quantize_mx(
                 out=codes[:, halves[h]].bitcast(X4),
@@ -128,57 +136,24 @@ def tile_modulatemlp_pa_w8_kernel(
                 in_=src[:, halves[h], :].rearrange("p o t -> p (o t)"),
             )
 
-        turn_weight(0)
-        nc.scalar.activation(w2[:, halves[0], :], wt[:, halves[0], :], ACT.Square)
-        wm = const.tile([P, N, 4], BF16, name="wm", align_bytes=64)
-        nc.vector.tensor_tensor(
-            out=wm[:].rearrange("p n (u e) -> p n u e", u=2),
-            in0=wtp[:].bitcast(BF16).rearrange("p u (n e) -> p n u e", e=2),
-            in1=wsc[:].rearrange("p (u e) -> p u e", u=2).unsqueeze(1).to_broadcast([P, N, 2, 2]),
-            op=ALU.mult,
-        )
-        swp = const.tile([P, C], I32, name="swp", align_bytes=64)
-        nc.vector.tensor_copy(
-            out=swp[:].rearrange("p (t m) -> p t m", t=4),
-            in_=sw[:].bitcast(I32).rearrange("p (m t) -> p t m", t=4),
-        )
-        wq = const.tile([P, N], U32, name="wq", align_bytes=64)
-        wqs = const.tile([P, N], U8, name="wqs", align_bytes=64)
-        nc.vector.quantize_mx(out=wq[:].bitcast(X4), scales=wqs[:], in_=wm[:].rearrange("p n t -> p (n t)"))
-        sscp = const.tile([P, C], U8, name="sscp", align_bytes=64)
-        nc.vector.tensor_copy(
-            out=sscp[:].rearrange("p (t m) -> p t m", t=4),
-            in_=ssc[:].rearrange("p (m t) -> p t m", t=4),
-        )
-        quantise_half(wc, wcs, wt, 0)
-
-        styT = const.tile([P, 4, N], F32, name="styT", align_bytes=64)
-        sp = [
-            psum.tile([P, 2, P], F32, name="sp0", tag="ya", bufs=1),
-            psum.tile([P, 2, P], F32, name="sp1", tag="yb", bufs=1),
-        ]
-        for t in range(4):
-            nc.tensor.matmul_mx(
-                out=sp[t // 2][:, t % 2, :],
-                lhsT=swp[:, P * t : P * t + P].bitcast(X4),
-                lhsT_scale=sscp[:, P * t : P * t + P],
-                rhs=wq[:].bitcast(X4),
-                rhs_scale=wqs[:],
-                start=True,
-                stop=True,
-            )
-        wscale = 1.0 / math.sqrt(WD)
-        for t in range(2):
+        def demod_half(h):
+            dp = psum.tile([P, 2, N], F32, name="dp", tag="zp", bufs=4)
+            for k in range(2):
+                ob = 2 * h + k
+                nc.tensor.matmul_mx(
+                    out=dp[:, k, :],
+                    lhsT=w2c[:, P * ob : P * ob + P].bitcast(X4),
+                    lhsT_scale=w2s[:, P * ob : P * ob + P],
+                    rhs=sqc[:].bitcast(X4),
+                    rhs_scale=sqs[:],
+                    start=True,
+                    stop=True,
+                )
             nc.scalar.activation(
-                styT[:, t, :], sp[0][:, t, :], ACT.Identity, scale=wscale, bias=sb[:, t : t + 1]
-            )
-        for t in range(2, 4):
-            nc.vector.tensor_scalar(
-                out=styT[:, t, :], in0=sp[1][:, t - 2, :], scalar1=wscale, scalar2=sb[:, t : t + 1],
-                op0=ALU.mult, op1=ALU.add,
+                dT[:, 2 * h : 2 * h + 2, :], dp[:], ACT.Abs_reciprocal_sqrt, scale=1.0 / gain**2, bias=EPS / gain**2
             )
 
-        xp, xm, xq, yy, aa, cc, zz, rr, oo, clipped = {}, {}, {}, {}, {}, {}, {}, {}, {}, {}
+        xp, xm, xq, yy, aa, uu, cc, zz, oo = {}, {}, {}, {}, {}, {}, {}, {}, {}
 
         def stage_x(g):
             xt, k = xtiles[g]
@@ -224,139 +199,160 @@ def tile_modulatemlp_pa_w8_kernel(
                     )
                 yy[g, h] = y
 
-        def stage_e(g, h, on_vector=False):
-            if h == 0:
-                aa[g] = ap.tile([P, 4, GT], F32, name="a")
-            y = yy.pop((g, h))
-            for k in range(2):
+        def stage_e(g, h, first=0, last=2 * NS, on_vector=False):
+            if g not in aa:
+                aa[g] = ap.tile([P, J, 4, P], F32, name="a", bufs=3)
+            y = yy[g, h]
+            for m in range(first, last):
+                k, n = divmod(m, NS)
                 ob = 2 * h + k
-                yv = y[:, k, :].rearrange("p (n j i) -> p n j i", j=J, n=NS)
-                av = aa[g][:, ob, :].rearrange("p (j n i) -> p n j i", j=J, n=NS)
-                for n in range(NS):
-                    s = NS * g + n
-                    if on_vector or (False):
-                        nc.vector.tensor_scalar(
-                            out=av[:, n], in0=yv[:, n], scalar1=dT[:, ob, s : s + 1], scalar2=bT[:, ob : ob + 1],
-                            op0=ALU.mult, op1=ALU.add,
-                        )
-                    else:
-                        nc.scalar.activation(
-                            av[:, n], yv[:, n], ACT.Identity, scale=dT[:, ob, s : s + 1], bias=bT[:, ob : ob + 1]
-                        )
+                s = NS * g + n
+                yv = y[:, k, :].rearrange("p (n j i) -> p n j i", j=J, n=NS)[:, n]
+                av = aa[g][:, :, ob, :].rearrange("p j (n i) -> p n j i", n=NS)[:, n]
+                if on_vector:
+                    nc.vector.tensor_scalar(
+                        out=av, in0=yv, scalar1=dT[:, ob, s : s + 1], scalar2=bT[:, ob : ob + 1],
+                        op0=ALU.mult, op1=ALU.add,
+                    )
+                else:
+                    nc.scalar.activation(av, yv, ACT.Identity, scale=dT[:, ob, s : s + 1], bias=bT[:, ob : ob + 1])
 
-        def stage_r(g, j):
+        def stage_k(g, engine, js=(0, J)):
+            src = aa[g][:].rearrange("p j b m -> p (j b m)")
+            if g not in uu:
+                uu[g] = xm[g + AHEAD][:] if g + AHEAD in xm else src
+            cols = slice(O * js[0], O * js[1])
+            engine.tensor_scalar(
+                out=uu[g][:, cols], in0=src[:, cols], scalar1=CLAMP / 5.0, scalar2=-CLAMP, op0=ALU.min, op1=ALU.max
+            )
+
+        def stage_r(g, j=1):
             if summed(g, j):
-                cc[g, j] = ap.tile([P, 4, P], F32, name="c", bufs=3)
+                cc[g, j] = ap.tile([P, O], F32, name="c", bufs=3)
                 nc.vector.tensor_scalar(
-                    out=cc[g, j][:], in0=aa[g][:, :, P * j : P * j + P], scalar1=0.0, scalar2=4.0,
+                    out=cc[g, j][:], in0=uu[g][:, O * j : O * j + O], scalar1=0.0, scalar2=4.0,
                     op0=ALU.max, op1=ALU.mult,
                 )
 
-        def stage_z(g, j):
-            z = psum.tile([P, O], F32, name="z", tag="zp", bufs=4)
+        def stage_z(g, j, tag="zp"):
+            z = psum.tile([P, O], F32, name="z", tag=tag, bufs=4 if tag == "zp" else 2)
             for ob in range(4):
                 dst = z[:, P * ob : P * ob + P]
-                src = aa[g][:, ob, P * j : P * j + P]
+                src = uu[g][:, O * j + P * ob : O * j + P * ob + P]
                 if summed(g, j):
                     nc.tensor.matmul(dst, lhsT=src, rhs=ident[:], start=True, stop=False, is_transpose=True)
                     nc.tensor.matmul(
-                        dst, lhsT=cc[g, j][:, ob, :], rhs=ident[:], start=False, stop=True, is_transpose=True
+                        dst, lhsT=cc[g, j][:, P * ob : P * ob + P], rhs=ident[:], start=False, stop=True, is_transpose=True
                     )
-                elif False:
-                    nc.tensor.matmul(dst, lhsT=src, rhs=ident[:], start=True, stop=True)
                 else:
                     nc.tensor.transpose(dst, src, ident[:])
             zz[g, j] = z
 
-        def out_view(g, j):
+        def stage_c(g, j, on_vector=False):
             if g not in oo:
                 oo[g] = op.tile([P, J, O], F32, name="o")
-            return oo[g][:, j, :]
-
-        def z_view(g, j):
-            return zz[g, j][:]
-
-        def on_vector_alone(g, j):
-            return summed(g, j) and (g % 3 == 1)
-
-        def stage_c(g, j):
-            if on_vector_alone(g, j):
-                return
-            if summed(g, j):
-                nc.scalar.copy(out=out_view(g, j), in_=z_view(g, j))
+            if on_vector:
+                nc.vector.tensor_copy(out=oo[g][:, j, :], in_=zz[g, j][:])
             else:
-                rr[g, j] = ap.tile([P, O], F32, name="r", bufs=4)
-                nc.scalar.copy(out=rr[g, j][:], in_=z_view(g, j))
+                nc.scalar.copy(out=oo[g][:, j, :], in_=zz[g, j][:])
 
         def stage_l(g, j):
-            if on_vector_alone(g, j):
-                nc.vector.tensor_copy(out=out_view(g, j), in_=z_view(g, j))
-            elif not summed(g, j):
+            if not summed(g, j):
                 nc.vector.scalar_tensor_tensor(
-                    out=out_view(g, j),
-                    in0=z_view(g, j),
-                    scalar=5.0,
-                    in1=rr.pop((g, j))[:],
-                    op0=ALU.mult,
-                    op1=ALU.max,
+                    out=oo[g][:, j, :], in0=zz[g, j][:], scalar=5.0, in1=oo[g][:, j, :], op0=ALU.mult, op1=ALU.max
                 )
 
-        def stage_k(g, j):
-            if g >= GROUPS - 3:
-                ov = oo[g][:, j, :]
-                nc.vector.tensor_scalar(out=ov, in0=ov, scalar1=CLAMP, scalar2=-CLAMP, op0=ALU.min, op1=ALU.max)
-            elif j == 1:
-                src = oo[g][:].rearrange("p j o -> p (j o)")
-                dst = xm[g + 3 + AHEAD][:] if g + 3 + AHEAD in xm else src
-                nc.gpsimd.tensor_scalar(out=dst, in0=src, scalar1=CLAMP, scalar2=-CLAMP, op0=ALU.min, op1=ALU.max)
-                clipped[g] = dst
-
-        def stage_o(g, j):
-            if g >= GROUPS - 3:
-                nc.sync.dma_start(out=og[g][:, j, :], in_=oo[g][:, j, :])
-            elif j == 1:
-                nc.sync.dma_start(out=og[g].rearrange("p j c -> p (j c)"), in_=clipped.pop(g))
+        def stage_o(g, j=None):
+            if j is None:
+                nc.sync.dma_start(out=og[g], in_=oo[g][:])
                 if g % 2 == 1 and loads:
                     load_x()
+            else:
+                nc.sync.dma_start(out=og[g][:, j, :], in_=oo[g][:, j, :])
 
-        dT = const.tile([P, 4, N], F32, name="dT")
-        bT = const.tile([P, 4], F32, name="bT")
+        w16 = const.tile([P, WD], BF16, name="w16", align_bytes=64)
+        nc.vector.tensor_copy(out=w16[:], in_=wb[:].bitcast(F8))
+        wtp = psum.tile([P, 2, P], F32, name="wtp", tag="xp", bufs=2)
+        transpose_words(wtp, w16[:].bitcast(F32))
+        turn_weight(0)
+        sscp = const.tile([P, C], U8, name="sscp", align_bytes=64)
+        nc.vector.tensor_copy(
+            out=sscp[:].rearrange("p (t m) -> p t m", t=4),
+            in_=ssc[:].rearrange("p (m t) -> p t m", t=4),
+        )
+        wm = const.tile([P, N, 4], BF16, name="wm", align_bytes=64)
+        nc.vector.tensor_tensor(
+            out=wm[:].rearrange("p n (u e) -> p n u e", u=2),
+            in0=wtp[:].bitcast(BF16).rearrange("p u (n e) -> p n u e", e=2),
+            in1=wsc[:].rearrange("p (u e) -> p u e", u=2).unsqueeze(1).to_broadcast([P, N, 2, 2]),
+            op=ALU.mult,
+        )
+        swp = const.tile([P, C], I32, name="swp", align_bytes=64)
+        nc.vector.tensor_copy(
+            out=swp[:].rearrange("p (t m) -> p t m", t=4),
+            in_=sw[:].bitcast(I32).rearrange("p (m t) -> p t m", t=4),
+        )
+        wq = const.tile([P, N], U32, name="wq", align_bytes=64)
+        wqs = const.tile([P, N], U8, name="wqs", align_bytes=64)
+        nc.vector.quantize_mx(out=wq[:].bitcast(X4), scales=wqs[:], in_=wm[:].rearrange("p n t -> p (n t)"))
 
-        def demod_half(h):
-            dp = psum.tile([P, 2, N], F32, name="dp", tag="zp", bufs=4)
-            for k in range(2):
-                ob = 2 * h + k
-                nc.tensor.matmul_mx(
-                    out=dp[:, k, :],
-                    lhsT=w2c[:, P * ob : P * ob + P].bitcast(X4),
-                    lhsT_scale=w2s[:, P * ob : P * ob + P],
-                    rhs=sqc[:].bitcast(X4),
-                    rhs_scale=sqs[:],
-                    start=True,
-                    stop=True,
-                )
-            nc.scalar.activation(
-                dT[:, 2 * h : 2 * h + 2, :], dp[:], ACT.Abs_reciprocal_sqrt, scale=1.0 / gain**2, bias=EPS / gain**2
+        sp = [
+            psum.tile([P, 2, P], F32, name="sp0", tag="ya", bufs=1),
+            psum.tile([P, 2, P], F32, name="sp1", tag="yb", bufs=1),
+        ]
+        for t in range(4):
+            nc.tensor.matmul_mx(
+                out=sp[t // 2][:, t % 2, :],
+                lhsT=swp[:, P * t : P * t + P].bitcast(X4),
+                lhsT_scale=sscp[:, P * t : P * t + P],
+                rhs=wq[:].bitcast(X4),
+                rhs_scale=wqs[:],
+                start=True,
+                stop=True,
             )
+        wscale = 1.0 / math.sqrt(WD)
 
+        def style_out():
+            for t in range(2):
+                nc.scalar.activation(
+                    styT[:, t, :], sp[0][:, t, :], ACT.Identity, scale=wscale, bias=sb[:, t : t + 1]
+                )
+            for t in range(2, 4):
+                nc.vector.tensor_scalar(
+                    out=styT[:, t, :], in0=sp[1][:, t - 2, :], scalar1=wscale, scalar2=sb[:, t : t + 1],
+                    op0=ALU.mult, op1=ALU.add,
+                )
+
+        def square_style():
+            nc.scalar.activation(sq[:], styT[:].rearrange("p t n -> p n t"), ACT.Square)
+
+        def quantise_sq():
+            nc.vector.quantize_mx(out=sqc[:].bitcast(X4), scales=sqs[:], in_=sq[:].rearrange("p n t -> p (n t)"))
+
+        def scale_bias():
+            nc.scalar.activation(bT[:], bb[:, :, 0], ACT.Copy, scale=gain)
+
+        square_half(0, True)
+        quantise_half(wc, wcs, wt, 0)
+        style_out()
         stage_x(0)
-        nc.scalar.activation(sq[:], styT[:].rearrange("p t n -> p n t"), ACT.Square)
+        square_style()
         turn_weight(1)
         stage_x(1)
-        nc.scalar.activation(w2[:, halves[1], :], wt[:, halves[1], :], ACT.Square)
-        nc.scalar.activation(bT[:], bb[:, :, 0], ACT.Copy, scale=gain)
+        square_half(1, False)
+        scale_bias()
         quantise_half(w2c, w2s, w2, 0)
         stage_a(0)
-        nc.vector.quantize_mx(out=sqc[:].bitcast(X4), scales=sqs[:], in_=sq[:].rearrange("p n t -> p (n t)"))
+        quantise_sq()
+        demod_half(0)
         quantise_half(wc, wcs, wt, 1)
         stage_b(0)
-        demod_half(0)
         stage_m(0)
-        quantise_half(w2c, w2s, w2, 1)
+        stage_x(2)
         stage_a(1)
+        quantise_half(w2c, w2s, w2, 1)
         stage_e(0, 0)
         demod_half(1)
-        stage_x(2)
         stage_x(3)
         stage_b(1)
         stage_a(2)
@@ -366,39 +362,56 @@ def tile_modulatemlp_pa_w8_kernel(
         def has(g):
             return 0 <= g < GROUPS
 
-        def prepared(i):
-            return [g for g in [i + AHEAD] if has(g)]
-
-        for i in range(1, GROUPS + 4):
-            todo = prepared(i)
-            if has(i):
-                stage_m(i)
+        LAST = GROUPS - AHEAD
+        for i in range(1, LAST):
+            share = SHARE if has(i - 3) else EARLY_SHARE
+            stage_k(i - 1, nc.gpsimd)
+            stage_m(i)
             if has(i - 2):
                 stage_z(i - 2, 0)
-            for g in todo:
-                if has(g + 1):
-                    stage_x(g + 1)
+            if has(i + AHEAD + 1):
+                stage_x(i + AHEAD + 1)
             if has(i - 2):
                 stage_z(i - 2, 1)
-            if has(i):
-                stage_e(i, 0)
-            for g in todo:
-                stage_a(g)
-            if has(i - 3):
-                stage_l(i - 3, 1)
-            if has(i):
-                stage_e(i, 1, on_vector=i >= GROUPS - 2)
+            stage_e(i, 0, 0, 2 * NS - share)
+            stage_a(i + AHEAD)
+            stage_e(i, 0, 2 * NS - share, 2 * NS, on_vector=True)
+            stage_e(i, 1)
             if has(i - 2):
                 stage_c(i - 2, 0)
-                stage_c(i - 2, 1)
+                if i + 1 < LAST:
+                    stage_c(i - 2, 1)
             if has(i - 3):
                 stage_l(i - 3, 0)
-            if has(i - 1):
-                stage_r(i - 1, 1)
-            for g in todo:
-                stage_b(g)
-            if has(i - 3):
-                stage_k(i - 3, 1)
-                stage_o(i - 3, 1)
-                stage_k(i - 3, 0)
-                stage_o(i - 3, 0)
+                stage_o(i - 3)
+            stage_b(i + AHEAD)
+            stage_r(i - 1)
+        stage_m(LAST)
+
+        a, b = GROUPS - 2, GROUPS - 1
+        stage_k(a - 1, nc.gpsimd)
+        stage_z(a - 2, 0)
+        stage_e(a, 0)
+        stage_e(a, 1, on_vector=True)
+        stage_m(b)
+        stage_z(a - 2, 1)
+        stage_k(a, nc.gpsimd)
+        stage_l(a - 3, 0)
+        stage_o(a - 3, 0)
+        stage_c(a - 2, 0)
+        stage_e(b, 0)
+        stage_c(a - 3, 1, on_vector=True)
+        stage_o(a - 3, 1)
+        stage_e(b, 1, on_vector=True)
+        stage_l(a - 2, 0)
+        stage_o(a - 2, 0)
+        stage_k(b, nc.gpsimd)
+        for g in range(GROUPS - TAIL, GROUPS):
+            for j in range(J):
+                stage_z(g, j, "zp" if g == a else "xp")
+                stage_c(g, j)
+                if (g, j) == (a - 1, 0):
+                    stage_c(a - 2, 1)
+                    stage_o(a - 2, 1)
+                stage_l(g, j)
+                stage_o(g, j)

@@ -25,10 +25,13 @@ EPS = 1e-8
 CLAMP = 256.0
 FLOPS = 2 * N * L * C * O + 2 * N * WD * C + 2 * N * C * O
 AHEAD = 2
-SHARE = 2
-EARLY_SHARE = 0
+EMPTIES_EVERY = 3
 TAIL = 3
 PRELOAD = 5
+
+
+def vector_empties(g):
+    return g % EMPTIES_EVERY == 1
 
 
 def summed(g, j):
@@ -364,7 +367,6 @@ def tile_modulatemlp_pa_w8_kernel(
 
         LAST = GROUPS - AHEAD
         for i in range(1, LAST):
-            share = SHARE if has(i - 3) else EARLY_SHARE
             stage_k(i - 1, nc.gpsimd)
             stage_m(i)
             if has(i - 2):
@@ -373,13 +375,14 @@ def tile_modulatemlp_pa_w8_kernel(
                 stage_x(i + AHEAD + 1)
             if has(i - 2):
                 stage_z(i - 2, 1)
-            stage_e(i, 0, 0, 2 * NS - share)
+            stage_e(i, 0)
             stage_a(i + AHEAD)
-            stage_e(i, 0, 2 * NS - share, 2 * NS, on_vector=True)
+            if has(i - 3) and vector_empties(i - 3):
+                stage_c(i - 3, 1, on_vector=True)
             stage_e(i, 1)
             if has(i - 2):
                 stage_c(i - 2, 0)
-                if i + 1 < LAST:
+                if i + 1 < LAST and not vector_empties(i - 2):
                     stage_c(i - 2, 1)
             if has(i - 3):
                 stage_l(i - 3, 0)
@@ -392,26 +395,26 @@ def tile_modulatemlp_pa_w8_kernel(
         stage_k(a - 1, nc.gpsimd)
         stage_z(a - 2, 0)
         stage_e(a, 0)
-        stage_e(a, 1, on_vector=True)
+        stage_e(a, 1)
         stage_m(b)
         stage_z(a - 2, 1)
         stage_k(a, nc.gpsimd)
         stage_l(a - 3, 0)
         stage_o(a - 3, 0)
-        stage_c(a - 2, 0)
-        stage_e(b, 0)
         stage_c(a - 3, 1, on_vector=True)
         stage_o(a - 3, 1)
-        stage_e(b, 1, on_vector=True)
+        stage_c(a - 2, 0)
+        stage_c(a - 2, 1, on_vector=True)
+        stage_o(a - 2, 1)
+        stage_e(b, 0)
+        stage_e(b, 1)
         stage_l(a - 2, 0)
         stage_o(a - 2, 0)
-        stage_k(b, nc.gpsimd)
         for g in range(GROUPS - TAIL, GROUPS):
+            if g == a - 1:
+                stage_k(b, nc.gpsimd)
             for j in range(J):
                 stage_z(g, j, "zp" if g == a else "xp")
-                stage_c(g, j)
-                if (g, j) == (a - 1, 0):
-                    stage_c(a - 2, 1)
-                    stage_o(a - 2, 1)
+                stage_c(g, j, on_vector=(g, j) in [])
                 stage_l(g, j)
                 stage_o(g, j)

@@ -34,6 +34,10 @@ def vector_empties(g):
     return g % EMPTIES_EVERY == 1
 
 
+def free_clip(g):
+    return vector_empties(g) and summed(g, 1)
+
+
 def summed(g, j):
     return j == 1 and g < GROUPS - TAIL
 
@@ -112,7 +116,7 @@ def tile_modulatemlp_pa_w8_kernel(
         sq = const.tile([P, N, 4], BF16, name="sq", align_bytes=64)
         sqc = const.tile([P, N], U32, name="sqc", align_bytes=64)
         sqs = const.tile([P, N], U8, name="sqs", align_bytes=64)
-        styT = const.tile([P, 4, N], F32, name="styT", align_bytes=64)
+        styT = const.tile([P, N, 4], F32, name="styT", align_bytes=64)
         dT = const.tile([P, 4, N], F32, name="dT")
         bT = const.tile([P, 4], F32, name="bT")
         halves = [slice(0, O // 2), slice(O // 2, O)]
@@ -170,8 +174,8 @@ def tile_modulatemlp_pa_w8_kernel(
                 out=xm[g][:, : 2 * GT].bitcast(BF16).rearrange("p (n i u e) -> p n i u e", n=NS, u=2, e=2),
                 in0=xp.pop(g)[:].rearrange("p u n j i -> p u (n j i)").bitcast(BF16)
                 .rearrange("p u (n i e) -> p n i u e", n=NS, e=2),
-                in1=styT[:, :, NS * g : NS * g + NS]
-                .rearrange("p (u e) n -> p n u e", u=2)
+                in1=styT[:, NS * g : NS * g + NS, :]
+                .rearrange("p n (u e) -> p n u e", u=2)
                 .unsqueeze(2)
                 .to_broadcast([P, NS, L, 2, 2]),
                 op=ALU.mult,
@@ -204,7 +208,7 @@ def tile_modulatemlp_pa_w8_kernel(
 
         def stage_e(g, h, first=0, last=2 * NS, on_vector=False):
             if g not in aa:
-                aa[g] = ap.tile([P, J, 4, P], F32, name="a", bufs=3)
+                aa[g] = ap.tile([P, J, 4, P], F32, name="a", bufs=4)
             y = yy[g, h]
             for m in range(first, last):
                 k, n = divmod(m, NS)
@@ -224,16 +228,23 @@ def tile_modulatemlp_pa_w8_kernel(
             src = aa[g][:].rearrange("p j b m -> p (j b m)")
             if g not in uu:
                 uu[g] = xm[g + AHEAD][:] if g + AHEAD in xm else src
+            if free_clip(g):
+                js = (0, 1)
             cols = slice(O * js[0], O * js[1])
             engine.tensor_scalar(
                 out=uu[g][:, cols], in0=src[:, cols], scalar1=CLAMP / 5.0, scalar2=-CLAMP, op0=ALU.min, op1=ALU.max
             )
 
+        def turned(g, j):
+            if j == 1 and free_clip(g):
+                return aa[g][:, j].rearrange("p b m -> p (b m)")
+            return uu[g][:, O * j : O * j + O]
+
         def stage_r(g, j=1):
             if summed(g, j):
                 cc[g, j] = ap.tile([P, O], F32, name="c", bufs=3)
                 nc.vector.tensor_scalar(
-                    out=cc[g, j][:], in0=uu[g][:, O * j : O * j + O], scalar1=0.0, scalar2=4.0,
+                    out=cc[g, j][:], in0=turned(g, j), scalar1=0.0, scalar2=4.0,
                     op0=ALU.max, op1=ALU.mult,
                 )
 
@@ -241,7 +252,7 @@ def tile_modulatemlp_pa_w8_kernel(
             z = psum.tile([P, O], F32, name="z", tag=tag, bufs=4 if tag == "zp" else 2)
             for ob in range(4):
                 dst = z[:, P * ob : P * ob + P]
-                src = uu[g][:, O * j + P * ob : O * j + P * ob + P]
+                src = turned(g, j)[:, P * ob : P * ob + P]
                 if summed(g, j):
                     nc.tensor.matmul(dst, lhsT=src, rhs=ident[:], start=True, stop=False, is_transpose=True)
                     nc.tensor.matmul(
@@ -254,7 +265,11 @@ def tile_modulatemlp_pa_w8_kernel(
         def stage_c(g, j, on_vector=False):
             if g not in oo:
                 oo[g] = op.tile([P, J, O], F32, name="o")
-            if on_vector:
+            if j == 1 and free_clip(g):
+                nc.vector.tensor_scalar(
+                    out=oo[g][:, j, :], in0=zz[g, j][:], scalar1=CLAMP, scalar2=-CLAMP, op0=ALU.min, op1=ALU.max
+                )
+            elif on_vector:
                 nc.vector.tensor_copy(out=oo[g][:, j, :], in_=zz[g, j][:])
             else:
                 nc.scalar.copy(out=oo[g][:, j, :], in_=zz[g, j][:])
@@ -299,13 +314,10 @@ def tile_modulatemlp_pa_w8_kernel(
         wqs = const.tile([P, N], U8, name="wqs", align_bytes=64)
         nc.vector.quantize_mx(out=wq[:].bitcast(X4), scales=wqs[:], in_=wm[:].rearrange("p n t -> p (n t)"))
 
-        sp = [
-            psum.tile([P, 2, P], F32, name="sp0", tag="ya", bufs=1),
-            psum.tile([P, 2, P], F32, name="sp1", tag="yb", bufs=1),
-        ]
+        sp = psum.tile([P, 4, N], F32, name="sp", tag="ya", bufs=1)
         for t in range(4):
             nc.tensor.matmul_mx(
-                out=sp[t // 2][:, t % 2, :],
+                out=sp[:, t, :],
                 lhsT=swp[:, P * t : P * t + P].bitcast(X4),
                 lhsT_scale=sscp[:, P * t : P * t + P],
                 rhs=wq[:].bitcast(X4),
@@ -316,18 +328,13 @@ def tile_modulatemlp_pa_w8_kernel(
         wscale = 1.0 / math.sqrt(WD)
 
         def style_out():
-            for t in range(2):
-                nc.scalar.activation(
-                    styT[:, t, :], sp[0][:, t, :], ACT.Identity, scale=wscale, bias=sb[:, t : t + 1]
-                )
-            for t in range(2, 4):
-                nc.vector.tensor_scalar(
-                    out=styT[:, t, :], in0=sp[1][:, t - 2, :], scalar1=wscale, scalar2=sb[:, t : t + 1],
-                    op0=ALU.mult, op1=ALU.add,
-                )
+            nc.vector.scalar_tensor_tensor(
+                out=styT[:], in0=sp[:].rearrange("p t n -> p n t"), scalar=wscale,
+                in1=sb[:].unsqueeze(1).to_broadcast([P, N, 4]), op0=ALU.mult, op1=ALU.add,
+            )
 
         def square_style():
-            nc.scalar.activation(sq[:], styT[:].rearrange("p t n -> p n t"), ACT.Square)
+            nc.scalar.activation(sq[:], styT[:], ACT.Square)
 
         def quantise_sq():
             nc.vector.quantize_mx(out=sqc[:].bitcast(X4), scales=sqs[:], in_=sq[:].rearrange("p n t -> p (n t)"))
@@ -389,32 +396,45 @@ def tile_modulatemlp_pa_w8_kernel(
                 stage_o(i - 3)
             stage_b(i + AHEAD)
             stage_r(i - 1)
-        stage_m(LAST)
 
         a, b = GROUPS - 2, GROUPS - 1
         stage_k(a - 1, nc.gpsimd)
+        stage_m(a)
         stage_z(a - 2, 0)
+        stage_z(a - 2, 1)
         stage_e(a, 0)
         stage_e(a, 1)
-        stage_m(b)
-        stage_z(a - 2, 1)
-        stage_k(a, nc.gpsimd)
         stage_l(a - 3, 0)
         stage_o(a - 3, 0)
         stage_c(a - 3, 1, on_vector=True)
         stage_o(a - 3, 1)
+        stage_m(b)
+        stage_k(a, nc.gpsimd)
+        stage_z(a - 1, 1, "xp")
+        stage_z(a - 1, 0, "xp")
         stage_c(a - 2, 0)
         stage_c(a - 2, 1, on_vector=True)
         stage_o(a - 2, 1)
         stage_e(b, 0)
-        stage_e(b, 1)
+        stage_e(b, 1, on_vector=True)
+        stage_k(b, nc.gpsimd, (0, 1))
+        stage_k(b, nc.gpsimd, (1, 2))
         stage_l(a - 2, 0)
         stage_o(a - 2, 0)
-        for g in range(GROUPS - TAIL, GROUPS):
-            if g == a - 1:
-                stage_k(b, nc.gpsimd)
-            for j in range(J):
-                stage_z(g, j, "zp" if g == a else "xp")
-                stage_c(g, j, on_vector=(g, j) in [])
-                stage_l(g, j)
-                stage_o(g, j)
+        stage_c(a - 1, 1)
+        stage_z(a, 0)
+        stage_z(a, 1)
+        stage_l(a - 1, 1)
+        stage_o(a - 1, 1)
+        stage_c(a - 1, 0)
+        stage_l(a - 1, 0)
+        stage_o(a - 1, 0)
+        stage_c(a, 0)
+        stage_z(b, 0)
+        stage_z(b, 1)
+        last = [(a, 0), (a, 1), (b, 0), (b, 1)]
+        for now, then in zip(last, last[1:] + [None]):
+            if then:
+                stage_c(*then)
+            stage_l(*now)
+            stage_o(*now)

@@ -20,7 +20,6 @@ J = 2
 GT = P * J
 GROUPS = N * L // GT
 NS = GT // L
-PS = P // NS
 EPS = 1e-8
 CLAMP = 256.0
 FLOPS = 2 * N * L * C * O + 2 * N * WD * C + 2 * N * C * O
@@ -47,8 +46,8 @@ def tile_modulatemlp_pa_w8_kernel(
 ):
     nc = tc.nc
     gain = 0.2 * math.sqrt(2.0)
-    xg = x.rearrange("n l c -> (n l) c").rearrange("(g p j) c -> g p j c", p=P, j=J)
-    og = out.rearrange("n l c -> (n l) c").rearrange("(g p j) c -> g p j c", p=P, j=J)
+    xg = x.rearrange("n l c -> (n l) c").rearrange("(g j p) c -> g p j c", p=P, j=J)
+    og = out.rearrange("n l c -> (n l) c").rearrange("(g j p) c -> g p j c", p=P, j=J)
 
     with ExitStack() as ctx:
         const = ctx.enter_context(tc.tile_pool(name="const", bufs=1))
@@ -68,9 +67,10 @@ def tile_modulatemlp_pa_w8_kernel(
         nc.sync.dma_start(out=wsc[:], in_=w_scale.rearrange("o (p t) -> p (o t)", t=4))
         wview = weight.rearrange("(b m) c -> m b c", b=4)
         wsb = [const.tile([P, 2, C], BF16, name="wsb%d" % h, align_bytes=64) for h in range(2)]
-        nc.sync.dma_start(out=wsb[0][:], in_=wview[:, 0:2, :])
         sw = const.tile([P, 4 * C], U8, name="sw", align_bytes=64)
         nc.sync.dma_start(out=sw[:], in_=style_w_words[0].rearrange("p n t -> p (n t)"))
+        nc.sync.dma_start(out=wsb[0][:], in_=wview[:, 0:2, :])
+        nc.sync.dma_start(out=wsb[1][:], in_=wview[:, 2:4, :])
         for q in range(4):
             nc.sync.dma_start(
                 out=ssc[32 * q : 32 * q + 4, :].bitcast(I32),
@@ -90,7 +90,6 @@ def tile_modulatemlp_pa_w8_kernel(
         sb = const.tile([P, 4], BF16, name="sb")
         load_x()
         nc.sync.dma_start(out=sb[:], in_=style_b.rearrange("(p t) -> p t", t=4))
-        nc.sync.dma_start(out=wsb[1][:], in_=wview[:, 2:4, :])
         load_x()
         with nc.allow_non_contiguous_dma(reason="one bias value a partition and block"):
             nc.sync.dma_start(out=bb[:, :, 0], in_=bias.rearrange("(b m) -> m b", b=4))
@@ -143,8 +142,10 @@ def tile_modulatemlp_pa_w8_kernel(
                 in_=src[:, halves[h], :].rearrange("p o t -> p (o t)"),
             )
 
+        dps = {}
+
         def demod_half(h):
-            dp = psum.tile([P, 2, N], F32, name="dp", tag="zp", bufs=4)
+            dp = dps[h] = psum.tile([P, 2, N], F32, name="dp", tag="zp", bufs=4)
             for k in range(2):
                 ob = 2 * h + k
                 nc.tensor.matmul_mx(
@@ -156,23 +157,25 @@ def tile_modulatemlp_pa_w8_kernel(
                     start=True,
                     stop=True,
                 )
+
+        def decoef_half(h):
             nc.scalar.activation(
-                dT[:, 2 * h : 2 * h + 2, :], dp[:], ACT.Abs_reciprocal_sqrt, scale=1.0 / gain**2, bias=EPS / gain**2
+                dT[:, 2 * h : 2 * h + 2, :], dps[h][:], ACT.Abs_reciprocal_sqrt, scale=1.0 / gain**2, bias=EPS / gain**2
             )
 
         xp, xm, xq, yy, aa, uu, cc, zz, oo = {}, {}, {}, {}, {}, {}, {}, {}, {}
 
         def stage_x(g):
             xt, k = xtiles[g]
-            xp[g] = psum.tile([P, 2, NS, J, PS], F32, name="xpt", tag="xp", bufs=2)
+            xp[g] = psum.tile([P, 2, J, P], F32, name="xpt", tag="xp", bufs=2)
             for j in range(J):
-                transpose_words(xp[g][:, :, :, j, :], xt[:, k, j, :].bitcast(F32))
+                transpose_words(xp[g][:, :, j, :], xt[:, k, j, :].bitcast(F32))
 
         def stage_a(g):
             xm[g] = xmp.tile([P, J * O], F32, name="xm", align_bytes=64, bufs=5)
             nc.vector.tensor_tensor(
                 out=xm[g][:, : 2 * GT].bitcast(BF16).rearrange("p (n i u e) -> p n i u e", n=NS, u=2, e=2),
-                in0=xp.pop(g)[:].rearrange("p u n j i -> p u (n j i)").bitcast(BF16)
+                in0=xp.pop(g)[:].rearrange("p u j q -> p u (j q)").bitcast(BF16)
                 .rearrange("p u (n i e) -> p n i u e", n=NS, e=2),
                 in1=styT[:, NS * g : NS * g + NS, :]
                 .rearrange("p n (u e) -> p n u e", u=2)
@@ -214,8 +217,8 @@ def tile_modulatemlp_pa_w8_kernel(
                 k, n = divmod(m, NS)
                 ob = 2 * h + k
                 s = NS * g + n
-                yv = y[:, k, :].rearrange("p (n j i) -> p n j i", j=J, n=NS)[:, n]
-                av = aa[g][:, :, ob, :].rearrange("p j (n i) -> p n j i", n=NS)[:, n]
+                yv = y[:, k, L * n : L * n + L]
+                av = aa[g][:, n // 2, ob, L * (n % 2) : L * (n % 2) + L]
                 if on_vector:
                     nc.vector.tensor_scalar(
                         out=av, in0=yv, scalar1=dT[:, ob, s : s + 1], scalar2=bT[:, ob : ob + 1],
@@ -293,10 +296,11 @@ def tile_modulatemlp_pa_w8_kernel(
         wtp = psum.tile([P, 2, P], F32, name="wtp", tag="xp", bufs=2)
         transpose_words(wtp, w16[:].bitcast(F32))
         turn_weight(0)
-        sscp = const.tile([P, C], U8, name="sscp", align_bytes=64)
+        turn_weight(1)
+        swp = const.tile([P, C], I32, name="swp", align_bytes=64)
         nc.vector.tensor_copy(
-            out=sscp[:].rearrange("p (t m) -> p t m", t=4),
-            in_=ssc[:].rearrange("p (m t) -> p t m", t=4),
+            out=swp[:].rearrange("p (t m) -> p t m", t=4),
+            in_=sw[:].bitcast(I32).rearrange("p (m t) -> p t m", t=4),
         )
         wm = const.tile([P, N, 4], BF16, name="wm", align_bytes=64)
         nc.vector.tensor_tensor(
@@ -305,10 +309,10 @@ def tile_modulatemlp_pa_w8_kernel(
             in1=wsc[:].rearrange("p (u e) -> p u e", u=2).unsqueeze(1).to_broadcast([P, N, 2, 2]),
             op=ALU.mult,
         )
-        swp = const.tile([P, C], I32, name="swp", align_bytes=64)
+        sscp = const.tile([P, C], U8, name="sscp", align_bytes=64)
         nc.vector.tensor_copy(
-            out=swp[:].rearrange("p (t m) -> p t m", t=4),
-            in_=sw[:].bitcast(I32).rearrange("p (m t) -> p t m", t=4),
+            out=sscp[:].rearrange("p (t m) -> p t m", t=4),
+            in_=ssc[:].rearrange("p (m t) -> p t m", t=4),
         )
         wq = const.tile([P, N], U32, name="wq", align_bytes=64)
         wqs = const.tile([P, N], U8, name="wqs", align_bytes=64)
@@ -342,27 +346,29 @@ def tile_modulatemlp_pa_w8_kernel(
         def scale_bias():
             nc.scalar.activation(bT[:], bb[:, :, 0], ACT.Copy, scale=gain)
 
-        square_half(0, True)
+        square_half(0, False)
         quantise_half(wc, wcs, wt, 0)
         style_out()
         stage_x(0)
         square_style()
-        turn_weight(1)
         stage_x(1)
         square_half(1, False)
         scale_bias()
-        quantise_half(w2c, w2s, w2, 0)
+        quantise_half(wc, wcs, wt, 1)
         stage_a(0)
         quantise_sq()
-        demod_half(0)
-        quantise_half(wc, wcs, wt, 1)
-        stage_b(0)
-        stage_m(0)
+        quantise_half(w2c, w2s, w2, 0)
         stage_x(2)
-        stage_a(1)
+        demod_half(0)
+        decoef_half(0)
+        stage_b(0)
+        stage_m(0, (0,))
         quantise_half(w2c, w2s, w2, 1)
-        stage_e(0, 0)
         demod_half(1)
+        stage_m(0, (1,))
+        stage_a(1)
+        stage_e(0, 0)
+        decoef_half(1)
         stage_x(3)
         stage_b(1)
         stage_a(2)

@@ -16,29 +16,33 @@ ACT = mybir.ActivationFunctionType
 
 N, L, WD, C, O = 128, 64, 512, 512, 512
 P = 128
-J = 2
-GT = P * J
-GROUPS = N * L // GT
-NS = GT // L
+PACK = 4
+TILES = 2
+TOKENS = P * TILES
+GROUPS = N * L // TOKENS
+SAMPLES = TOKENS // L
+BLOCKS = O // P
 EPS = 1e-8
 CLAMP = 256.0
 FLOPS = 2 * N * L * C * O + 2 * N * WD * C + 2 * N * C * O
+
 AHEAD = 2
-EMPTIES_EVERY = 3
+EMPTIES_PERIOD = 7
 TAIL = 3
 PRELOAD = 5
-
-
-def vector_empties(g):
-    return g % EMPTIES_EVERY == 1
-
-
-def free_clip(g):
-    return vector_empties(g) and summed(g, 1)
+SUM_BANKS, TURN_BANKS = 4, 2
 
 
 def summed(g, j):
     return j == 1 and g < GROUPS - TAIL
+
+
+def vector_empties(g):
+    return g % EMPTIES_PERIOD in (0, EMPTIES_PERIOD // 2)
+
+
+def clipped_on_the_way_out(g):
+    return vector_empties(g) and summed(g, 1)
 
 
 def tile_modulatemlp_pa_w8_kernel(
@@ -46,53 +50,53 @@ def tile_modulatemlp_pa_w8_kernel(
 ):
     nc = tc.nc
     gain = 0.2 * math.sqrt(2.0)
-    xg = x.rearrange("n l c -> (n l) c").rearrange("(g j p) c -> g p j c", p=P, j=J)
-    og = out.rearrange("n l c -> (n l) c").rearrange("(g j p) c -> g p j c", p=P, j=J)
+    x_groups = x.rearrange("n l c -> (n l) c").rearrange("(g j p) c -> g p j c", p=P, j=TILES)
+    out_groups = out.rearrange("n l c -> (n l) c").rearrange("(g j p) c -> g p j c", p=P, j=TILES)
 
     with ExitStack() as ctx:
         const = ctx.enter_context(tc.tile_pool(name="const", bufs=1))
-        xmp = ctx.enter_context(tc.tile_pool(name="xmp", bufs=AHEAD + 2))
-        ap = ctx.enter_context(tc.tile_pool(name="ap", bufs=3))
-        op = ctx.enter_context(tc.tile_pool(name="op", bufs=5))
+        x_pool = ctx.enter_context(tc.tile_pool(name="x_pool", bufs=AHEAD + 2))
+        s_pool = ctx.enter_context(tc.tile_pool(name="s_pool", bufs=3))
+        out_pool = ctx.enter_context(tc.tile_pool(name="out_pool", bufs=5))
         psum = ctx.enter_context(tc.psum_pool(name="psum", bufs=1))
         ctx.enter_context(tc.manual_schedule())
 
-        ssc = const.tile([P, C], U8, name="ssc", align_bytes=64)
-        nc.vector.memset(ssc[:].bitcast(U32), 0)
+        sw_scales = const.tile([P, C], U8, name="sw_scales", align_bytes=64)
+        nc.vector.memset(sw_scales[:].bitcast(U32), 0)
         one = const.tile([P, 1], F32, name="one")
         nc.vector.memset(one[:], 1.0)
-        wb = const.tile([P, WD], U8, name="wb", align_bytes=64)
-        nc.sync.dma_start(out=wb[:], in_=w_bytes)
-        wsc = const.tile([P, 4], F32, name="wsc")
-        nc.sync.dma_start(out=wsc[:], in_=w_scale.rearrange("o (p t) -> p (o t)", t=4))
-        wview = weight.rearrange("(b m) c -> m b c", b=4)
-        wsb = [const.tile([P, 2, C], BF16, name="wsb%d" % h, align_bytes=64) for h in range(2)]
-        sw = const.tile([P, 4 * C], U8, name="sw", align_bytes=64)
-        nc.sync.dma_start(out=sw[:], in_=style_w_words[0].rearrange("p n t -> p (n t)"))
-        nc.sync.dma_start(out=wsb[0][:], in_=wview[:, 0:2, :])
-        nc.sync.dma_start(out=wsb[1][:], in_=wview[:, 2:4, :])
+        w_codes_in = const.tile([P, WD], U8, name="w_codes_in", align_bytes=64)
+        nc.sync.dma_start(out=w_codes_in[:], in_=w_bytes)
+        w_scale_pt = const.tile([P, PACK], F32, name="w_scale_pt")
+        nc.sync.dma_start(out=w_scale_pt[:], in_=w_scale.rearrange("o (p t) -> p (o t)", t=PACK))
+        weight_rows = weight.rearrange("(b m) c -> m b c", b=BLOCKS)
+        weight_in = [const.tile([P, 2, C], BF16, name="weight_in%d" % h, align_bytes=64) for h in range(2)]
+        sw_words = const.tile([P, PACK * C], U8, name="sw_words", align_bytes=64)
+        nc.sync.dma_start(out=sw_words[:], in_=style_w_words[0].rearrange("p n t -> p (n t)"))
+        for h in range(2):
+            nc.sync.dma_start(out=weight_in[h][:], in_=weight_rows[:, 2 * h : 2 * h + 2, :])
         for q in range(4):
             nc.sync.dma_start(
-                out=ssc[32 * q : 32 * q + 4, :].bitcast(I32),
+                out=sw_scales[32 * q : 32 * q + 4, :].bitcast(I32),
                 in_=style_w_scales[0][4 * q : 4 * q + 4, :].bitcast(I32),
             )
-        xtiles = {}
-        bb = const.tile([P, 4, 2], BF16, name="bb")
-        loads = [(0, 1), (1, 1)] + [(g, 2) for g in range(2, GROUPS, 2)]
+        x_in = {}
+        bias_in = const.tile([P, BLOCKS, 2], BF16, name="bias_in")
+        x_loads = [(0, 1), (1, 1)] + [(g, 2) for g in range(2, GROUPS, 2)]
 
         def load_x():
-            g0, n_g = loads.pop(0)
-            xt = const.tile([P, n_g, J, C], BF16, name="x%d" % g0, align_bytes=64)
-            nc.sync.dma_start(out=xt[:], in_=xg[g0 : g0 + n_g].rearrange("g p j c -> p g j c"))
-            for k in range(n_g):
-                xtiles[g0 + k] = (xt, k)
+            first, count = x_loads.pop(0)
+            xt = const.tile([P, count, TILES, C], BF16, name="x%d" % first, align_bytes=64)
+            nc.sync.dma_start(out=xt[:], in_=x_groups[first : first + count].rearrange("g p j c -> p g j c"))
+            for k in range(count):
+                x_in[first + k] = xt[:, k]
 
-        sb = const.tile([P, 4], BF16, name="sb")
+        style_b_pt = const.tile([P, PACK], BF16, name="style_b_pt")
         load_x()
-        nc.sync.dma_start(out=sb[:], in_=style_b.rearrange("(p t) -> p t", t=4))
+        nc.sync.dma_start(out=style_b_pt[:], in_=style_b.rearrange("(p t) -> p t", t=PACK))
         load_x()
         with nc.allow_non_contiguous_dma(reason="one bias value a partition and block"):
-            nc.sync.dma_start(out=bb[:, :, 0], in_=bias.rearrange("(b m) -> m b", b=4))
+            nc.sync.dma_start(out=bias_in[:, :, 0], in_=bias.rearrange("(b m) -> m b", b=BLOCKS))
         for k in range(PRELOAD):
             load_x()
 
@@ -101,346 +105,317 @@ def tile_modulatemlp_pa_w8_kernel(
         ident = const.tile([P, P], F32, name="ident")
         make_identity(nc, ident[:])
 
-        def transpose_words(dst, words):
+        def turn_words(dst, rows):
+            words = rows.bitcast(F32)
             for u in range(2):
                 nc.tensor.transpose(dst[:, u], words[:, u : C // 2 : 2], ident[:])
 
-        wt = const.tile([P, O, 4], BF16, name="wt", align_bytes=64)
-        wt32 = wt[:].rearrange("p o t -> p (o t)").bitcast(F32)
-        wc = const.tile([P, O], U32, name="wc", align_bytes=64)
-        wcs = const.tile([P, O], U8, name="wcs", align_bytes=64)
-        w2 = const.tile([P, O, 4], BF16, name="w2", align_bytes=64)
-        w2c = const.tile([P, O], U32, name="w2c", align_bytes=64)
-        w2s = const.tile([P, O], U8, name="w2s", align_bytes=64)
-        sq = const.tile([P, N, 4], BF16, name="sq", align_bytes=64)
-        sqc = const.tile([P, N], U32, name="sqc", align_bytes=64)
-        sqs = const.tile([P, N], U8, name="sqs", align_bytes=64)
-        styT = const.tile([P, N, 4], F32, name="styT", align_bytes=64)
-        dT = const.tile([P, 4, N], F32, name="dT")
-        bT = const.tile([P, 4], F32, name="bT")
-        halves = [slice(0, O // 2), slice(O // 2, O)]
-
-        def turn_weight(h):
-            ww = psum.tile([P, 2, 2, P], F32, name="ww", tag="zp", bufs=4)
-            for k in range(2):
-                transpose_words(ww[:, k], wsb[h][:, k, :].bitcast(F32))
-            nc.scalar.copy(
-                out=wt32[:, 512 * h : 512 * h + 512].rearrange("p (b r u) -> p b r u", b=2, u=2),
-                in_=ww[:].rearrange("p b u r -> p b r u"),
-            )
-
-        def square_half(h, on_vector):
-            if on_vector:
-                nc.vector.tensor_tensor(out=w2[:, halves[h], :], in0=wt[:, halves[h], :], in1=wt[:, halves[h], :], op=ALU.mult)
-            else:
-                nc.scalar.activation(w2[:, halves[h], :], wt[:, halves[h], :], ACT.Square)
-
-        def quantise_half(codes, scales, src, h):
-            nc.vector.quantize_mx(
-                out=codes[:, halves[h]].bitcast(X4),
-                scales=scales[:, halves[h]],
-                in_=src[:, halves[h], :].rearrange("p o t -> p (o t)"),
-            )
-
-        dps = {}
-
-        def demod_half(h):
-            dp = dps[h] = psum.tile([P, 2, N], F32, name="dp", tag="zp", bufs=4)
-            for k in range(2):
-                ob = 2 * h + k
-                nc.tensor.matmul_mx(
-                    out=dp[:, k, :],
-                    lhsT=w2c[:, P * ob : P * ob + P].bitcast(X4),
-                    lhsT_scale=w2s[:, P * ob : P * ob + P],
-                    rhs=sqc[:].bitcast(X4),
-                    rhs_scale=sqs[:],
-                    start=True,
-                    stop=True,
-                )
-
-        def decoef_half(h):
-            nc.scalar.activation(
-                dT[:, 2 * h : 2 * h + 2, :], dps[h][:], ACT.Abs_reciprocal_sqrt, scale=1.0 / gain**2, bias=EPS / gain**2
-            )
-
-        xp, xm, xq, yy, aa, uu, cc, zz, oo = {}, {}, {}, {}, {}, {}, {}, {}, {}
-
-        def stage_x(g):
-            xt, k = xtiles[g]
-            xp[g] = psum.tile([P, 2, J, P], F32, name="xpt", tag="xp", bufs=2)
-            for j in range(J):
-                transpose_words(xp[g][:, :, j, :], xt[:, k, j, :].bitcast(F32))
-
-        def stage_a(g):
-            xm[g] = xmp.tile([P, J * O], F32, name="xm", align_bytes=64, bufs=5)
-            nc.vector.tensor_tensor(
-                out=xm[g][:, : 2 * GT].bitcast(BF16).rearrange("p (n i u e) -> p n i u e", n=NS, u=2, e=2),
-                in0=xp.pop(g)[:].rearrange("p u j q -> p u (j q)").bitcast(BF16)
-                .rearrange("p u (n i e) -> p n i u e", n=NS, e=2),
-                in1=styT[:, NS * g : NS * g + NS, :]
-                .rearrange("p n (u e) -> p n u e", u=2)
-                .unsqueeze(2)
-                .to_broadcast([P, NS, L, 2, 2]),
-                op=ALU.mult,
-            )
-
-        def stage_b(g):
-            xc = xmp.tile([P, GT], U32, name="xc", align_bytes=64)
-            xs = xmp.tile([P, GT], U8, name="xs", align_bytes=64)
-            nc.vector.quantize_mx(
-                out=xc[:].bitcast(X4), scales=xs[:], in_=xm[g][:, : 2 * GT].bitcast(BF16)
-            )
-            xq[g] = (xc, xs)
-
-        def stage_m(g, hs=(0, 1)):
-            xc, xs = xq[g]
-            for h in hs:
-                y = psum.tile([P, 2, GT], F32, name="y%d" % h, tag="ya" if h == 0 else "yb", bufs=1)
-                for k in range(2):
-                    ob = 2 * h + k
-                    nc.tensor.matmul_mx(
-                        out=y[:, k, :],
-                        lhsT=wc[:, P * ob : P * ob + P].bitcast(X4),
-                        lhsT_scale=wcs[:, P * ob : P * ob + P],
-                        rhs=xc[:].bitcast(X4),
-                        rhs_scale=xs[:],
-                        start=True,
-                        stop=True,
-                    )
-                yy[g, h] = y
-
-        def stage_e(g, h, first=0, last=2 * NS, on_vector=False):
-            if g not in aa:
-                aa[g] = ap.tile([P, J, 4, P], F32, name="a", bufs=4)
-            y = yy[g, h]
-            for m in range(first, last):
-                k, n = divmod(m, NS)
-                ob = 2 * h + k
-                s = NS * g + n
-                yv = y[:, k, L * n : L * n + L]
-                av = aa[g][:, n // 2, ob, L * (n % 2) : L * (n % 2) + L]
-                if on_vector:
-                    nc.vector.tensor_scalar(
-                        out=av, in0=yv, scalar1=dT[:, ob, s : s + 1], scalar2=bT[:, ob : ob + 1],
-                        op0=ALU.mult, op1=ALU.add,
-                    )
-                else:
-                    nc.scalar.activation(av, yv, ACT.Identity, scale=dT[:, ob, s : s + 1], bias=bT[:, ob : ob + 1])
-
-        def stage_k(g, engine, js=(0, J)):
-            src = aa[g][:].rearrange("p j b m -> p (j b m)")
-            if g not in uu:
-                uu[g] = xm[g + AHEAD][:] if g + AHEAD in xm else src
-            if free_clip(g):
-                js = (0, 1)
-            cols = slice(O * js[0], O * js[1])
-            engine.tensor_scalar(
-                out=uu[g][:, cols], in0=src[:, cols], scalar1=CLAMP / 5.0, scalar2=-CLAMP, op0=ALU.min, op1=ALU.max
-            )
-
-        def turned(g, j):
-            if j == 1 and free_clip(g):
-                return aa[g][:, j].rearrange("p b m -> p (b m)")
-            return uu[g][:, O * j : O * j + O]
-
-        def stage_r(g, j=1):
-            if summed(g, j):
-                cc[g, j] = ap.tile([P, O], F32, name="c", bufs=3)
-                nc.vector.tensor_scalar(
-                    out=cc[g, j][:], in0=turned(g, j), scalar1=0.0, scalar2=4.0,
-                    op0=ALU.max, op1=ALU.mult,
-                )
-
-        def stage_z(g, j, tag="zp"):
-            z = psum.tile([P, O], F32, name="z", tag=tag, bufs=4 if tag == "zp" else 2)
-            for ob in range(4):
-                dst = z[:, P * ob : P * ob + P]
-                src = turned(g, j)[:, P * ob : P * ob + P]
-                if summed(g, j):
-                    nc.tensor.matmul(dst, lhsT=src, rhs=ident[:], start=True, stop=False, is_transpose=True)
-                    nc.tensor.matmul(
-                        dst, lhsT=cc[g, j][:, P * ob : P * ob + P], rhs=ident[:], start=False, stop=True, is_transpose=True
-                    )
-                else:
-                    nc.tensor.transpose(dst, src, ident[:])
-            zz[g, j] = z
-
-        def stage_c(g, j, on_vector=False):
-            if g not in oo:
-                oo[g] = op.tile([P, J, O], F32, name="o")
-            if j == 1 and free_clip(g):
-                nc.vector.tensor_scalar(
-                    out=oo[g][:, j, :], in0=zz[g, j][:], scalar1=CLAMP, scalar2=-CLAMP, op0=ALU.min, op1=ALU.max
-                )
-            elif on_vector:
-                nc.vector.tensor_copy(out=oo[g][:, j, :], in_=zz[g, j][:])
-            else:
-                nc.scalar.copy(out=oo[g][:, j, :], in_=zz[g, j][:])
-
-        def stage_l(g, j):
-            if not summed(g, j):
-                nc.vector.scalar_tensor_tensor(
-                    out=oo[g][:, j, :], in0=zz[g, j][:], scalar=5.0, in1=oo[g][:, j, :], op0=ALU.mult, op1=ALU.max
-                )
-
-        def stage_o(g, j=None):
-            if j is None:
-                nc.sync.dma_start(out=og[g], in_=oo[g][:])
-                if g % 2 == 1 and loads:
-                    load_x()
-            else:
-                nc.sync.dma_start(out=og[g][:, j, :], in_=oo[g][:, j, :])
-
-        w16 = const.tile([P, WD], BF16, name="w16", align_bytes=64)
-        nc.vector.tensor_copy(out=w16[:], in_=wb[:].bitcast(F8))
-        wtp = psum.tile([P, 2, P], F32, name="wtp", tag="xp", bufs=2)
-        transpose_words(wtp, w16[:].bitcast(F32))
-        turn_weight(0)
-        turn_weight(1)
-        swp = const.tile([P, C], I32, name="swp", align_bytes=64)
-        nc.vector.tensor_copy(
-            out=swp[:].rearrange("p (t m) -> p t m", t=4),
-            in_=sw[:].bitcast(I32).rearrange("p (m t) -> p t m", t=4),
-        )
-        wm = const.tile([P, N, 4], BF16, name="wm", align_bytes=64)
-        nc.vector.tensor_tensor(
-            out=wm[:].rearrange("p n (u e) -> p n u e", u=2),
-            in0=wtp[:].bitcast(BF16).rearrange("p u (n e) -> p n u e", e=2),
-            in1=wsc[:].rearrange("p (u e) -> p u e", u=2).unsqueeze(1).to_broadcast([P, N, 2, 2]),
-            op=ALU.mult,
-        )
-        sscp = const.tile([P, C], U8, name="sscp", align_bytes=64)
-        nc.vector.tensor_copy(
-            out=sscp[:].rearrange("p (t m) -> p t m", t=4),
-            in_=ssc[:].rearrange("p (m t) -> p t m", t=4),
-        )
-        wq = const.tile([P, N], U32, name="wq", align_bytes=64)
-        wqs = const.tile([P, N], U8, name="wqs", align_bytes=64)
-        nc.vector.quantize_mx(out=wq[:].bitcast(X4), scales=wqs[:], in_=wm[:].rearrange("p n t -> p (n t)"))
-
-        sp = psum.tile([P, 4, N], F32, name="sp", tag="ya", bufs=1)
-        for t in range(4):
+        def mx_pass(dst, stationary, moving):
             nc.tensor.matmul_mx(
-                out=sp[:, t, :],
-                lhsT=swp[:, P * t : P * t + P].bitcast(X4),
-                lhsT_scale=sscp[:, P * t : P * t + P],
-                rhs=wq[:].bitcast(X4),
-                rhs_scale=wqs[:],
+                out=dst,
+                lhsT=stationary[0].bitcast(X4),
+                lhsT_scale=stationary[1],
+                rhs=moving[0].bitcast(X4),
+                rhs_scale=moving[1],
                 start=True,
                 stop=True,
             )
-        wscale = 1.0 / math.sqrt(WD)
 
-        def style_out():
-            nc.vector.scalar_tensor_tensor(
-                out=styT[:], in0=sp[:].rearrange("p t n -> p n t"), scalar=wscale,
-                in1=sb[:].unsqueeze(1).to_broadcast([P, N, 4]), op0=ALU.mult, op1=ALU.add,
+        def block(pair, b):
+            return [t[:, P * b : P * b + P] for t in pair]
+
+        weight_k = const.tile([P, O, PACK], BF16, name="weight_k", align_bytes=64)
+        weight_k_words = weight_k[:].rearrange("p o t -> p (o t)").bitcast(F32)
+        weight_mx = (
+            const.tile([P, O], U32, name="weight_codes", align_bytes=64),
+            const.tile([P, O], U8, name="weight_scales", align_bytes=64),
+        )
+        weight2_k = const.tile([P, O, PACK], BF16, name="weight2_k", align_bytes=64)
+        weight2_mx = (
+            const.tile([P, O], U32, name="weight2_codes", align_bytes=64),
+            const.tile([P, O], U8, name="weight2_scales", align_bytes=64),
+        )
+        style2_k = const.tile([P, N, PACK], BF16, name="style2_k", align_bytes=64)
+        style2_mx = (
+            const.tile([P, N], U32, name="style2_codes", align_bytes=64),
+            const.tile([P, N], U8, name="style2_scales", align_bytes=64),
+        )
+        style_k = const.tile([P, N, PACK], F32, name="style_k", align_bytes=64)
+        decoef = const.tile([P, BLOCKS, N], F32, name="decoef")
+        bias_col = const.tile([P, BLOCKS], F32, name="bias_col")
+        halves = [slice(0, O // 2), slice(O // 2, O)]
+
+        def turn_weight(h):
+            bank = psum.tile([P, 2, 2, P], F32, name="weight_bank", tag="sum", bufs=SUM_BANKS)
+            for k in range(2):
+                turn_words(bank[:, k], weight_in[h][:, k, :])
+            nc.scalar.copy(
+                out=weight_k_words[:, O * h : O * h + O].rearrange("p (b r u) -> p b r u", b=2, u=2),
+                in_=bank[:].rearrange("p b u r -> p b r u"),
             )
 
-        def square_style():
-            nc.scalar.activation(sq[:], styT[:], ACT.Square)
+        def square_weight(h):
+            nc.scalar.activation(weight2_k[:, halves[h], :], weight_k[:, halves[h], :], ACT.Square)
 
-        def quantise_sq():
-            nc.vector.quantize_mx(out=sqc[:].bitcast(X4), scales=sqs[:], in_=sq[:].rearrange("p n t -> p (n t)"))
+        def quantise(pair, src, cols=slice(None)):
+            nc.vector.quantize_mx(
+                out=pair[0][:, cols].bitcast(X4), scales=pair[1][:, cols], in_=src[:, cols, :].rearrange("p c t -> p (c t)")
+            )
 
-        def scale_bias():
-            nc.scalar.activation(bT[:], bb[:, :, 0], ACT.Copy, scale=gain)
+        d_bank = {}
 
-        square_half(0, False)
-        quantise_half(wc, wcs, wt, 0)
-        style_out()
-        stage_x(0)
-        square_style()
-        stage_x(1)
-        square_half(1, False)
-        scale_bias()
-        quantise_half(wc, wcs, wt, 1)
-        stage_a(0)
-        quantise_sq()
-        quantise_half(w2c, w2s, w2, 0)
-        stage_x(2)
-        demod_half(0)
-        decoef_half(0)
-        stage_b(0)
-        stage_m(0, (0,))
-        quantise_half(w2c, w2s, w2, 1)
-        demod_half(1)
-        stage_m(0, (1,))
-        stage_a(1)
-        stage_e(0, 0)
-        decoef_half(1)
-        stage_x(3)
-        stage_b(1)
-        stage_a(2)
-        stage_e(0, 1)
-        stage_b(2)
+        def demod_sums(h):
+            d_bank[h] = psum.tile([P, 2, N], F32, name="d_bank", tag="sum", bufs=SUM_BANKS)
+            for k in range(2):
+                mx_pass(d_bank[h][:, k, :], block(weight2_mx, 2 * h + k), [t[:] for t in style2_mx])
 
-        def has(g):
-            return 0 <= g < GROUPS
+        def demod_coefficients(h):
+            nc.scalar.activation(
+                decoef[:, 2 * h : 2 * h + 2, :], d_bank[h][:], ACT.Abs_reciprocal_sqrt,
+                scale=1.0 / gain**2, bias=EPS / gain**2,
+            )
 
-        LAST = GROUPS - AHEAD
-        for i in range(1, LAST):
-            stage_k(i - 1, nc.gpsimd)
-            stage_m(i)
-            if has(i - 2):
-                stage_z(i - 2, 0)
-            if has(i + AHEAD + 1):
-                stage_x(i + AHEAD + 1)
-            if has(i - 2):
-                stage_z(i - 2, 1)
-            stage_e(i, 0)
-            stage_a(i + AHEAD)
-            if has(i - 3) and vector_empties(i - 3):
-                stage_c(i - 3, 1, on_vector=True)
-            stage_e(i, 1)
-            if has(i - 2):
-                stage_c(i - 2, 0)
-                if i + 1 < LAST and not vector_empties(i - 2):
-                    stage_c(i - 2, 1)
-            if has(i - 3):
-                stage_l(i - 3, 0)
-                stage_o(i - 3)
-            stage_b(i + AHEAD)
-            stage_r(i - 1)
+        x_bank, staging, x_mx, y_bank, s_tile, c_tile, relu4, back_bank, out_tile = {}, {}, {}, {}, {}, {}, {}, {}, {}
 
-        a, b = GROUPS - 2, GROUPS - 1
-        stage_k(a - 1, nc.gpsimd)
-        stage_m(a)
-        stage_z(a - 2, 0)
-        stage_z(a - 2, 1)
-        stage_e(a, 0)
-        stage_e(a, 1)
-        stage_l(a - 3, 0)
-        stage_o(a - 3, 0)
-        stage_c(a - 3, 1, on_vector=True)
-        stage_o(a - 3, 1)
-        stage_m(b)
-        stage_k(a, nc.gpsimd)
-        stage_z(a - 1, 1, "xp")
-        stage_z(a - 1, 0, "xp")
-        stage_c(a - 2, 0)
-        stage_c(a - 2, 1, on_vector=True)
-        stage_o(a - 2, 1)
-        stage_e(b, 0)
-        stage_e(b, 1, on_vector=True)
-        stage_k(b, nc.gpsimd, (0, 1))
-        stage_k(b, nc.gpsimd, (1, 2))
-        stage_l(a - 2, 0)
-        stage_o(a - 2, 0)
-        stage_c(a - 1, 1)
-        stage_z(a, 0)
-        stage_z(a, 1)
-        stage_l(a - 1, 1)
-        stage_o(a - 1, 1)
-        stage_c(a - 1, 0)
-        stage_l(a - 1, 0)
-        stage_o(a - 1, 0)
-        stage_c(a, 0)
-        stage_z(b, 0)
-        stage_z(b, 1)
-        last = [(a, 0), (a, 1), (b, 0), (b, 1)]
-        for now, then in zip(last, last[1:] + [None]):
-            if then:
-                stage_c(*then)
-            stage_l(*now)
-            stage_o(*now)
+        def turn_x(g):
+            x_bank[g] = psum.tile([P, 2, TILES, P], F32, name="x_bank", tag="turn", bufs=TURN_BANKS)
+            for j in range(TILES):
+                turn_words(x_bank[g][:, :, j, :], x_in[g][:, j, :])
+
+        def modulate(g):
+            staging[g] = x_pool.tile([P, TILES * O], F32, name="staging", align_bytes=64, bufs=5)
+            nc.vector.tensor_tensor(
+                out=staging[g][:, : 2 * TOKENS].bitcast(BF16).rearrange("p (n l u e) -> p n l u e", n=SAMPLES, u=2, e=2),
+                in0=x_bank.pop(g)[:].rearrange("p u j q -> p u (j q)").bitcast(BF16)
+                .rearrange("p u (n l e) -> p n l u e", n=SAMPLES, e=2),
+                in1=style_k[:, SAMPLES * g : SAMPLES * g + SAMPLES, :]
+                .rearrange("p n (u e) -> p n u e", u=2)
+                .unsqueeze(2)
+                .to_broadcast([P, SAMPLES, L, 2, 2]),
+                op=ALU.mult,
+            )
+
+        def quantise_x(g):
+            codes = x_pool.tile([P, TOKENS], U32, name="x_codes", align_bytes=64)
+            scales = x_pool.tile([P, TOKENS], U8, name="x_scales", align_bytes=64)
+            nc.vector.quantize_mx(
+                out=codes[:].bitcast(X4), scales=scales[:], in_=staging[g][:, : 2 * TOKENS].bitcast(BF16)
+            )
+            x_mx[g] = (codes[:], scales[:])
+
+        def multiply(g, banks=(0, 1)):
+            for h in banks:
+                y_bank[g, h] = psum.tile([P, 2, TOKENS], F32, name="y_bank", tag="y%d" % h, bufs=1)
+                for k in range(2):
+                    mx_pass(y_bank[g, h][:, k, :], block(weight_mx, 2 * h + k), x_mx[g])
+
+        def scale_and_bias(g, h, on_vector=False):
+            if g not in s_tile:
+                s_tile[g] = s_pool.tile([P, TILES, BLOCKS, P], F32, name="s_tile", bufs=4)
+            for k in range(2):
+                b = 2 * h + k
+                for n in range(SAMPLES):
+                    j, place = divmod(n, SAMPLES // TILES)
+                    src = y_bank[g, h][:, k, L * n : L * n + L]
+                    dst = s_tile[g][:, j, b, L * place : L * place + L]
+                    coefficient = decoef[:, b, SAMPLES * g + n : SAMPLES * g + n + 1]
+                    if on_vector:
+                        nc.vector.tensor_scalar(
+                            out=dst, in0=src, scalar1=coefficient, scalar2=bias_col[:, b : b + 1],
+                            op0=ALU.mult, op1=ALU.add,
+                        )
+                    else:
+                        nc.scalar.activation(dst, src, ACT.Identity, scale=coefficient, bias=bias_col[:, b : b + 1])
+
+        def clip(g, first=0, last=TILES):
+            src = s_tile[g][:].rearrange("p j b m -> p (j b m)")
+            if g not in c_tile:
+                c_tile[g] = staging[g + AHEAD][:] if g + AHEAD in staging else src
+            if clipped_on_the_way_out(g):
+                last = 1
+            cols = slice(O * first, O * last)
+            nc.gpsimd.tensor_scalar(
+                out=c_tile[g][:, cols], in0=src[:, cols], scalar1=CLAMP / 5.0, scalar2=-CLAMP, op0=ALU.min, op1=ALU.max
+            )
+
+        def to_turn_back(g, j):
+            if j == 1 and clipped_on_the_way_out(g):
+                return s_tile[g][:, j].rearrange("p b m -> p (b m)")
+            return c_tile[g][:, O * j : O * j + O]
+
+        def positive_part(g):
+            if summed(g, 1):
+                relu4[g] = s_pool.tile([P, O], F32, name="relu4", bufs=3)
+                nc.vector.tensor_scalar(
+                    out=relu4[g][:], in0=to_turn_back(g, 1), scalar1=0.0, scalar2=4.0, op0=ALU.max, op1=ALU.mult
+                )
+
+        def turn_back(g, j, in_turn_bank=False):
+            tag, bufs = ("turn", TURN_BANKS) if in_turn_bank else ("sum", SUM_BANKS)
+            back_bank[g, j] = psum.tile([P, O], F32, name="back_bank", tag=tag, bufs=bufs)
+            for b in range(BLOCKS):
+                dst = back_bank[g, j][:, P * b : P * b + P]
+                src = to_turn_back(g, j)[:, P * b : P * b + P]
+                if summed(g, j):
+                    nc.tensor.matmul(dst, lhsT=src, rhs=ident[:], start=True, stop=False, is_transpose=True)
+                    nc.tensor.matmul(
+                        dst, lhsT=relu4[g][:, P * b : P * b + P], rhs=ident[:], start=False, stop=True, is_transpose=True
+                    )
+                else:
+                    nc.tensor.transpose(dst, src, ident[:])
+
+        def copy_out(g, j, on_vector=False):
+            if g not in out_tile:
+                out_tile[g] = out_pool.tile([P, TILES, O], F32, name="out_tile")
+            dst, src = out_tile[g][:, j, :], back_bank[g, j][:]
+            if j == 1 and clipped_on_the_way_out(g):
+                nc.vector.tensor_scalar(out=dst, in0=src, scalar1=CLAMP, scalar2=-CLAMP, op0=ALU.min, op1=ALU.max)
+            elif on_vector:
+                nc.vector.tensor_copy(out=dst, in_=src)
+            else:
+                nc.scalar.copy(out=dst, in_=src)
+
+        def leaky_relu(g, j):
+            nc.vector.scalar_tensor_tensor(
+                out=out_tile[g][:, j, :], in0=back_bank[g, j][:], scalar=5.0, in1=out_tile[g][:, j, :],
+                op0=ALU.mult, op1=ALU.max,
+            )
+
+        def store_group(g):
+            nc.sync.dma_start(out=out_groups[g], in_=out_tile[g][:])
+            if g % 2 == 1 and x_loads:
+                load_x()
+
+        def store_tile(g, j):
+            nc.sync.dma_start(out=out_groups[g][:, j, :], in_=out_tile[g][:, j, :])
+
+        w_wide = const.tile([P, WD], BF16, name="w_wide", align_bytes=64)
+        nc.vector.tensor_copy(out=w_wide[:], in_=w_codes_in[:].bitcast(F8))
+        w_bank = psum.tile([P, 2, P], F32, name="w_bank", tag="turn", bufs=TURN_BANKS)
+        turn_words(w_bank, w_wide[:])
+        turn_weight(0)
+        turn_weight(1)
+        sw_words_tm = const.tile([P, C], I32, name="sw_words_tm", align_bytes=64)
+        nc.vector.tensor_copy(
+            out=sw_words_tm[:].rearrange("p (t m) -> p t m", t=PACK),
+            in_=sw_words[:].bitcast(I32).rearrange("p (m t) -> p t m", t=PACK),
+        )
+        w_k = const.tile([P, N, PACK], BF16, name="w_k", align_bytes=64)
+        nc.vector.tensor_tensor(
+            out=w_k[:].rearrange("p n (u e) -> p n u e", u=2),
+            in0=w_bank[:].bitcast(BF16).rearrange("p u (n e) -> p n u e", e=2),
+            in1=w_scale_pt[:].rearrange("p (u e) -> p u e", u=2).unsqueeze(1).to_broadcast([P, N, 2, 2]),
+            op=ALU.mult,
+        )
+        sw_scales_tm = const.tile([P, C], U8, name="sw_scales_tm", align_bytes=64)
+        nc.vector.tensor_copy(
+            out=sw_scales_tm[:].rearrange("p (t m) -> p t m", t=PACK),
+            in_=sw_scales[:].rearrange("p (m t) -> p t m", t=PACK),
+        )
+        w_mx = (
+            const.tile([P, N], U32, name="w_codes", align_bytes=64),
+            const.tile([P, N], U8, name="w_scales", align_bytes=64),
+        )
+        quantise(w_mx, w_k)
+        style_bank = psum.tile([P, PACK, N], F32, name="style_bank", tag="y0", bufs=1)
+        for t in range(PACK):
+            mx_pass(style_bank[:, t, :], block((sw_words_tm, sw_scales_tm), t), [tile[:] for tile in w_mx])
+
+        square_weight(0)
+        quantise(weight_mx, weight_k, halves[0])
+        nc.vector.scalar_tensor_tensor(
+            out=style_k[:], in0=style_bank[:].rearrange("p t n -> p n t"), scalar=1.0 / math.sqrt(WD),
+            in1=style_b_pt[:].unsqueeze(1).to_broadcast([P, N, PACK]), op0=ALU.mult, op1=ALU.add,
+        )
+        turn_x(0)
+        nc.scalar.activation(style2_k[:], style_k[:], ACT.Square)
+        turn_x(1)
+        square_weight(1)
+        nc.scalar.activation(bias_col[:], bias_in[:, :, 0], ACT.Copy, scale=gain)
+        quantise(weight_mx, weight_k, halves[1])
+        modulate(0)
+        quantise(style2_mx, style2_k)
+        quantise(weight2_mx, weight2_k, halves[0])
+        turn_x(2)
+        demod_sums(0)
+        demod_coefficients(0)
+        quantise_x(0)
+        multiply(0, (0,))
+        quantise(weight2_mx, weight2_k, halves[1])
+        demod_sums(1)
+        multiply(0, (1,))
+        modulate(1)
+        scale_and_bias(0, 0)
+        demod_coefficients(1)
+        turn_x(3)
+        quantise_x(1)
+        modulate(2)
+        scale_and_bias(0, 1)
+        quantise_x(2)
+
+        steps = GROUPS - AHEAD
+        for i in range(1, steps):
+            clip(i - 1)
+            multiply(i)
+            if i >= 2:
+                turn_back(i - 2, 0)
+            if i + AHEAD + 1 < GROUPS:
+                turn_x(i + AHEAD + 1)
+            if i >= 2:
+                turn_back(i - 2, 1)
+            scale_and_bias(i, 0)
+            modulate(i + AHEAD)
+            if i >= 3 and vector_empties(i - 3):
+                copy_out(i - 3, 1, on_vector=True)
+            scale_and_bias(i, 1)
+            if i >= 2:
+                copy_out(i - 2, 0)
+                if i + 1 < steps and not vector_empties(i - 2):
+                    copy_out(i - 2, 1)
+            if i >= 3:
+                leaky_relu(i - 3, 0)
+                store_group(i - 3)
+            quantise_x(i + AHEAD)
+            positive_part(i - 1)
+
+        g0, g1, g2, g3, g4 = range(GROUPS - 5, GROUPS)
+        clip(g2)
+        multiply(g3)
+        turn_back(g1, 0)
+        turn_back(g1, 1)
+        scale_and_bias(g3, 0)
+        scale_and_bias(g3, 1)
+        leaky_relu(g0, 0)
+        store_tile(g0, 0)
+        copy_out(g0, 1, on_vector=True)
+        store_tile(g0, 1)
+        multiply(g4)
+        clip(g3)
+        turn_back(g2, 1, in_turn_bank=True)
+        turn_back(g2, 0, in_turn_bank=True)
+        copy_out(g1, 0)
+        copy_out(g1, 1, on_vector=True)
+        store_tile(g1, 1)
+        scale_and_bias(g4, 0)
+        scale_and_bias(g4, 1, on_vector=True)
+        for j in range(TILES):
+            clip(g4, j, j + 1)
+        leaky_relu(g1, 0)
+        store_tile(g1, 0)
+        copy_out(g2, 1)
+        turn_back(g3, 0)
+        turn_back(g3, 1)
+        leaky_relu(g2, 1)
+        store_tile(g2, 1)
+        copy_out(g2, 0)
+        leaky_relu(g2, 0)
+        store_tile(g2, 0)
+        copy_out(g3, 0)
+        turn_back(g4, 0)
+        turn_back(g4, 1)
+        remaining = [(g3, 0), (g3, 1), (g4, 0), (g4, 1)]
+        for k, (g, j) in enumerate(remaining):
+            if k + 1 < len(remaining):
+                copy_out(*remaining[k + 1])
+            leaky_relu(g, j)
+            store_tile(g, j)

@@ -38,7 +38,7 @@ def summed(g, j):
 
 
 def vector_empties(g):
-    return g % EMPTIES_PERIOD in (0, EMPTIES_PERIOD // 2)
+    return g == 0 or g % EMPTIES_PERIOD in (1, 1 + (EMPTIES_PERIOD + 1) // 2)
 
 
 def clipped_on_the_way_out(g):
@@ -341,10 +341,10 @@ def tile_modulatemlp_pa_w8_kernel(
         demod_coefficients(0)
         quantise_x(0)
         multiply(0, (0,))
-        quantise(weight2_mx, weight2_k, halves[1])
-        demod_sums(1)
         multiply(0, (1,))
         modulate(1)
+        quantise(weight2_mx, weight2_k, halves[1])
+        demod_sums(1)
         scale_and_bias(0, 0)
         demod_coefficients(1)
         turn_x(3)
@@ -375,8 +375,12 @@ def tile_modulatemlp_pa_w8_kernel(
             if i >= 3:
                 leaky_relu(i - 3, 0)
                 store_group(i - 3)
-            quantise_x(i + AHEAD)
-            positive_part(i - 1)
+            if i >= 3:
+                quantise_x(i + AHEAD)
+                positive_part(i - 1)
+            else:
+                positive_part(i - 1)
+                quantise_x(i + AHEAD)
 
         g0, g1, g2, g3, g4 = range(GROUPS - 5, GROUPS)
         clip(g2)

@@ -26,23 +26,19 @@ EPS = 1e-8
 CLAMP = 256.0
 FLOPS = 2 * N * L * C * O + 2 * N * WD * C + 2 * N * C * O
 
-AHEAD = 2
-EMPTIES_PERIOD = 7
+ON_GPSIMD = 1
+LEAD = 3
+RAMP = 3
+SHARED_FROM = LEAD + 4
 TAIL = 3
+ALONE = 1
+SPLIT = 192
 PRELOAD = 5
-SUM_BANKS, TURN_BANKS = 4, 2
+TURN_BANKS = 2
 
 
-def summed(g, j):
-    return j == 1 and g < GROUPS - TAIL
-
-
-def vector_empties(g):
-    return g == 0 or g % EMPTIES_PERIOD in (1, 1 + (EMPTIES_PERIOD + 1) // 2)
-
-
-def clipped_on_the_way_out(g):
-    return vector_empties(g) and summed(g, 1)
+def scalar_columns(g):
+    return SPLIT if RAMP <= g < GROUPS - 5 else 0
 
 
 def tile_modulatemlp_pa_w8_kernel(
@@ -55,7 +51,7 @@ def tile_modulatemlp_pa_w8_kernel(
 
     with ExitStack() as ctx:
         const = ctx.enter_context(tc.tile_pool(name="const", bufs=1))
-        x_pool = ctx.enter_context(tc.tile_pool(name="x_pool", bufs=AHEAD + 2))
+        x_pool = ctx.enter_context(tc.tile_pool(name="x_pool", bufs=LEAD + 2))
         s_pool = ctx.enter_context(tc.tile_pool(name="s_pool", bufs=3))
         out_pool = ctx.enter_context(tc.tile_pool(name="out_pool", bufs=5))
         psum = ctx.enter_context(tc.psum_pool(name="psum", bufs=1))
@@ -66,22 +62,13 @@ def tile_modulatemlp_pa_w8_kernel(
         one = const.tile([P, 1], F32, name="one")
         nc.vector.memset(one[:], 1.0)
         w_codes_in = const.tile([P, WD], U8, name="w_codes_in", align_bytes=64)
-        nc.sync.dma_start(out=w_codes_in[:], in_=w_bytes)
         w_scale_pt = const.tile([P, PACK], F32, name="w_scale_pt")
-        nc.sync.dma_start(out=w_scale_pt[:], in_=w_scale.rearrange("o (p t) -> p (o t)", t=PACK))
         weight_rows = weight.rearrange("(b m) c -> m b c", b=BLOCKS)
         weight_in = [const.tile([P, 2, C], BF16, name="weight_in%d" % h, align_bytes=64) for h in range(2)]
         sw_words = const.tile([P, PACK * C], U8, name="sw_words", align_bytes=64)
-        nc.sync.dma_start(out=sw_words[:], in_=style_w_words[0].rearrange("p n t -> p (n t)"))
-        for h in range(2):
-            nc.sync.dma_start(out=weight_in[h][:], in_=weight_rows[:, 2 * h : 2 * h + 2, :])
-        for q in range(4):
-            nc.sync.dma_start(
-                out=sw_scales[32 * q : 32 * q + 4, :].bitcast(I32),
-                in_=style_w_scales[0][4 * q : 4 * q + 4, :].bitcast(I32),
-            )
-        x_in = {}
+        style_b_pt = const.tile([P, PACK], BF16, name="style_b_pt")
         bias_in = const.tile([P, BLOCKS, 2], BF16, name="bias_in")
+        x_in = {}
         x_loads = [(0, 1), (1, 1)] + [(g, 2) for g in range(2, GROUPS, 2)]
 
         def load_x():
@@ -91,7 +78,19 @@ def tile_modulatemlp_pa_w8_kernel(
             for k in range(count):
                 x_in[first + k] = xt[:, k]
 
-        style_b_pt = const.tile([P, PACK], BF16, name="style_b_pt")
+        def load_weight(h):
+            nc.sync.dma_start(out=weight_in[h][:], in_=weight_rows[:, 2 * h : 2 * h + 2, :])
+
+        nc.sync.dma_start(out=w_codes_in[:], in_=w_bytes)
+        load_weight(0)
+        for q in range(4):
+            nc.sync.dma_start(
+                out=sw_scales[32 * q : 32 * q + 4, :].bitcast(I32),
+                in_=style_w_scales[0][4 * q : 4 * q + 4, :].bitcast(I32),
+            )
+        nc.sync.dma_start(out=sw_words[:], in_=style_w_words[0].rearrange("p n t -> p (n t)"))
+        nc.sync.dma_start(out=w_scale_pt[:], in_=w_scale.rearrange("o (p t) -> p (o t)", t=PACK))
+        load_weight(1)
         load_x()
         nc.sync.dma_start(out=style_b_pt[:], in_=style_b.rearrange("(p t) -> p t", t=PACK))
         load_x()
@@ -145,17 +144,26 @@ def tile_modulatemlp_pa_w8_kernel(
         bias_col = const.tile([P, BLOCKS], F32, name="bias_col")
         halves = [slice(0, O // 2), slice(O // 2, O)]
 
+        weight_bank = {}
+
         def turn_weight(h):
-            bank = psum.tile([P, 2, 2, P], F32, name="weight_bank", tag="sum", bufs=SUM_BANKS)
+            bank = weight_bank[h] = psum.tile([P, 2, 2, P], F32, name="weight_bank", tag="back0", bufs=2)
             for k in range(2):
                 turn_words(bank[:, k], weight_in[h][:, k, :])
+
+        def copy_weight(h):
+            bank = weight_bank[h]
             nc.scalar.copy(
                 out=weight_k_words[:, O * h : O * h + O].rearrange("p (b r u) -> p b r u", b=2, u=2),
                 in_=bank[:].rearrange("p b u r -> p b r u"),
             )
 
-        def square_weight(h):
-            nc.scalar.activation(weight2_k[:, halves[h], :], weight_k[:, halves[h], :], ACT.Square)
+        def square_weight(h, on_vector=False):
+            src, dst = weight_k[:, halves[h], :], weight2_k[:, halves[h], :]
+            if on_vector:
+                nc.vector.tensor_tensor(out=dst, in0=src, in1=src, op=ALU.mult)
+            else:
+                nc.scalar.activation(dst, src, ACT.Square)
 
         def quantise(pair, src, cols=slice(None)):
             nc.vector.quantize_mx(
@@ -165,7 +173,7 @@ def tile_modulatemlp_pa_w8_kernel(
         d_bank = {}
 
         def demod_sums(h):
-            d_bank[h] = psum.tile([P, 2, N], F32, name="d_bank", tag="sum", bufs=SUM_BANKS)
+            d_bank[h] = psum.tile([P, 2, N], F32, name="d_bank", tag="back1", bufs=2)
             for k in range(2):
                 mx_pass(d_bank[h][:, k, :], block(weight2_mx, 2 * h + k), [t[:] for t in style2_mx])
 
@@ -175,23 +183,41 @@ def tile_modulatemlp_pa_w8_kernel(
                 scale=1.0 / gain**2, bias=EPS / gain**2,
             )
 
-        x_bank, staging, x_mx, y_bank, s_tile, c_tile, relu4, back_bank, out_tile = {}, {}, {}, {}, {}, {}, {}, {}, {}
+        x_bank, x_words, x_mod, x_mx, y_bank, s_tile, copied, c_tile, relu4, back_bank, out_tile = ({} for k in range(11))
 
-        def turn_x(g):
-            x_bank[g] = psum.tile([P, 2, TILES, P], F32, name="x_bank", tag="turn", bufs=TURN_BANKS)
+        def turn_x(g, tag="turn"):
+            x_bank[g] = psum.tile([P, 2, TILES, P], F32, name="x_bank", tag=tag, bufs=2)
             for j in range(TILES):
                 turn_words(x_bank[g][:, :, j, :], x_in[g][:, j, :])
 
-        def modulate(g):
-            staging[g] = x_pool.tile([P, TILES * O], F32, name="staging", align_bytes=64, bufs=5)
+        def modulated(g):
+            if g not in x_mod:
+                tile = copied.get((g - SHARED_FROM, 0)) or s_pool.tile([P, O], F32, name="copied", align_bytes=64, bufs=8)
+                x_mod[g] = tile[:].bitcast(BF16)
+            return x_mod[g].rearrange("p (n l t) -> p n l t", l=L, t=PACK)
+
+        def modulate(g, count=SAMPLES - ON_GPSIMD):
             nc.vector.tensor_tensor(
-                out=staging[g][:, : 2 * TOKENS].bitcast(BF16).rearrange("p (n l u e) -> p n l u e", n=SAMPLES, u=2, e=2),
-                in0=x_bank.pop(g)[:].rearrange("p u j q -> p u (j q)").bitcast(BF16)
-                .rearrange("p u (n l e) -> p n l u e", n=SAMPLES, e=2),
-                in1=style_k[:, SAMPLES * g : SAMPLES * g + SAMPLES, :]
-                .rearrange("p n (u e) -> p n u e", u=2)
-                .unsqueeze(2)
-                .to_broadcast([P, SAMPLES, L, 2, 2]),
+                out=modulated(g)[:, :count].rearrange("p n l (u e) -> p n l u e", u=2),
+                in0=x_bank[g][:].rearrange("p u j q -> p u (j q)")[:, :, : L * count].bitcast(BF16)
+                .rearrange("p u (n l e) -> p n l u e", l=L, e=2),
+                in1=style_k[:, SAMPLES * g : SAMPLES * g + count, :]
+                .rearrange("p n (u e) -> p n u e", u=2).unsqueeze(2).to_broadcast([P, count, L, 2, 2]),
+                op=ALU.mult,
+            )
+
+        def copy_words(g):
+            x_words[g] = x_pool.tile([P, L * ON_GPSIMD, 2], F32, name="x_words", align_bytes=64)
+            words = x_bank[g][:].rearrange("p u j q -> p (j q) u")
+            nc.scalar.copy(out=x_words[g][:], in_=words[:, TOKENS - L * ON_GPSIMD :, :])
+
+        def modulate_words(g):
+            first = SAMPLES - ON_GPSIMD
+            nc.gpsimd.tensor_tensor(
+                out=modulated(g)[:, first:],
+                in0=x_words[g][:].rearrange("p q u -> p (q u)").bitcast(BF16).rearrange("p (n l t) -> p n l t", l=L, t=PACK),
+                in1=style_k[:, SAMPLES * g + first : SAMPLES * g + SAMPLES, :]
+                .unsqueeze(2).to_broadcast([P, ON_GPSIMD, L, PACK]),
                 op=ALU.mult,
             )
 
@@ -199,19 +225,19 @@ def tile_modulatemlp_pa_w8_kernel(
             codes = x_pool.tile([P, TOKENS], U32, name="x_codes", align_bytes=64)
             scales = x_pool.tile([P, TOKENS], U8, name="x_scales", align_bytes=64)
             nc.vector.quantize_mx(
-                out=codes[:].bitcast(X4), scales=scales[:], in_=staging[g][:, : 2 * TOKENS].bitcast(BF16)
+                out=codes[:].bitcast(X4), scales=scales[:], in_=x_mod[g]
             )
             x_mx[g] = (codes[:], scales[:])
 
-        def multiply(g, banks=(0, 1)):
+        def multiply(g, banks=(0, 1), tag=None):
             for h in banks:
-                y_bank[g, h] = psum.tile([P, 2, TOKENS], F32, name="y_bank", tag="y%d" % h, bufs=1)
+                y_bank[g, h] = psum.tile([P, 2, TOKENS], F32, name="y_bank", tag=tag or "y%d" % h, bufs=2 if tag else 1)
                 for k in range(2):
                     mx_pass(y_bank[g, h][:, k, :], block(weight_mx, 2 * h + k), x_mx[g])
 
         def scale_and_bias(g, h, on_vector=False):
             if g not in s_tile:
-                s_tile[g] = s_pool.tile([P, TILES, BLOCKS, P], F32, name="s_tile", bufs=4)
+                s_tile[g] = s_pool.tile([P, TILES, BLOCKS, P], F32, name="s_tile", bufs=5)
             for k in range(2):
                 b = 2 * h + k
                 for n in range(SAMPLES):
@@ -227,58 +253,60 @@ def tile_modulatemlp_pa_w8_kernel(
                     else:
                         nc.scalar.activation(dst, src, ACT.Identity, scale=coefficient, bias=bias_col[:, b : b + 1])
 
-        def clip(g, first=0, last=TILES):
-            src = s_tile[g][:].rearrange("p j b m -> p (j b m)")
-            if g not in c_tile:
-                c_tile[g] = staging[g + AHEAD][:] if g + AHEAD in staging else src
-            if clipped_on_the_way_out(g):
-                last = 1
-            cols = slice(O * first, O * last)
+        def s_of(g, j):
+            return s_tile[g][:, j].rearrange("p b m -> p (b m)")
+
+        def clip(g, first=0, last=None):
+            last = last or O + P * math.ceil(scalar_columns(g) / P)
+            part = s_tile[g][:].rearrange("p j b m -> p (j b m)")[:, first:last]
+            c_tile[g] = x_mod[g + LEAD].bitcast(F32) if g < RAMP else part
             nc.gpsimd.tensor_scalar(
-                out=c_tile[g][:, cols], in0=src[:, cols], scalar1=CLAMP / 5.0, scalar2=-CLAMP, op0=ALU.min, op1=ALU.max
+                out=c_tile[g], in0=part, scalar1=CLAMP / 5.0, scalar2=-CLAMP, op0=ALU.min, op1=ALU.max
             )
 
-        def to_turn_back(g, j):
-            if j == 1 and clipped_on_the_way_out(g):
-                return s_tile[g][:, j].rearrange("p b m -> p (b m)")
-            return c_tile[g][:, O * j : O * j + O]
+        def positive_part(g, j=1):
+            relu4[g, j] = s_pool.tile([P, O], F32, name="relu4", bufs=3)
+            nc.vector.tensor_scalar(out=relu4[g, j][:], in0=s_of(g, j), scalar1=0.0, scalar2=4.0, op0=ALU.max, op1=ALU.mult)
 
-        def positive_part(g):
-            if summed(g, 1):
-                relu4[g] = s_pool.tile([P, O], F32, name="relu4", bufs=3)
-                nc.vector.tensor_scalar(
-                    out=relu4[g][:], in0=to_turn_back(g, 1), scalar1=0.0, scalar2=4.0, op0=ALU.max, op1=ALU.mult
-                )
+        def leaky_relu_in_place(g, j):
+            nc.vector.scalar_tensor_tensor(
+                out=s_of(g, j), in0=s_of(g, j), scalar=5.0, in1=s_of(g, j), op0=ALU.mult, op1=ALU.max
+            )
 
-        def turn_back(g, j, in_turn_bank=False):
-            tag, bufs = ("turn", TURN_BANKS) if in_turn_bank else ("sum", SUM_BANKS)
-            back_bank[g, j] = psum.tile([P, O], F32, name="back_bank", tag=tag, bufs=bufs)
+        def turn_back(g, j, tag=None):
+            back_bank[g, j] = psum.tile([P, O], F32, name="back_bank", tag=tag or "back%d" % j, bufs=1 if tag in ("y0", "y1") else 2)
             for b in range(BLOCKS):
-                dst = back_bank[g, j][:, P * b : P * b + P]
-                src = to_turn_back(g, j)[:, P * b : P * b + P]
-                if summed(g, j):
-                    nc.tensor.matmul(dst, lhsT=src, rhs=ident[:], start=True, stop=False, is_transpose=True)
-                    nc.tensor.matmul(
-                        dst, lhsT=relu4[g][:, P * b : P * b + P], rhs=ident[:], start=False, stop=True, is_transpose=True
-                    )
+                cols = slice(P * b, P * b + P)
+                dst = back_bank[g, j][:, cols]
+                if (g, j) in relu4:
+                    nc.tensor.matmul(dst, lhsT=s_of(g, j)[:, cols], rhs=ident[:], start=True, stop=False, is_transpose=True)
+                    nc.tensor.matmul(dst, lhsT=relu4[g, j][:, cols], rhs=ident[:], start=False, stop=True, is_transpose=True)
                 else:
-                    nc.tensor.transpose(dst, src, ident[:])
+                    nc.tensor.transpose(dst, (c_tile[g] if g < RAMP else s_of(g, j))[:, cols], ident[:])
 
-        def copy_out(g, j, on_vector=False):
+        def out_of(g, j):
             if g not in out_tile:
                 out_tile[g] = out_pool.tile([P, TILES, O], F32, name="out_tile")
-            dst, src = out_tile[g][:, j, :], back_bank[g, j][:]
-            if j == 1 and clipped_on_the_way_out(g):
-                nc.vector.tensor_scalar(out=dst, in0=src, scalar1=CLAMP, scalar2=-CLAMP, op0=ALU.min, op1=ALU.max)
-            elif on_vector:
-                nc.vector.tensor_copy(out=dst, in_=src)
-            else:
-                nc.scalar.copy(out=dst, in_=src)
+            return out_tile[g][:, j, :]
 
-        def leaky_relu(g, j):
+        def copy_back(g, j=0):
+            copied[g, j] = s_pool.tile([P, O], F32, name="copied", align_bytes=64, bufs=8)
+            nc.scalar.copy(out=copied[g, j][:], in_=back_bank[g, j][:])
+
+        def copy_out(g, j=1):
+            split = scalar_columns(g)
+            if split:
+                nc.scalar.copy(out=out_of(g, j)[:, :split], in_=back_bank[g, j][:, :split])
+
+        def clip_out(g, j=1):
+            split = scalar_columns(g)
+            nc.vector.tensor_scalar(
+                out=out_of(g, j)[:, split:], in0=back_bank[g, j][:, split:], scalar1=CLAMP, scalar2=-CLAMP, op0=ALU.min, op1=ALU.max
+            )
+
+        def leaky_relu(g, j=0):
             nc.vector.scalar_tensor_tensor(
-                out=out_tile[g][:, j, :], in0=back_bank[g, j][:], scalar=5.0, in1=out_tile[g][:, j, :],
-                op0=ALU.mult, op1=ALU.max,
+                out=out_of(g, j), in0=back_bank[g, j][:], scalar=5.0, in1=copied[g, j][:], op0=ALU.mult, op1=ALU.max
             )
 
         def store_group(g):
@@ -290,136 +318,161 @@ def tile_modulatemlp_pa_w8_kernel(
             nc.sync.dma_start(out=out_groups[g][:, j, :], in_=out_tile[g][:, j, :])
 
         w_wide = const.tile([P, WD], BF16, name="w_wide", align_bytes=64)
-        nc.vector.tensor_copy(out=w_wide[:], in_=w_codes_in[:].bitcast(F8))
-        w_bank = psum.tile([P, 2, P], F32, name="w_bank", tag="turn", bufs=TURN_BANKS)
-        turn_words(w_bank, w_wide[:])
-        turn_weight(0)
-        turn_weight(1)
         sw_words_tm = const.tile([P, C], I32, name="sw_words_tm", align_bytes=64)
-        nc.vector.tensor_copy(
-            out=sw_words_tm[:].rearrange("p (t m) -> p t m", t=PACK),
-            in_=sw_words[:].bitcast(I32).rearrange("p (m t) -> p t m", t=PACK),
-        )
-        w_k = const.tile([P, N, PACK], BF16, name="w_k", align_bytes=64)
-        nc.vector.tensor_tensor(
-            out=w_k[:].rearrange("p n (u e) -> p n u e", u=2),
-            in0=w_bank[:].bitcast(BF16).rearrange("p u (n e) -> p n u e", e=2),
-            in1=w_scale_pt[:].rearrange("p (u e) -> p u e", u=2).unsqueeze(1).to_broadcast([P, N, 2, 2]),
-            op=ALU.mult,
-        )
         sw_scales_tm = const.tile([P, C], U8, name="sw_scales_tm", align_bytes=64)
-        nc.vector.tensor_copy(
-            out=sw_scales_tm[:].rearrange("p (t m) -> p t m", t=PACK),
-            in_=sw_scales[:].rearrange("p (m t) -> p t m", t=PACK),
-        )
+        w_k = const.tile([P, N, PACK], BF16, name="w_k", align_bytes=64)
         w_mx = (
             const.tile([P, N], U32, name="w_codes", align_bytes=64),
             const.tile([P, N], U8, name="w_scales", align_bytes=64),
         )
-        quantise(w_mx, w_k)
+        w_bank = psum.tile([P, 2, P], F32, name="w_bank", tag="y1", bufs=1)
         style_bank = psum.tile([P, PACK, N], F32, name="style_bank", tag="y0", bufs=1)
-        for t in range(PACK):
-            mx_pass(style_bank[:, t, :], block((sw_words_tm, sw_scales_tm), t), [tile[:] for tile in w_mx])
 
-        square_weight(0)
-        quantise(weight_mx, weight_k, halves[0])
-        nc.vector.scalar_tensor_tensor(
-            out=style_k[:], in0=style_bank[:].rearrange("p t n -> p n t"), scalar=1.0 / math.sqrt(WD),
-            in1=style_b_pt[:].unsqueeze(1).to_broadcast([P, N, PACK]), op0=ALU.mult, op1=ALU.add,
-        )
-        turn_x(0)
-        nc.scalar.activation(style2_k[:], style_k[:], ACT.Square)
-        turn_x(1)
+        def reorder(dst, src):
+            nc.vector.tensor_copy(
+                out=dst.rearrange("p (t m) -> p t m", t=PACK), in_=src.rearrange("p (m t) -> p t m", t=PACK)
+            )
+
+        def scale_w():
+            nc.vector.tensor_tensor(
+                out=w_k[:].rearrange("p n (u e) -> p n u e", u=2),
+                in0=w_bank[:].bitcast(BF16).rearrange("p u (n e) -> p n u e", e=2),
+                in1=w_scale_pt[:].rearrange("p (u e) -> p u e", u=2).unsqueeze(1).to_broadcast([P, N, 2, 2]),
+                op=ALU.mult,
+            )
+
+        def style_sums():
+            for t in range(PACK):
+                mx_pass(style_bank[:, t, :], block((sw_words_tm, sw_scales_tm), t), [tile[:] for tile in w_mx])
+
+        def finish_style():
+            nc.vector.scalar_tensor_tensor(
+                out=style_k[:], in0=style_bank[:].rearrange("p t n -> p n t"), scalar=1.0 / math.sqrt(WD),
+                in1=style_b_pt[:].unsqueeze(1).to_broadcast([P, N, PACK]), op0=ALU.mult, op1=ALU.add,
+            )
+
+        nc.vector.tensor_copy(out=w_wide[:], in_=w_codes_in[:].bitcast(F8))
+        turn_words(w_bank, w_wide[:])
+        turn_weight(0)
+        copy_weight(0)
+        turn_weight(1)
+        copy_weight(1)
+        reorder(sw_scales_tm[:], sw_scales[:])
+        scale_w()
+        reorder(sw_words_tm[:], sw_words[:].bitcast(I32))
+        quantise(w_mx, w_k)
+        style_sums()
+        square_weight(0, on_vector=True)
         square_weight(1)
+        quantise(weight_mx, weight_k, halves[0])
+        finish_style()
+        turn_x(0)
+        turn_x(1)
+        turn_x(2, "back0")
+        nc.scalar.activation(style2_k[:], style_k[:], ACT.Square)
         nc.scalar.activation(bias_col[:], bias_in[:, :, 0], ACT.Copy, scale=gain)
-        quantise(weight_mx, weight_k, halves[1])
-        modulate(0)
-        quantise(style2_mx, style2_k)
         quantise(weight2_mx, weight2_k, halves[0])
-        turn_x(2)
+        modulate(0, SAMPLES)
+        quantise(style2_mx, style2_k)
+        quantise(weight_mx, weight_k, halves[1])
+        quantise_x(0)
+        turn_x(3, "back0")
         demod_sums(0)
         demod_coefficients(0)
-        quantise_x(0)
         multiply(0, (0,))
-        multiply(0, (1,))
-        modulate(1)
+        modulate(1, SAMPLES)
         quantise(weight2_mx, weight2_k, halves[1])
+        multiply(0, (1,))
         demod_sums(1)
         scale_and_bias(0, 0)
         demod_coefficients(1)
-        turn_x(3)
-        quantise_x(1)
-        modulate(2)
         scale_and_bias(0, 1)
-        quantise_x(2)
+        quantise_x(1)
+        modulate(2, SAMPLES)
+        turn_x(4)
+        for g in range(3, LEAD + 1):
+            modulate(g, SAMPLES)
+            quantise_x(g - 1)
+            if g + 2 <= LEAD + 1:
+                turn_x(g + 2)
 
-        steps = GROUPS - AHEAD
+        steps = GROUPS - LEAD
         for i in range(1, steps):
-            clip(i - 1)
-            multiply(i)
+            x = i + LEAD
+            multiply(i, tag="back1" if i == 1 else None)
+            if 2 <= i <= RAMP:
+                positive_part(i - 2)
+            if x - 1 < GROUPS:
+                quantise_x(x - 1)
+            if i > RAMP:
+                positive_part(i - 2)
+            if SHARED_FROM <= x < GROUPS:
+                modulate_words(x)
+            if i + 1 < steps:
+                clip(i - 1)
             if i >= 2:
                 turn_back(i - 2, 0)
-            if i + AHEAD + 1 < GROUPS:
-                turn_x(i + AHEAD + 1)
+            if i >= 3:
+                clip_out(i - 3)
+            if x < GROUPS:
+                modulate(x, SAMPLES - ON_GPSIMD if x >= SHARED_FROM else SAMPLES)
+            if x + 1 < GROUPS and x + 1 not in x_bank:
+                turn_x(x + 1)
             if i >= 2:
                 turn_back(i - 2, 1)
             scale_and_bias(i, 0)
-            modulate(i + AHEAD)
-            if i >= 3 and vector_empties(i - 3):
-                copy_out(i - 3, 1, on_vector=True)
             scale_and_bias(i, 1)
             if i >= 2:
-                copy_out(i - 2, 0)
-                if i + 1 < steps and not vector_empties(i - 2):
-                    copy_out(i - 2, 1)
+                copy_back(i - 2)
+            if SHARED_FROM <= x + 1 < GROUPS:
+                copy_words(x + 1)
+            if i >= 2:
+                copy_out(i - 2)
             if i >= 3:
-                leaky_relu(i - 3, 0)
+                leaky_relu(i - 3)
                 store_group(i - 3)
-            if i >= 3:
-                quantise_x(i + AHEAD)
-                positive_part(i - 1)
-            else:
-                positive_part(i - 1)
-                quantise_x(i + AHEAD)
 
-        g0, g1, g2, g3, g4 = range(GROUPS - 5, GROUPS)
-        clip(g2)
+        g0, g1, g2, g3, g4, g5 = range(GROUPS - 6, GROUPS)
         multiply(g3)
-        turn_back(g1, 0)
+        quantise_x(g5)
+        positive_part(g1)
+        multiply(g4, tag="turn")
         turn_back(g1, 1)
         scale_and_bias(g3, 0)
         scale_and_bias(g3, 1)
-        leaky_relu(g0, 0)
-        store_tile(g0, 0)
-        copy_out(g0, 1, on_vector=True)
-        store_tile(g0, 1)
-        multiply(g4)
-        clip(g3)
-        turn_back(g2, 1, in_turn_bank=True)
-        turn_back(g2, 0, in_turn_bank=True)
-        copy_out(g1, 0)
-        copy_out(g1, 1, on_vector=True)
-        store_tile(g1, 1)
+        leaky_relu_in_place(g1, 0)
+        positive_part(g2)
+        leaky_relu_in_place(g2, 0)
+        clip(g3, 0, 2 * O)
+        leaky_relu(g0)
+        clip_out(g0)
+        store_group(g0)
+        multiply(g5)
+        turn_back(g1, 0)
         scale_and_bias(g4, 0)
-        scale_and_bias(g4, 1, on_vector=True)
-        for j in range(TILES):
-            clip(g4, j, j + 1)
-        leaky_relu(g1, 0)
-        store_tile(g1, 0)
-        copy_out(g2, 1)
-        turn_back(g3, 0)
-        turn_back(g3, 1)
-        leaky_relu(g2, 1)
-        store_tile(g2, 1)
-        copy_out(g2, 0)
-        leaky_relu(g2, 0)
+        scale_and_bias(g4, 1)
+        clip(g4, 0, 2 * O)
+        turn_back(g2, 0)
+        turn_back(g2, 1)
+        clip_out(g1, 1)
+        clip_out(g1, 0)
+        store_group(g1)
+        scale_and_bias(g5, 0)
+        scale_and_bias(g5, 1)
+        clip(g5, 0, O)
+        clip(g5, O, 2 * O)
+        turn_back(g3, 0, "turn")
+        turn_back(g3, 1, "turn")
+        clip_out(g2, 0)
         store_tile(g2, 0)
-        copy_out(g3, 0)
+        clip_out(g2, 1)
+        store_tile(g2, 1)
         turn_back(g4, 0)
         turn_back(g4, 1)
-        remaining = [(g3, 0), (g3, 1), (g4, 0), (g4, 1)]
-        for k, (g, j) in enumerate(remaining):
-            if k + 1 < len(remaining):
-                copy_out(*remaining[k + 1])
-            leaky_relu(g, j)
-            store_tile(g, j)
+        turn_back(g5, 0, "y0")
+        turn_back(g5, 1, "y1")
+        for g in (g3, g4, g5):
+            for j in range(TILES):
+                copy_back(g, j)
+                leaky_relu(g, j)
+                store_tile(g, j)

@@ -90,8 +90,8 @@ def tile_modulatemlp_pa_w8_kernel(
             )
         nc.sync.dma_start(out=sw_words[:], in_=style_w_words[0].rearrange("p n t -> p (n t)"))
         nc.sync.dma_start(out=w_scale_pt[:], in_=w_scale.rearrange("o (p t) -> p (o t)", t=PACK))
-        load_weight(1)
         load_x()
+        load_weight(1)
         nc.sync.dma_start(out=style_b_pt[:], in_=style_b.rearrange("(p t) -> p t", t=PACK))
         load_x()
         with nc.allow_non_contiguous_dma(reason="one bias value a partition and block"):
@@ -190,9 +190,12 @@ def tile_modulatemlp_pa_w8_kernel(
             for j in range(TILES):
                 turn_words(x_bank[g][:, :, j, :], x_in[g][:, j, :])
 
+        x_tile = {}
+
         def modulated(g):
             if g not in x_mod:
-                tile = copied.get((g - SHARED_FROM, 0)) or s_pool.tile([P, O], F32, name="copied", align_bytes=64, bufs=8)
+                tile = copied.get((g - SHARED_FROM, 0)) or (x_tile[1] if g == 3 else None) or s_pool.tile([P, O], F32, name="copied", align_bytes=64, bufs=8)
+                x_tile[g] = tile
                 x_mod[g] = tile[:].bitcast(BF16)
             return x_mod[g].rearrange("p (n l t) -> p n l t", l=L, t=PACK)
 
@@ -345,56 +348,56 @@ def tile_modulatemlp_pa_w8_kernel(
             for t in range(PACK):
                 mx_pass(style_bank[:, t, :], block((sw_words_tm, sw_scales_tm), t), [tile[:] for tile in w_mx])
 
-        def finish_style():
+        def finish_style(first, last):
             nc.vector.scalar_tensor_tensor(
-                out=style_k[:], in0=style_bank[:].rearrange("p t n -> p n t"), scalar=1.0 / math.sqrt(WD),
-                in1=style_b_pt[:].unsqueeze(1).to_broadcast([P, N, PACK]), op0=ALU.mult, op1=ALU.add,
+                out=style_k[:, first:last], in0=style_bank[:, :, first:last].rearrange("p t n -> p n t"), scalar=1.0 / math.sqrt(WD),
+                in1=style_b_pt[:].unsqueeze(1).to_broadcast([P, last - first, PACK]), op0=ALU.mult, op1=ALU.add,
             )
 
         nc.vector.tensor_copy(out=w_wide[:], in_=w_codes_in[:].bitcast(F8))
         turn_words(w_bank, w_wide[:])
         turn_weight(0)
         copy_weight(0)
-        turn_weight(1)
-        copy_weight(1)
         reorder(sw_scales_tm[:], sw_scales[:])
         scale_w()
         reorder(sw_words_tm[:], sw_words[:].bitcast(I32))
         quantise(w_mx, w_k)
         style_sums()
-        square_weight(0, on_vector=True)
-        square_weight(1)
-        quantise(weight_mx, weight_k, halves[0])
-        finish_style()
         turn_x(0)
+        turn_weight(1)
+        square_weight(0, on_vector=True)
+        quantise(weight_mx, weight_k, halves[0])
+        finish_style(0, 2 * SAMPLES)
+        finish_style(2 * SAMPLES, N)
         turn_x(1)
         turn_x(2, "back0")
         nc.scalar.activation(style2_k[:], style_k[:], ACT.Square)
+        copy_weight(1)
+        square_weight(1)
         nc.scalar.activation(bias_col[:], bias_in[:, :, 0], ACT.Copy, scale=gain)
-        quantise(weight2_mx, weight2_k, halves[0])
         modulate(0, SAMPLES)
+        quantise(weight2_mx, weight2_k, halves[0])
         quantise(style2_mx, style2_k)
-        quantise(weight_mx, weight_k, halves[1])
         quantise_x(0)
-        turn_x(3, "back0")
+        quantise(weight_mx, weight_k, halves[1])
         demod_sums(0)
         demod_coefficients(0)
         multiply(0, (0,))
         modulate(1, SAMPLES)
         quantise(weight2_mx, weight2_k, halves[1])
         multiply(0, (1,))
+        turn_x(3, "back0")
         demod_sums(1)
         scale_and_bias(0, 0)
+        copy_words(3)
         demod_coefficients(1)
         scale_and_bias(0, 1)
         quantise_x(1)
+        modulate_words(3)
         modulate(2, SAMPLES)
         turn_x(4)
-        for g in range(3, LEAD + 1):
-            modulate(g, SAMPLES)
-            quantise_x(g - 1)
-            if g + 2 <= LEAD + 1:
-                turn_x(g + 2)
+        modulate(3)
+        quantise_x(2)
 
         steps = GROUPS - LEAD
         for i in range(1, steps):
@@ -408,8 +411,9 @@ def tile_modulatemlp_pa_w8_kernel(
                 positive_part(i - 2)
             if SHARED_FROM <= x < GROUPS:
                 modulate_words(x)
-            if i + 1 < steps:
-                clip(i - 1)
+            clip(i - 1)
+            if x + 1 < GROUPS and x + 1 not in x_bank:
+                turn_x(x + 1)
             if i >= 2:
                 turn_back(i - 2, 0)
             if i >= 3:
@@ -440,31 +444,33 @@ def tile_modulatemlp_pa_w8_kernel(
         turn_back(g1, 1)
         scale_and_bias(g3, 0)
         scale_and_bias(g3, 1)
-        leaky_relu_in_place(g1, 0)
         positive_part(g2)
         leaky_relu_in_place(g2, 0)
         clip(g3, 0, 2 * O)
         leaky_relu(g0)
+        store_tile(g0, 0)
         clip_out(g0)
-        store_group(g0)
+        store_tile(g0, 1)
         multiply(g5)
         turn_back(g1, 0)
         scale_and_bias(g4, 0)
         scale_and_bias(g4, 1)
+        copy_back(g1)
         clip(g4, 0, 2 * O)
         turn_back(g2, 0)
         turn_back(g2, 1)
         clip_out(g1, 1)
-        clip_out(g1, 0)
-        store_group(g1)
+        store_tile(g1, 1)
         scale_and_bias(g5, 0)
-        scale_and_bias(g5, 1)
-        clip(g5, 0, O)
-        clip(g5, O, 2 * O)
         turn_back(g3, 0, "turn")
         turn_back(g3, 1, "turn")
+        scale_and_bias(g5, 1, on_vector=True)
+        clip(g5, 0, O)
+        clip(g5, O, 2 * O)
         clip_out(g2, 0)
         store_tile(g2, 0)
+        leaky_relu(g1)
+        store_tile(g1, 0)
         clip_out(g2, 1)
         store_tile(g2, 1)
         turn_back(g4, 0)

@@ -412,8 +412,6 @@ def tile_modulatemlp_pa_w8_kernel(
             if SHARED_FROM <= x < GROUPS:
                 modulate_words(x)
             clip(i - 1)
-            if x + 1 < GROUPS and x + 1 not in x_bank:
-                turn_x(x + 1)
             if i >= 2:
                 turn_back(i - 2, 0)
             if i >= 3:

@@ -53,7 +53,7 @@ def tile_modulatemlp_pa_w8_kernel(
         const = ctx.enter_context(tc.tile_pool(name="const", bufs=1))
         x_pool = ctx.enter_context(tc.tile_pool(name="x_pool", bufs=LEAD + 2))
         s_pool = ctx.enter_context(tc.tile_pool(name="s_pool", bufs=3))
-        out_pool = ctx.enter_context(tc.tile_pool(name="out_pool", bufs=5))
+        out_pool = ctx.enter_context(tc.tile_pool(name="out_pool", bufs=26))
         psum = ctx.enter_context(tc.psum_pool(name="psum", bufs=1))
         ctx.enter_context(tc.manual_schedule())
 
@@ -73,7 +73,7 @@ def tile_modulatemlp_pa_w8_kernel(
 
         def load_x():
             first, count = x_loads.pop(0)
-            xt = const.tile([P, count, TILES, C], BF16, name="x%d" % first, align_bytes=64)
+            xt = x_pool.tile([P, count, TILES, C], BF16, name="x_in%d" % count, align_bytes=64, bufs=PRELOAD + 1 if count == 2 else 2)
             nc.sync.dma_start(out=xt[:], in_=x_groups[first : first + count].rearrange("g p j c -> p g j c"))
             for k in range(count):
                 x_in[first + k] = xt[:, k]
@@ -190,13 +190,17 @@ def tile_modulatemlp_pa_w8_kernel(
             for j in range(TILES):
                 turn_words(x_bank[g][:, :, j, :], x_in[g][:, j, :])
 
-        x_tile = {}
+        x_tile, stage = {}, {}
+        ahead = O - O * ON_GPSIMD // SAMPLES
+
+        def new_stage():
+            return s_pool.tile([P, ahead + O], F32, name="stage", align_bytes=64, bufs=9)
 
         def modulated(g):
             if g not in x_mod:
-                tile = copied.get((g - SHARED_FROM, 0)) or (x_tile[1] if g == 3 else None) or s_pool.tile([P, O], F32, name="copied", align_bytes=64, bufs=8)
+                tile = stage.get(g - SHARED_FROM) or (x_tile[1] if g == 3 else None) or new_stage()
                 x_tile[g] = tile
-                x_mod[g] = tile[:].bitcast(BF16)
+                x_mod[g] = tile[:, :O].bitcast(BF16)
             return x_mod[g].rearrange("p (n l t) -> p n l t", l=L, t=PACK)
 
         def modulate(g, count=SAMPLES - ON_GPSIMD):
@@ -293,8 +297,9 @@ def tile_modulatemlp_pa_w8_kernel(
             return out_tile[g][:, j, :]
 
         def copy_back(g, j=0):
-            copied[g, j] = s_pool.tile([P, O], F32, name="copied", align_bytes=64, bufs=8)
-            nc.scalar.copy(out=copied[g, j][:], in_=back_bank[g, j][:])
+            stage[g] = new_stage()
+            copied[g, j] = stage[g][:, ahead:]
+            nc.scalar.copy(out=copied[g, j], in_=back_bank[g, j][:])
 
         def copy_out(g, j=1):
             split = scalar_columns(g)
@@ -309,7 +314,7 @@ def tile_modulatemlp_pa_w8_kernel(
 
         def leaky_relu(g, j=0):
             nc.vector.scalar_tensor_tensor(
-                out=out_of(g, j), in0=back_bank[g, j][:], scalar=5.0, in1=copied[g, j][:], op0=ALU.mult, op1=ALU.max
+                out=out_of(g, j), in0=back_bank[g, j][:], scalar=5.0, in1=copied[g, j], op0=ALU.mult, op1=ALU.max
             )
 
         def store_group(g):
@@ -405,8 +410,8 @@ def tile_modulatemlp_pa_w8_kernel(
             multiply(i, tag="back1" if i == 1 else None)
             if 2 <= i <= RAMP:
                 positive_part(i - 2)
-            if x - 1 < GROUPS:
-                quantise_x(x - 1)
+            if i != RAMP + 1:
+                quantise_x(x - 1 if i <= RAMP else x - 2)
             if i > RAMP:
                 positive_part(i - 2)
             if SHARED_FROM <= x < GROUPS:
@@ -414,20 +419,20 @@ def tile_modulatemlp_pa_w8_kernel(
             clip(i - 1)
             if i >= 2:
                 turn_back(i - 2, 0)
-            if i >= 3:
-                clip_out(i - 3)
             if x < GROUPS:
                 modulate(x, SAMPLES - ON_GPSIMD if x >= SHARED_FROM else SAMPLES)
+            if i >= 3:
+                clip_out(i - 3)
             if x + 1 < GROUPS and x + 1 not in x_bank:
                 turn_x(x + 1)
             if i >= 2:
                 turn_back(i - 2, 1)
             scale_and_bias(i, 0)
             scale_and_bias(i, 1)
-            if i >= 2:
-                copy_back(i - 2)
             if SHARED_FROM <= x + 1 < GROUPS:
                 copy_words(x + 1)
+            if i >= 2:
+                copy_back(i - 2)
             if i >= 2:
                 copy_out(i - 2)
             if i >= 3:
@@ -436,6 +441,7 @@ def tile_modulatemlp_pa_w8_kernel(
 
         g0, g1, g2, g3, g4, g5 = range(GROUPS - 6, GROUPS)
         multiply(g3)
+        quantise_x(g4)
         quantise_x(g5)
         positive_part(g1)
         multiply(g4, tag="turn")

@@ -59,8 +59,8 @@ def tile_modulatemlp_pa_w8_kernel(
 
         sw_scales = const.tile([P, C], U8, name="sw_scales", align_bytes=64)
         nc.vector.memset(sw_scales[:].bitcast(U32), 0)
-        one = const.tile([P, 1], F32, name="one")
-        nc.vector.memset(one[:], 1.0)
+        ones = const.tile([P, 3 * P], F32, name="ones")
+        nc.vector.memset(ones[:], 1.0)
         w_codes_in = const.tile([P, WD], U8, name="w_codes_in", align_bytes=64)
         w_scale_pt = const.tile([P, PACK], F32, name="w_scale_pt")
         weight_rows = weight.rearrange("(b m) c -> m b c", b=BLOCKS)
@@ -100,7 +100,7 @@ def tile_modulatemlp_pa_w8_kernel(
             load_x()
 
         warm = const.tile([P, 1], F32, name="warm")
-        nc.scalar.activation(warm[:], one[:], ACT.Abs_reciprocal_sqrt)
+        nc.scalar.activation(warm[:], ones[:, :1], ACT.Abs_reciprocal_sqrt)
         ident = const.tile([P, P], F32, name="ident")
         make_identity(nc, ident[:])
 
@@ -336,6 +336,10 @@ def tile_modulatemlp_pa_w8_kernel(
         w_bank = psum.tile([P, 2, P], F32, name="w_bank", tag="y1", bufs=1)
         style_bank = psum.tile([P, PACK, N], F32, name="style_bank", tag="y0", bufs=1)
 
+        def warm_up(width):
+            bank = psum.tile([P, O], F32, name="warm_bank", tag="back1", bufs=2)
+            nc.tensor.matmul(bank[:, :width], lhsT=ones[:, :P], rhs=ones[:, :width], start=True, stop=True)
+
         def reorder(dst, src):
             nc.vector.tensor_copy(
                 out=dst.rearrange("p (t m) -> p t m", t=PACK), in_=src.rearrange("p (m t) -> p t m", t=PACK)
@@ -359,9 +363,11 @@ def tile_modulatemlp_pa_w8_kernel(
                 in1=style_b_pt[:].unsqueeze(1).to_broadcast([P, last - first, PACK]), op0=ALU.mult, op1=ALU.add,
             )
 
+        warm_up(384)
         nc.vector.tensor_copy(out=w_wide[:], in_=w_codes_in[:].bitcast(F8))
         turn_words(w_bank, w_wide[:])
         turn_weight(0)
+        warm_up(384)
         copy_weight(0)
         reorder(sw_scales_tm[:], sw_scales[:])
         scale_w()
@@ -374,6 +380,7 @@ def tile_modulatemlp_pa_w8_kernel(
         quantise(weight_mx, weight_k, halves[0])
         finish_style(0, 2 * SAMPLES)
         finish_style(2 * SAMPLES, N)
+        warm_up(256)
         turn_x(1)
         turn_x(2, "back0")
         nc.scalar.activation(style2_k[:], style_k[:], ACT.Square)

@@ -376,7 +376,7 @@ def tile_modulatemlp_pa_w8_kernel(
         style_sums()
         turn_x(0)
         turn_weight(1)
-        square_weight(0, on_vector=True)
+        square_weight(0)
         quantise(weight_mx, weight_k, halves[0])
         finish_style(0, 2 * SAMPLES)
         finish_style(2 * SAMPLES, N)
@@ -424,10 +424,12 @@ def tile_modulatemlp_pa_w8_kernel(
             if SHARED_FROM <= x < GROUPS:
                 modulate_words(x)
             clip(i - 1)
+            if x == SHARED_FROM - 1:
+                modulate_words(x)
             if i >= 2:
                 turn_back(i - 2, 0)
             if x < GROUPS:
-                modulate(x, SAMPLES - ON_GPSIMD if x >= SHARED_FROM else SAMPLES)
+                modulate(x, SAMPLES - ON_GPSIMD if x >= SHARED_FROM - 1 else SAMPLES)
             if i >= 3:
                 clip_out(i - 3)
             if x + 1 < GROUPS and x + 1 not in x_bank:
@@ -436,7 +438,7 @@ def tile_modulatemlp_pa_w8_kernel(
                 turn_back(i - 2, 1)
             scale_and_bias(i, 0)
             scale_and_bias(i, 1)
-            if SHARED_FROM <= x + 1 < GROUPS:
+            if SHARED_FROM - 1 <= x + 1 < GROUPS:
                 copy_words(x + 1)
             if i >= 2:
                 copy_back(i - 2)

@@ -32,7 +32,7 @@ RAMP = 3
 SHARED_FROM = LEAD + 4
 TAIL = 3
 ALONE = 1
-SPLIT = 192
+SPLIT = 208
 PRELOAD = 5
 TURN_BANKS = 2
 
@@ -426,13 +426,17 @@ def tile_modulatemlp_pa_w8_kernel(
             clip(i - 1)
             if x == SHARED_FROM - 1:
                 modulate_words(x)
+            if i == 2:
+                turn_x(6, "back1")
             if i >= 2:
                 turn_back(i - 2, 0)
             if x < GROUPS:
                 modulate(x, SAMPLES - ON_GPSIMD if x >= SHARED_FROM - 1 else SAMPLES)
             if i >= 3:
                 clip_out(i - 3)
-            if x + 1 < GROUPS and x + 1 not in x_bank:
+            if i in (2, 3):
+                turn_x(x + 2)
+            elif x + 1 < GROUPS and x + 1 not in x_bank:
                 turn_x(x + 1)
             if i >= 2:
                 turn_back(i - 2, 1)

@@ -32,7 +32,7 @@ RAMP = 3
 SHARED_FROM = LEAD + 4
 TAIL = 3
 ALONE = 1
-SPLIT = 208
+SPLIT = 192
 PRELOAD = 5
 TURN_BANKS = 2
 

from contextlib import ExitStack
import math

import concourse.mybir as mybir
from concourse.masks import make_identity

F32 = mybir.dt.float32
BF16 = mybir.dt.bfloat16
U32 = mybir.dt.uint32
I32 = mybir.dt.int32
U8 = mybir.dt.uint8
F8 = mybir.dt.float8_e4m3fn
X4 = mybir.dt.float8_e4m3fn_x4
ALU = mybir.AluOpType
ACT = mybir.ActivationFunctionType

N, L, WD, C, O = 128, 64, 512, 512, 512
P = 128
PACK = 4
TILES = 2
TOKENS = P * TILES
GROUPS = N * L // TOKENS
SAMPLES = TOKENS // L
BLOCKS = O // P
EPS = 1e-8
CLAMP = 256.0
FLOPS = 2 * N * L * C * O + 2 * N * WD * C + 2 * N * C * O

ON_GPSIMD = 1
LEAD = 3
RAMP = 3
SHARED_FROM = LEAD + 4
TAIL = 3
ALONE = 1
SPLIT = 192
PRELOAD = 5
TURN_BANKS = 2


def scalar_columns(g):
    return SPLIT if RAMP <= g < GROUPS - 5 else 0


def tile_modulatemlp_pa_w8_kernel(
    tc, x, w_bytes, w_scale, weight, style_w_words, style_w_scales, style_b, bias, out
):
    nc = tc.nc
    gain = 0.2 * math.sqrt(2.0)
    x_groups = x.rearrange("n l c -> (n l) c").rearrange("(g j p) c -> g p j c", p=P, j=TILES)
    out_groups = out.rearrange("n l c -> (n l) c").rearrange("(g j p) c -> g p j c", p=P, j=TILES)

    with ExitStack() as ctx:
        const = ctx.enter_context(tc.tile_pool(name="const", bufs=1))
        x_pool = ctx.enter_context(tc.tile_pool(name="x_pool", bufs=LEAD + 2))
        s_pool = ctx.enter_context(tc.tile_pool(name="s_pool", bufs=3))
        out_pool = ctx.enter_context(tc.tile_pool(name="out_pool", bufs=26))
        psum = ctx.enter_context(tc.psum_pool(name="psum", bufs=1))
        ctx.enter_context(tc.manual_schedule())

        sw_scales = const.tile([P, C], U8, name="sw_scales", align_bytes=64)
        nc.vector.memset(sw_scales[:].bitcast(U32), 0)
        ones = const.tile([P, 3 * P], F32, name="ones")
        nc.vector.memset(ones[:], 1.0)
        w_codes_in = const.tile([P, WD], U8, name="w_codes_in", align_bytes=64)
        w_scale_pt = const.tile([P, PACK], F32, name="w_scale_pt")
        weight_rows = weight.rearrange("(b m) c -> m b c", b=BLOCKS)
        weight_in = [const.tile([P, 2, C], BF16, name="weight_in%d" % h, align_bytes=64) for h in range(2)]
        sw_words = const.tile([P, PACK * C], U8, name="sw_words", align_bytes=64)
        style_b_pt = const.tile([P, PACK], BF16, name="style_b_pt")
        bias_in = const.tile([P, BLOCKS, 2], BF16, name="bias_in")
        x_in = {}
        x_loads = [(0, 1), (1, 1)] + [(g, 2) for g in range(2, GROUPS, 2)]

        def load_x():
            first, count = x_loads.pop(0)
            xt = x_pool.tile([P, count, TILES, C], BF16, name="x_in%d" % count, align_bytes=64, bufs=PRELOAD + 1 if count == 2 else 2)
            nc.sync.dma_start(out=xt[:], in_=x_groups[first : first + count].rearrange("g p j c -> p g j c"))
            for k in range(count):
                x_in[first + k] = xt[:, k]

        def load_weight(h):
            nc.sync.dma_start(out=weight_in[h][:], in_=weight_rows[:, 2 * h : 2 * h + 2, :])

        nc.sync.dma_start(out=w_codes_in[:], in_=w_bytes)
        load_weight(0)
        for q in range(4):
            nc.sync.dma_start(
                out=sw_scales[32 * q : 32 * q + 4, :].bitcast(I32),
                in_=style_w_scales[0][4 * q : 4 * q + 4, :].bitcast(I32),
            )
        nc.sync.dma_start(out=sw_words[:], in_=style_w_words[0].rearrange("p n t -> p (n t)"))
        nc.sync.dma_start(out=w_scale_pt[:], in_=w_scale.rearrange("o (p t) -> p (o t)", t=PACK))
        load_x()
        load_weight(1)
        nc.sync.dma_start(out=style_b_pt[:], in_=style_b.rearrange("(p t) -> p t", t=PACK))
        load_x()
        with nc.allow_non_contiguous_dma(reason="one bias value a partition and block"):
            nc.sync.dma_start(out=bias_in[:, :, 0], in_=bias.rearrange("(b m) -> m b", b=BLOCKS))
        for k in range(PRELOAD):
            load_x()

        warm = const.tile([P, 1], F32, name="warm")
        nc.scalar.activation(warm[:], ones[:, :1], ACT.Abs_reciprocal_sqrt)
        ident = const.tile([P, P], F32, name="ident")
        make_identity(nc, ident[:])

        def turn_words(dst, rows):
            words = rows.bitcast(F32)
            for u in range(2):
                nc.tensor.transpose(dst[:, u], words[:, u : C // 2 : 2], ident[:])

        def mx_pass(dst, stationary, moving):
            nc.tensor.matmul_mx(
                out=dst,
                lhsT=stationary[0].bitcast(X4),
                lhsT_scale=stationary[1],
                rhs=moving[0].bitcast(X4),
                rhs_scale=moving[1],
                start=True,
                stop=True,
            )

        def block(pair, b):
            return [t[:, P * b : P * b + P] for t in pair]

        weight_k = const.tile([P, O, PACK], BF16, name="weight_k", align_bytes=64)
        weight_k_words = weight_k[:].rearrange("p o t -> p (o t)").bitcast(F32)
        weight_mx = (
            const.tile([P, O], U32, name="weight_codes", align_bytes=64),
            const.tile([P, O], U8, name="weight_scales", align_bytes=64),
        )
        weight2_k = const.tile([P, O, PACK], BF16, name="weight2_k", align_bytes=64)
        weight2_mx = (
            const.tile([P, O], U32, name="weight2_codes", align_bytes=64),
            const.tile([P, O], U8, name="weight2_scales", align_bytes=64),
        )
        style2_k = const.tile([P, N, PACK], BF16, name="style2_k", align_bytes=64)
        style2_mx = (
            const.tile([P, N], U32, name="style2_codes", align_bytes=64),
            const.tile([P, N], U8, name="style2_scales", align_bytes=64),
        )
        style_k = const.tile([P, N, PACK], F32, name="style_k", align_bytes=64)
        decoef = const.tile([P, BLOCKS, N], F32, name="decoef")
        bias_col = const.tile([P, BLOCKS], F32, name="bias_col")
        halves = [slice(0, O // 2), slice(O // 2, O)]

        weight_bank = {}

        def turn_weight(h):
            bank = weight_bank[h] = psum.tile([P, 2, 2, P], F32, name="weight_bank", tag="back0", bufs=2)
            for k in range(2):
                turn_words(bank[:, k], weight_in[h][:, k, :])

        def copy_weight(h):
            bank = weight_bank[h]
            nc.scalar.copy(
                out=weight_k_words[:, O * h : O * h + O].rearrange("p (b r u) -> p b r u", b=2, u=2),
                in_=bank[:].rearrange("p b u r -> p b r u"),
            )

        def square_weight(h, on_vector=False):
            src, dst = weight_k[:, halves[h], :], weight2_k[:, halves[h], :]
            if on_vector:
                nc.vector.tensor_tensor(out=dst, in0=src, in1=src, op=ALU.mult)
            else:
                nc.scalar.activation(dst, src, ACT.Square)

        def quantise(pair, src, cols=slice(None)):
            nc.vector.quantize_mx(
                out=pair[0][:, cols].bitcast(X4), scales=pair[1][:, cols], in_=src[:, cols, :].rearrange("p c t -> p (c t)")
            )

        d_bank = {}

        def demod_sums(h):
            d_bank[h] = psum.tile([P, 2, N], F32, name="d_bank", tag="back1", bufs=2)
            for k in range(2):
                mx_pass(d_bank[h][:, k, :], block(weight2_mx, 2 * h + k), [t[:] for t in style2_mx])

        def demod_coefficients(h):
            nc.scalar.activation(
                decoef[:, 2 * h : 2 * h + 2, :], d_bank[h][:], ACT.Abs_reciprocal_sqrt,
                scale=1.0 / gain**2, bias=EPS / gain**2,
            )

        x_bank, x_words, x_mod, x_mx, y_bank, s_tile, copied, c_tile, relu4, back_bank, out_tile = ({} for k in range(11))

        def turn_x(g, tag="turn"):
            x_bank[g] = psum.tile([P, 2, TILES, P], F32, name="x_bank", tag=tag, bufs=2)
            for j in range(TILES):
                turn_words(x_bank[g][:, :, j, :], x_in[g][:, j, :])

        x_tile, stage = {}, {}
        ahead = O - O * ON_GPSIMD // SAMPLES

        def new_stage():
            return s_pool.tile([P, ahead + O], F32, name="stage", align_bytes=64, bufs=9)

        def modulated(g):
            if g not in x_mod:
                tile = stage.get(g - SHARED_FROM) or (x_tile[1] if g == 3 else None) or new_stage()
                x_tile[g] = tile
                x_mod[g] = tile[:, :O].bitcast(BF16)
            return x_mod[g].rearrange("p (n l t) -> p n l t", l=L, t=PACK)

        def modulate(g, count=SAMPLES - ON_GPSIMD):
            nc.vector.tensor_tensor(
                out=modulated(g)[:, :count].rearrange("p n l (u e) -> p n l u e", u=2),
                in0=x_bank[g][:].rearrange("p u j q -> p u (j q)")[:, :, : L * count].bitcast(BF16)
                .rearrange("p u (n l e) -> p n l u e", l=L, e=2),
                in1=style_k[:, SAMPLES * g : SAMPLES * g + count, :]
                .rearrange("p n (u e) -> p n u e", u=2).unsqueeze(2).to_broadcast([P, count, L, 2, 2]),
                op=ALU.mult,
            )

        def copy_words(g):
            x_words[g] = x_pool.tile([P, L * ON_GPSIMD, 2], F32, name="x_words", align_bytes=64)
            words = x_bank[g][:].rearrange("p u j q -> p (j q) u")
            nc.scalar.copy(out=x_words[g][:], in_=words[:, TOKENS - L * ON_GPSIMD :, :])

        def modulate_words(g):
            first = SAMPLES - ON_GPSIMD
            nc.gpsimd.tensor_tensor(
                out=modulated(g)[:, first:],
                in0=x_words[g][:].rearrange("p q u -> p (q u)").bitcast(BF16).rearrange("p (n l t) -> p n l t", l=L, t=PACK),
                in1=style_k[:, SAMPLES * g + first : SAMPLES * g + SAMPLES, :]
                .unsqueeze(2).to_broadcast([P, ON_GPSIMD, L, PACK]),
                op=ALU.mult,
            )

        def quantise_x(g):
            codes = x_pool.tile([P, TOKENS], U32, name="x_codes", align_bytes=64)
            scales = x_pool.tile([P, TOKENS], U8, name="x_scales", align_bytes=64)
            nc.vector.quantize_mx(
                out=codes[:].bitcast(X4), scales=scales[:], in_=x_mod[g]
            )
            x_mx[g] = (codes[:], scales[:])

        def multiply(g, banks=(0, 1), tag=None):
            for h in banks:
                y_bank[g, h] = psum.tile([P, 2, TOKENS], F32, name="y_bank", tag=tag or "y%d" % h, bufs=2 if tag else 1)
                for k in range(2):
                    mx_pass(y_bank[g, h][:, k, :], block(weight_mx, 2 * h + k), x_mx[g])

        def scale_and_bias(g, h, on_vector=False):
            if g not in s_tile:
                s_tile[g] = s_pool.tile([P, TILES, BLOCKS, P], F32, name="s_tile", bufs=5)
            for k in range(2):
                b = 2 * h + k
                for n in range(SAMPLES):
                    j, place = divmod(n, SAMPLES // TILES)
                    src = y_bank[g, h][:, k, L * n : L * n + L]
                    dst = s_tile[g][:, j, b, L * place : L * place + L]
                    coefficient = decoef[:, b, SAMPLES * g + n : SAMPLES * g + n + 1]
                    if on_vector:
                        nc.vector.tensor_scalar(
                            out=dst, in0=src, scalar1=coefficient, scalar2=bias_col[:, b : b + 1],
                            op0=ALU.mult, op1=ALU.add,
                        )
                    else:
                        nc.scalar.activation(dst, src, ACT.Identity, scale=coefficient, bias=bias_col[:, b : b + 1])

        def s_of(g, j):
            return s_tile[g][:, j].rearrange("p b m -> p (b m)")

        def clip(g, first=0, last=None):
            last = last or O + P * math.ceil(scalar_columns(g) / P)
            part = s_tile[g][:].rearrange("p j b m -> p (j b m)")[:, first:last]
            c_tile[g] = x_mod[g + LEAD].bitcast(F32) if g < RAMP else part
            nc.gpsimd.tensor_scalar(
                out=c_tile[g], in0=part, scalar1=CLAMP / 5.0, scalar2=-CLAMP, op0=ALU.min, op1=ALU.max
            )

        def positive_part(g, j=1):
            relu4[g, j] = s_pool.tile([P, O], F32, name="relu4", bufs=3)
            nc.vector.tensor_scalar(out=relu4[g, j][:], in0=s_of(g, j), scalar1=0.0, scalar2=4.0, op0=ALU.max, op1=ALU.mult)

        def leaky_relu_in_place(g, j):
            nc.vector.scalar_tensor_tensor(
                out=s_of(g, j), in0=s_of(g, j), scalar=5.0, in1=s_of(g, j), op0=ALU.mult, op1=ALU.max
            )

        def turn_back(g, j, tag=None):
            back_bank[g, j] = psum.tile([P, O], F32, name="back_bank", tag=tag or "back%d" % j, bufs=1 if tag in ("y0", "y1") else 2)
            for b in range(BLOCKS):
                cols = slice(P * b, P * b + P)
                dst = back_bank[g, j][:, cols]
                if (g, j) in relu4:
                    nc.tensor.matmul(dst, lhsT=s_of(g, j)[:, cols], rhs=ident[:], start=True, stop=False, is_transpose=True)
                    nc.tensor.matmul(dst, lhsT=relu4[g, j][:, cols], rhs=ident[:], start=False, stop=True, is_transpose=True)
                else:
                    nc.tensor.transpose(dst, (c_tile[g] if g < RAMP else s_of(g, j))[:, cols], ident[:])

        def out_of(g, j):
            if g not in out_tile:
                out_tile[g] = out_pool.tile([P, TILES, O], F32, name="out_tile")
            return out_tile[g][:, j, :]

        def copy_back(g, j=0):
            stage[g] = new_stage()
            copied[g, j] = stage[g][:, ahead:]
            nc.scalar.copy(out=copied[g, j], in_=back_bank[g, j][:])

        def copy_out(g, j=1):
            split = scalar_columns(g)
            if split:
                nc.scalar.copy(out=out_of(g, j)[:, :split], in_=back_bank[g, j][:, :split])

        def clip_out(g, j=1):
            split = scalar_columns(g)
            nc.vector.tensor_scalar(
                out=out_of(g, j)[:, split:], in0=back_bank[g, j][:, split:], scalar1=CLAMP, scalar2=-CLAMP, op0=ALU.min, op1=ALU.max
            )

        def leaky_relu(g, j=0):
            nc.vector.scalar_tensor_tensor(
                out=out_of(g, j), in0=back_bank[g, j][:], scalar=5.0, in1=copied[g, j], op0=ALU.mult, op1=ALU.max
            )

        def store_group(g):
            nc.sync.dma_start(out=out_groups[g], in_=out_tile[g][:])
            if g % 2 == 1 and x_loads:
                load_x()

        def store_tile(g, j):
            nc.sync.dma_start(out=out_groups[g][:, j, :], in_=out_tile[g][:, j, :])

        w_wide = const.tile([P, WD], BF16, name="w_wide", align_bytes=64)
        sw_words_tm = const.tile([P, C], I32, name="sw_words_tm", align_bytes=64)
        sw_scales_tm = const.tile([P, C], U8, name="sw_scales_tm", align_bytes=64)
        w_k = const.tile([P, N, PACK], BF16, name="w_k", align_bytes=64)
        w_mx = (
            const.tile([P, N], U32, name="w_codes", align_bytes=64),
            const.tile([P, N], U8, name="w_scales", align_bytes=64),
        )
        w_bank = psum.tile([P, 2, P], F32, name="w_bank", tag="y1", bufs=1)
        style_bank = psum.tile([P, PACK, N], F32, name="style_bank", tag="y0", bufs=1)

        def warm_up(width):
            bank = psum.tile([P, O], F32, name="warm_bank", tag="back1", bufs=2)
            nc.tensor.matmul(bank[:, :width], lhsT=ones[:, :P], rhs=ones[:, :width], start=True, stop=True)

        def reorder(dst, src):
            nc.vector.tensor_copy(
                out=dst.rearrange("p (t m) -> p t m", t=PACK), in_=src.rearrange("p (m t) -> p t m", t=PACK)
            )

        def scale_w():
            nc.vector.tensor_tensor(
                out=w_k[:].rearrange("p n (u e) -> p n u e", u=2),
                in0=w_bank[:].bitcast(BF16).rearrange("p u (n e) -> p n u e", e=2),
                in1=w_scale_pt[:].rearrange("p (u e) -> p u e", u=2).unsqueeze(1).to_broadcast([P, N, 2, 2]),
                op=ALU.mult,
            )

        def style_sums():
            for t in range(PACK):
                mx_pass(style_bank[:, t, :], block((sw_words_tm, sw_scales_tm), t), [tile[:] for tile in w_mx])

        def finish_style(first, last):
            nc.vector.scalar_tensor_tensor(
                out=style_k[:, first:last], in0=style_bank[:, :, first:last].rearrange("p t n -> p n t"), scalar=1.0 / math.sqrt(WD),
                in1=style_b_pt[:].unsqueeze(1).to_broadcast([P, last - first, PACK]), op0=ALU.mult, op1=ALU.add,
            )

        warm_up(384)
        nc.vector.tensor_copy(out=w_wide[:], in_=w_codes_in[:].bitcast(F8))
        turn_words(w_bank, w_wide[:])
        turn_weight(0)
        warm_up(384)
        copy_weight(0)
        reorder(sw_scales_tm[:], sw_scales[:])
        scale_w()
        reorder(sw_words_tm[:], sw_words[:].bitcast(I32))
        quantise(w_mx, w_k)
        style_sums()
        turn_x(0)
        turn_weight(1)
        square_weight(0)
        quantise(weight_mx, weight_k, halves[0])
        finish_style(0, 2 * SAMPLES)
        finish_style(2 * SAMPLES, N)
        warm_up(256)
        turn_x(1)
        turn_x(2, "back0")
        nc.scalar.activation(style2_k[:], style_k[:], ACT.Square)
        copy_weight(1)
        square_weight(1)
        nc.scalar.activation(bias_col[:], bias_in[:, :, 0], ACT.Copy, scale=gain)
        modulate(0, SAMPLES)
        quantise(weight2_mx, weight2_k, halves[0])
        quantise(style2_mx, style2_k)
        quantise_x(0)
        quantise(weight_mx, weight_k, halves[1])
        demod_sums(0)
        demod_coefficients(0)
        multiply(0, (0,))
        modulate(1, SAMPLES)
        quantise(weight2_mx, weight2_k, halves[1])
        multiply(0, (1,))
        turn_x(3, "back0")
        demod_sums(1)
        scale_and_bias(0, 0)
        copy_words(3)
        demod_coefficients(1)
        scale_and_bias(0, 1)
        quantise_x(1)
        modulate_words(3)
        modulate(2, SAMPLES)
        turn_x(4)
        modulate(3)
        quantise_x(2)

        steps = GROUPS - LEAD
        for i in range(1, steps):
            x = i + LEAD
            multiply(i, tag="back1" if i == 1 else None)
            if 2 <= i <= RAMP:
                positive_part(i - 2)
            if i != RAMP + 1:
                quantise_x(x - 1 if i <= RAMP else x - 2)
            if i > RAMP:
                positive_part(i - 2)
            if SHARED_FROM <= x < GROUPS:
                modulate_words(x)
            clip(i - 1)
            if x == SHARED_FROM - 1:
                modulate_words(x)
            if i == 2:
                turn_x(6, "back1")
            if i >= 2:
                turn_back(i - 2, 0)
            if x < GROUPS:
                modulate(x, SAMPLES - ON_GPSIMD if x >= SHARED_FROM - 1 else SAMPLES)
            if i >= 3:
                clip_out(i - 3)
            if i in (2, 3):
                turn_x(x + 2)
            elif x + 1 < GROUPS and x + 1 not in x_bank:
                turn_x(x + 1)
            if i >= 2:
                turn_back(i - 2, 1)
            scale_and_bias(i, 0)
            scale_and_bias(i, 1)
            if SHARED_FROM - 1 <= x + 1 < GROUPS:
                copy_words(x + 1)
            if i >= 2:
                copy_back(i - 2)
            if i >= 2:
                copy_out(i - 2)
            if i >= 3:
                leaky_relu(i - 3)
                store_group(i - 3)

        g0, g1, g2, g3, g4, g5 = range(GROUPS - 6, GROUPS)
        multiply(g3)
        quantise_x(g4)
        quantise_x(g5)
        positive_part(g1)
        multiply(g4, tag="turn")
        turn_back(g1, 1)
        scale_and_bias(g3, 0)
        scale_and_bias(g3, 1)
        positive_part(g2)
        leaky_relu_in_place(g2, 0)
        clip(g3, 0, 2 * O)
        leaky_relu(g0)
        store_tile(g0, 0)
        clip_out(g0)
        store_tile(g0, 1)
        multiply(g5)
        turn_back(g1, 0)
        scale_and_bias(g4, 0)
        scale_and_bias(g4, 1)
        copy_back(g1)
        clip(g4, 0, 2 * O)
        turn_back(g2, 0)
        turn_back(g2, 1)
        clip_out(g1, 1)
        store_tile(g1, 1)
        scale_and_bias(g5, 0)
        turn_back(g3, 0, "turn")
        turn_back(g3, 1, "turn")
        scale_and_bias(g5, 1, on_vector=True)
        clip(g5, 0, O)
        clip(g5, O, 2 * O)
        clip_out(g2, 0)
        store_tile(g2, 0)
        leaky_relu(g1)
        store_tile(g1, 0)
        clip_out(g2, 1)
        store_tile(g2, 1)
        turn_back(g4, 0)
        turn_back(g4, 1)
        turn_back(g5, 0, "y0")
        turn_back(g5, 1, "y1")
        for g in (g3, g4, g5):
            for j in range(TILES):
                copy_back(g, j)
                leaky_relu(g, j)
                store_tile(g, j)
